import numpy as np
import ml_dtypes


def mxq(x, axis, fmt="e4m3"):
    dtype, down = {"e4m3": (ml_dtypes.float8_e4m3fn, 7), "e5m2": (ml_dtypes.float8_e5m2, 14)}[fmt]
    v = np.moveaxis(np.asarray(x, np.float32).astype(ml_dtypes.bfloat16).astype(np.float64), axis, -1)
    blocks = v.reshape(v.shape[:-1] + (-1, 32))
    amax = np.abs(blocks).max(-1, keepdims=True)
    byte = np.maximum(np.where(amax > 0, np.frexp(amax)[1] - 1 + 127, 0) - down, 1)
    scale = np.exp2(byte - 127.0)
    codes = (blocks / scale).astype(np.float32).astype(dtype).astype(np.float64)
    return np.moveaxis((codes * scale).reshape(v.shape), -1, axis)


WIDE = False


def mx_kscale(k):
    if not WIDE:
        return np.ones(k)
    levels = np.array([10, -10, 5, -5, 0])
    a = np.random.permutation(np.resize(levels, k // 512 * 4)).reshape(k // 512, 4)
    idx = np.arange(k)
    return np.exp2(a[idx // 512, idx % 128 // 32])


BF16 = ml_dtypes.bfloat16


def bf(x):
    return np.asarray(x, np.float32).astype(BF16)


def f64(x):
    return np.asarray(x).astype(np.float64)


B, SQ, SV, DV, DQ, DK, DO, H = 2, 512, 512, 1024, 1280, 1024, 1024, 8
DHK = DK // H


def heads(x):
    b, s, d = x.shape
    return x.reshape(b, s, H, d // H).transpose(0, 2, 1, 3)


def sigmoid(a):
    return 1.0 / (1.0 + np.exp(-a))


def setup_inputs():
    s = mx_kscale(DV)
    kept = (np.random.uniform(size=(B, SV)) < 0.9).astype(np.float64)
    k_offset = np.random.standard_normal(DK) * 0.6
    return {"q": bf(np.random.standard_normal((B, SQ, DK)) * 1.5),
            "k": bf(np.random.standard_normal((B, SV, DK)) * 1.5 + k_offset),
            "pre_value_key": bf(np.random.standard_normal((B, SV, DV)) * s),
            "Wv": bf(np.random.standard_normal((DV, DO)) * 1.5 / np.sqrt(DV) / s[:, None]),
            "bv": bf(np.random.standard_normal(DO) * 0.3),
            "value_key_masks": bf(kept),
            "value_key_counts": bf(np.maximum(kept.sum(-1), 1.0)),
            "overall_gain": bf(1.0 + 0.2 * np.random.standard_normal((1, H, 1, 1))),
            "overall_bias": bf(-0.5 + 0.5 * np.random.standard_normal((1, H, 1, 1))),
            "pre_query": bf(np.random.standard_normal((B, SQ, DQ)))}


def reference(q, k, pre_value_key, Wv, bv, value_key_masks, value_key_counts, overall_gain, overall_bias, pre_query):
    qh, kh = heads(f64(q)), heads(f64(k))
    v = heads((mxq(f64(pre_value_key), 2, "e4m3") @ mxq(f64(Wv), 0, "e4m3")) + f64(bv))
    scores = qh @ kh.transpose(0, 1, 3, 2) / np.sqrt(DHK)
    mask = f64(value_key_masks)
    pooled = (scores * mask[:, None, None, :]).sum(-1, keepdims=True)
    pooled = pooled / f64(value_key_counts)[:, None, None, None]
    w = sigmoid(pooled * f64(overall_gain) + f64(overall_bias))
    sm = scores + np.where(mask == 0, -np.inf, 0.0)[:, None, None, :]
    e = np.exp(sm - sm.max(-1, keepdims=True))
    h = (mxq(e, 3, "e4m3") @ mxq(v, 2, "e4m3")) / e.sum(-1, keepdims=True)
    pq = f64(pre_query)
    mix = heads(pq[:, :, :DO]) * (1.0 - w) + h * w
    mix = mix.transpose(0, 2, 1, 3).reshape(B, SQ, DO)
    return np.concatenate([mix, pq[:, :, DO:]], axis=-1)

@@ -1,0 +1,382 @@
+from contextlib import ExitStack
+import math
+
+import concourse.mybir as mybir
+from concourse.masks import make_identity
+
+F32 = mybir.dt.float32
+BF16 = mybir.dt.bfloat16
+U32 = mybir.dt.uint32
+U8 = mybir.dt.uint8
+FP8X4 = mybir.dt.float8_e4m3fn_x4
+ALU = mybir.AluOpType
+ACT = mybir.ActivationFunctionType
+AX = mybir.AxisListType
+
+P = 128
+B = 2
+S = 512
+H = 8
+D = 1024
+DQ = 1280
+NT = S // P
+PASSES = D // (4 * P)
+HG = 4
+W = HG * P
+SCALE = 1.0 / math.sqrt(P)
+MASKED = 1.0e30
+
+GAIN0 = D
+GATE_BIAS0 = D + 16
+COUNT0 = D + 32
+ROW_W = D + 48
+
+FLOPS = 2 * B * S * D * D + 2 * 2 * B * H * S * S * P
+
+
+def tile_multiheadedselfattention_pa_kernel(
+    tc, q, k, pre_value_key, Wv, bv, value_key_masks, value_key_counts,
+    overall_gain, overall_bias, pre_query, out,
+):
+    nc = tc.nc
+    with ExitStack() as ctx:
+        const = ctx.enter_context(tc.tile_pool(name="const", bufs=1))
+        raw = ctx.enter_context(tc.tile_pool(name="raw", bufs=1))
+        keep = ctx.enter_context(tc.tile_pool(name="keep", bufs=1))
+        stage = ctx.enter_context(tc.tile_pool(name="stage", bufs=2))
+        small = ctx.enter_context(tc.tile_pool(name="small", bufs=3))
+        psum_s = ctx.enter_context(tc.psum_pool(name="psum_s", bufs=4))
+        psum_b = ctx.enter_context(tc.psum_pool(name="psum_b", bufs=2))
+        psum_h = ctx.enter_context(tc.psum_pool(name="psum_h", bufs=1))
+        psum_c = ctx.enter_context(tc.psum_pool(name="psum_c", bufs=1))
+
+        mask_rows = const.tile([P, P], BF16)
+        nc.vector.memset(mask_rows[:], 0.0)
+        nc.scalar.dma_start(
+            out=mask_rows[0 : B * NT, :], in_=value_key_masks.rearrange("b (t p) -> (b t) p", p=P)
+        )
+        small_row = const.tile([P, ROW_W], BF16)
+        nc.vector.memset(small_row[:], 0.0)
+        nc.scalar.dma_start(out=small_row[0:1, 0:D], in_=bv.rearrange("(o n) -> o n", o=1))
+        nc.scalar.dma_start(
+            out=small_row[0:1, GAIN0 : GAIN0 + H], in_=overall_gain.rearrange("a h b c -> a (h b c)")
+        )
+        nc.scalar.dma_start(
+            out=small_row[0:1, GATE_BIAS0 : GATE_BIAS0 + H], in_=overall_bias.rearrange("a h b c -> a (h b c)")
+        )
+        nc.scalar.dma_start(
+            out=small_row[0:1, COUNT0 : COUNT0 + B], in_=value_key_counts.rearrange("(o n) -> o n", o=1)
+        )
+
+        wv_raw = raw.tile([P, PASSES, 4, D], BF16)
+        k_sb = {}
+        q_sb = {}
+        pvk_sb = {}
+        pq_sb = {}
+
+        def load_wv(g):
+            nc.sync.dma_start(
+                out=wv_raw[:, g].rearrange("p (u e) n -> p u (e n)", e=2),
+                in_=Wv[g * 4 * P : (g + 1) * 4 * P, :].rearrange("(u p e) n -> p u (e n)", u=2, e=2),
+            )
+
+        def load_k_q(b, hg):
+            cols = slice(hg * W, (hg + 1) * W)
+            k_sb[b, hg] = raw.tile([P, NT, W], BF16, name="k_sb%d%d" % (b, hg))
+            nc.sync.dma_start(out=k_sb[b, hg][:], in_=k[b][:, cols].rearrange("(t p) d -> p t d", p=P))
+            q_sb[b, hg] = raw.tile([P, NT, W], BF16, name="q_sb%d%d" % (b, hg))
+            nc.sync.dma_start(out=q_sb[b, hg][:], in_=q[b][:, cols].rearrange("(p t) d -> p t d", t=NT))
+
+        def load_pvk(b):
+            pvk_sb[b] = raw.tile([P, NT, D], BF16, name="pvk_sb%d" % b)
+            nc.sync.dma_start(
+                out=pvk_sb[b][:].rearrange("p (u e) d -> p u (e d)", e=2),
+                in_=pre_value_key[b].rearrange("(u p e) d -> p u (e d)", u=2, e=2),
+            )
+
+        def load_pq(b):
+            pq_sb[b] = raw.tile([P, NT, DQ], BF16, name="pq_sb%d" % b)
+            nc.sync.dma_start(out=pq_sb[b][:], in_=pre_query[b].rearrange("(p t) c -> p t c", t=NT))
+
+        load_wv(0)
+        load_k_q(0, 0)
+        load_wv(1)
+        load_pvk(0)
+        load_k_q(0, 1)
+        load_pq(0)
+        load_k_q(1, 0)
+        load_pvk(1)
+        load_k_q(1, 1)
+        load_pq(1)
+
+        ident_bf = const.tile([P, P], BF16)
+        make_identity(nc, ident_bf[:])
+        ident_f32 = const.tile([P, P], F32)
+        make_identity(nc, ident_f32[:])
+        ones_bf = const.tile([P, P], BF16)
+        nc.vector.memset(ones_bf[:], 1.0)
+
+        mask_t_ps = psum_c.tile([P, P], BF16, tag="c")
+        nc.tensor.transpose(mask_t_ps[:], mask_rows[:], ident_bf[:])
+        mask_t = const.tile([P, B * NT], BF16)
+        nc.vector.tensor_copy(out=mask_t[:], in_=mask_t_ps[:, 0 : B * NT])
+        mask_bias_t = const.tile([P, B * NT, P], F32)
+        nc.vector.tensor_scalar(
+            out=mask_bias_t[:], in0=mask_t[:].unsqueeze(2).to_broadcast([P, B * NT, P]),
+            scalar1=1.0, scalar2=MASKED, op0=ALU.subtract, op1=ALU.mult,
+        )
+
+        small_bc = const.tile([P, ROW_W], F32)
+        for first in range(0, ROW_W, S):
+            width = min(S, ROW_W - first)
+            bc_ps = psum_s.tile([P, S], F32, tag="s")
+            nc.tensor.matmul(
+                out=bc_ps[:, 0:width], lhsT=ones_bf[:], rhs=small_row[:, first : first + width], start=True, stop=True
+            )
+            nc.scalar.copy(out=small_bc[:, first : first + width], in_=bc_ps[:, 0:width])
+        inv_count = const.tile([P, B], F32)
+        nc.vector.reciprocal(out=inv_count[:], in_=small_bc[:, COUNT0 : COUNT0 + B])
+
+        wv_codes = keep.tile([P, PASSES, D], U32, align_bytes=64)
+        wv_scales = keep.tile([P, PASSES, D], U8, align_bytes=64)
+        for g in range(PASSES):
+            grouped_v = stage.tile([P, S, 4], BF16, align_bytes=64)
+            nc.vector.tensor_copy(
+                out=grouped_v[:].rearrange("p (c i) t -> p c t i", i=4),
+                in_=wv_raw[:, g, :, 0:S].rearrange("p t (c i) -> p c t i", i=4),
+            )
+            grouped_s = stage.tile([P, S, 4], BF16, align_bytes=64)
+            nc.scalar.copy(
+                out=grouped_s[:].rearrange("p (c i) t -> p c t i", i=4),
+                in_=wv_raw[:, g, :, S:D].rearrange("p t (c i) -> p c t i", i=4),
+            )
+            for half, grouped in enumerate((grouped_v, grouped_s)):
+                cols = slice(half * S, (half + 1) * S)
+                nc.vector.quantize_mx(
+                    out=wv_codes[:, g, cols].bitcast(FP8X4),
+                    scales=wv_scales[:, g, cols],
+                    in_=grouped[:].rearrange("p c t -> p (c t)"),
+                )
+
+        pvk_codes = keep.tile([P, PASSES, B * S], U32, align_bytes=64)
+        pvk_scales = keep.tile([P, PASSES, B * S], U8, align_bytes=64)
+        v_codes = keep.tile([P, B, D], U32, align_bytes=64)
+        v_scales = keep.tile([P, B, D], U8, align_bytes=64)
+        kqT = [keep.tile([P, H, 2, S], BF16, name="kqT%d" % b) for b in range(B)]
+        gate = {}
+        one_minus_gate = {}
+
+        def prepare_tokens(b):
+            pvk_words = pvk_sb[b][:].bitcast(F32)
+            pvk_grouped = stage.tile([P, PASSES, S, 4], BF16, align_bytes=64, bufs=1)
+            pvk_grouped_words = pvk_grouped[:].bitcast(F32)
+            for t in range(NT):
+                w_bank = psum_b.tile([P, PASSES, 2, P], F32, tag="b")
+                for g in range(PASSES):
+                    for u in range(2):
+                        first = (2 * g + u) * P
+                        nc.tensor.transpose(w_bank[:, g, u, :], pvk_words[:, t, first : first + P], ident_f32[:])
+                nc.scalar.copy(
+                    out=pvk_grouped_words[:, :, t * P : (t + 1) * P, :],
+                    in_=w_bank[:].rearrange("p g u r -> p g r u"),
+                )
+            for g in range(PASSES):
+                nc.vector.quantize_mx(
+                    out=pvk_codes[:, g, b * S : (b + 1) * S].bitcast(FP8X4),
+                    scales=pvk_scales[:, g, b * S : (b + 1) * S],
+                    in_=pvk_grouped[:, g].rearrange("p r t -> p (r t)"),
+                )
+            tail = stage.tile([P, NT, DQ - D], F32, bufs=1)
+            nc.gpsimd.tensor_scalar(
+                out=tail[:], in0=pq_sb[b][:, :, D:DQ], scalar1=1.0, scalar2=0.0, op0=ALU.mult, op1=ALU.add
+            )
+            nc.sync.dma_start(out=out[b].rearrange("(p t) c -> p t c", t=NT)[:, :, D:DQ], in_=tail[:])
+
+        def prepare_head(b, h, banks, tag):
+            hg, hh = divmod(h, HG)
+            t_bank = banks.tile([P, 2, NT, P], BF16, tag=tag)
+            for side, x_sb in enumerate((k_sb[b, hg], q_sb[b, hg])):
+                for t in range(NT):
+                    nc.tensor.transpose(t_bank[:, side, t, :], x_sb[:, t, hh * P : (hh + 1) * P], ident_bf[:])
+            nc.scalar.copy(out=kqT[b][:, h], in_=t_bank[:].rearrange("p a t r -> p a (t r)"))
+
+            cols = slice(h * P, (h + 1) * P)
+            v_bank = banks.tile([P, NT, P], F32, tag=tag)
+            for t in range(NT):
+                toks = slice(b * S + t * P, b * S + (t + 1) * P)
+                for g in range(PASSES):
+                    nc.tensor.matmul_mx(
+                        out=v_bank[:, t, :],
+                        lhsT=pvk_codes[:, g, toks].bitcast(FP8X4),
+                        lhsT_scale=pvk_scales[:, g, toks],
+                        rhs=wv_codes[:, g, cols].bitcast(FP8X4),
+                        rhs_scale=wv_scales[:, g, cols],
+                        start=(g == 0),
+                        stop=(g == PASSES - 1),
+                    )
+            v_grouped = stage.tile([P, P, NT], BF16, align_bytes=64)
+            nc.vector.tensor_tensor(
+                out=v_grouped[:],
+                in0=v_bank[:].rearrange("p t c -> p c t"),
+                in1=small_bc[:, cols].unsqueeze(2).to_broadcast([P, P, NT]),
+                op=ALU.add,
+            )
+            nc.vector.quantize_mx(
+                out=v_codes[:, b, cols].bitcast(FP8X4),
+                scales=v_scales[:, b, cols],
+                in_=v_grouped[:].rearrange("p c t -> p (c t)"),
+            )
+
+        def prepare_gate(b, hg):
+            ksum_ps = psum_c.tile([P, HG], F32, tag="c")
+            for hh in range(HG):
+                for t in range(NT):
+                    nc.tensor.matmul(
+                        out=ksum_ps[:, hh : hh + 1],
+                        lhsT=k_sb[b, hg][:, t, hh * P : (hh + 1) * P],
+                        rhs=mask_t[:, b * NT + t : b * NT + t + 1],
+                        start=(t == 0),
+                        stop=(t == NT - 1),
+                    )
+            ksum_terms = small.tile([P, HG, 2], BF16)
+            nc.vector.tensor_copy(out=ksum_terms[:, :, 0], in_=ksum_ps[:])
+            ksum_rest = small.tile([P, HG], F32)
+            nc.vector.tensor_tensor(out=ksum_rest[:], in0=ksum_ps[:], in1=ksum_terms[:, :, 0], op=ALU.subtract)
+            nc.vector.tensor_copy(out=ksum_terms[:, :, 1], in_=ksum_rest[:])
+            pooled_ps = psum_c.tile([P, NT, HG, 2], F32, tag="c")
+            for it in range(NT):
+                for hh in range(HG):
+                    nc.tensor.matmul(
+                        out=pooled_ps[:, it, hh, :],
+                        lhsT=kqT[b][:, hg * HG + hh, 1, it * P : (it + 1) * P],
+                        rhs=ksum_terms[:, hh, :],
+                        start=True,
+                        stop=True,
+                    )
+            heads = slice(hg * HG, (hg + 1) * HG)
+            pooled = small.tile([P, NT, HG], F32)
+            nc.vector.tensor_reduce(out=pooled[:], in_=pooled_ps[:], axis=AX.X, op=ALU.add)
+            nc.vector.tensor_scalar(
+                out=pooled[:], in0=pooled[:], scalar1=inv_count[:, b : b + 1], scalar2=SCALE,
+                op0=ALU.mult, op1=ALU.mult,
+            )
+            gain = small_bc[:, GAIN0:GATE_BIAS0][:, heads].unsqueeze(1).to_broadcast([P, NT, HG])
+            nc.vector.tensor_tensor(out=pooled[:], in0=pooled[:], in1=gain, op=ALU.mult)
+            gate_bias = small_bc[:, GATE_BIAS0:COUNT0][:, heads].unsqueeze(1).to_broadcast([P, NT, HG])
+            nc.vector.tensor_tensor(out=pooled[:], in0=pooled[:], in1=gate_bias, op=ALU.add)
+            exp_neg = small.tile([P, NT, HG], F32)
+            nc.scalar.activation(out=exp_neg[:], in_=pooled[:], func=ACT.Exp, scale=-1.0)
+            nc.vector.tensor_scalar_add(out=exp_neg[:], in0=exp_neg[:], scalar1=1.0)
+            gate[b, hg] = keep.tile([P, NT, HG], F32, name="gate%d%d" % (b, hg))
+            nc.vector.reciprocal(out=gate[b, hg][:], in_=exp_neg[:])
+            one_minus_gate[b, hg] = keep.tile([P, NT, HG], F32, name="one_minus_gate%d%d" % (b, hg))
+            nc.vector.tensor_scalar(
+                out=one_minus_gate[b, hg][:], in0=gate[b, hg][:], scalar1=-1.0, scalar2=1.0,
+                op0=ALU.mult, op1=ALU.add,
+            )
+
+        def attention(b, hg, it):
+            rows = slice(it * P, (it + 1) * P)
+            result = stage.tile([P, W], F32, bufs=3)
+            for hh in range(HG):
+                nc.gpsimd.tensor_scalar(
+                    out=result[:, hh * P : (hh + 1) * P],
+                    in0=pq_sb[b][:, it, (hg * HG + hh) * P : (hg * HG + hh + 1) * P],
+                    scalar1=one_minus_gate[b, hg][:, it, hh : hh + 1],
+                    scalar2=0.0,
+                    op0=ALU.mult,
+                    op1=ALU.add,
+                )
+            row_max = small.tile([P, HG], F32)
+            exp_bias = small.tile([P, HG], F32)
+            e_bf = stage.tile([P, HG, S], BF16, bufs=3)
+            row_sum = small.tile([P, HG], F32)
+            for hh in range(HG):
+                h = hg * HG + hh
+                s_bank = psum_s.tile([P, S], F32, tag="s", name="s_bank%d" % hh)
+                for t in range(NT):
+                    nc.tensor.matmul(
+                        out=s_bank[:, t * P : (t + 1) * P], lhsT=mask_bias_t[:, b * NT + t, :], rhs=ident_f32[:],
+                        is_transpose=True, start=(t == 0), stop=False,
+                    )
+                nc.tensor.matmul(
+                    out=s_bank[:], lhsT=kqT[b][:, h, 1, rows], rhs=kqT[b][:, h, 0, :], start=False, stop=True
+                )
+                nc.vector.tensor_reduce(out=row_max[:, hh : hh + 1], in_=s_bank[:], axis=AX.X, op=ALU.max)
+                nc.gpsimd.tensor_scalar(
+                    out=exp_bias[:, hh : hh + 1], in0=row_max[:, hh : hh + 1], scalar1=-SCALE, scalar2=0.0,
+                    op0=ALU.mult, op1=ALU.add,
+                )
+                nc.scalar.activation(
+                    out=e_bf[:, hh, :],
+                    in_=s_bank[:],
+                    func=ACT.Exp,
+                    bias=exp_bias[:, hh : hh + 1],
+                    scale=SCALE,
+                    accum_out=row_sum[:, hh : hh + 1],
+                )
+            e_words = e_bf[:].bitcast(F32)
+            e_grouped = stage.tile([P, HG, P, 4], BF16, align_bytes=64)
+            e_grouped_words = e_grouped[:].bitcast(F32)
+            for pair in range(HG // 2):
+                e_bank = psum_b.tile([P, 2, 2, P], F32, tag="b")
+                for h2 in range(2):
+                    for u in range(2):
+                        nc.tensor.transpose(
+                            e_bank[:, h2, u, :], e_words[:, 2 * pair + h2, u * P : (u + 1) * P], ident_f32[:]
+                        )
+                nc.scalar.copy(
+                    out=e_grouped_words[:, 2 * pair : 2 * pair + 2, :, :],
+                    in_=e_bank[:].rearrange("p h u i -> p h i u"),
+                )
+            e_codes = stage.tile([P, W], U32, align_bytes=64, bufs=3)
+            e_scales = stage.tile([P, W], U8, align_bytes=64, bufs=3)
+            nc.vector.quantize_mx(
+                out=e_codes[:].bitcast(FP8X4),
+                scales=e_scales[:],
+                in_=e_grouped[:].rearrange("p h i t -> p (h i t)"),
+            )
+            h_bank = psum_h.tile([P, HG, P], F32, tag="h")
+            for hh in range(HG):
+                h = hg * HG + hh
+                nc.tensor.matmul_mx(
+                    out=h_bank[:, hh, :],
+                    lhsT=e_codes[:, hh * P : (hh + 1) * P].bitcast(FP8X4),
+                    lhsT_scale=e_scales[:, hh * P : (hh + 1) * P],
+                    rhs=v_codes[:, b, h * P : (h + 1) * P].bitcast(FP8X4),
+                    rhs_scale=v_scales[:, b, h * P : (h + 1) * P],
+                    start=True,
+                    stop=True,
+                )
+            weight = small.tile([P, HG], F32)
+            nc.vector.reciprocal(out=weight[:], in_=row_sum[:])
+            nc.vector.tensor_tensor(out=weight[:], in0=weight[:], in1=gate[b, hg][:, it, :], op=ALU.mult)
+            for hh in range(HG):
+                cols = slice(hh * P, (hh + 1) * P)
+                nc.vector.scalar_tensor_tensor(
+                    out=result[:, cols],
+                    in0=h_bank[:, hh, :],
+                    scalar=weight[:, hh : hh + 1],
+                    in1=result[:, cols],
+                    op0=ALU.mult,
+                    op1=ALU.add,
+                )
+            nc.sync.dma_start(
+                out=out[b].rearrange("(p t) c -> p t c", t=NT)[:, it, hg * W : (hg + 1) * W], in_=result[:]
+            )
+
+        groups = [(b, hg) for b in range(B) for hg in range(H // HG)]
+        prepare_tokens(0)
+        for hh in range(HG):
+            prepare_head(0, hh, psum_s, "s")
+        prepare_gate(0, 0)
+        for n, (b, hg) in enumerate(groups):
+            following = groups[n + 1] if n + 1 < len(groups) else None
+            if following is not None and following[0] != b:
+                prepare_tokens(following[0])
+            for it in range(NT):
+                attention(b, hg, it)
+                if following is not None:
+                    prepare_head(following[0], following[1] * HG + it, psum_c, "c")
+            if following is not None:
+                prepare_gate(following[0], following[1])

@@ -40,11 +40,12 @@ def tile_multiheadedselfattention_pa_kernel(
 ):
     nc = tc.nc
     with ExitStack() as ctx:
+        ctx.enter_context(tc.manual_schedule())
         const = ctx.enter_context(tc.tile_pool(name="const", bufs=1))
         raw = ctx.enter_context(tc.tile_pool(name="raw", bufs=1))
         keep = ctx.enter_context(tc.tile_pool(name="keep", bufs=1))
         stage = ctx.enter_context(tc.tile_pool(name="stage", bufs=2))
-        small = ctx.enter_context(tc.tile_pool(name="small", bufs=3))
+        small = ctx.enter_context(tc.tile_pool(name="small", bufs=2))
         psum_s = ctx.enter_context(tc.psum_pool(name="psum_s", bufs=4))
         psum_b = ctx.enter_context(tc.psum_pool(name="psum_b", bufs=2))
         psum_h = ctx.enter_context(tc.psum_pool(name="psum_h", bufs=1))
@@ -69,45 +70,26 @@ def tile_multiheadedselfattention_pa_kernel(
         )
 
         wv_raw = raw.tile([P, PASSES, 4, D], BF16)
-        k_sb = {}
-        q_sb = {}
-        pvk_sb = {}
-        pq_sb = {}
-
-        def load_wv(g):
+        for g in range(PASSES):
             nc.sync.dma_start(
                 out=wv_raw[:, g].rearrange("p (u e) n -> p u (e n)", e=2),
                 in_=Wv[g * 4 * P : (g + 1) * 4 * P, :].rearrange("(u p e) n -> p u (e n)", u=2, e=2),
             )
-
-        def load_k_q(b, hg):
-            cols = slice(hg * W, (hg + 1) * W)
-            k_sb[b, hg] = raw.tile([P, NT, W], BF16, name="k_sb%d%d" % (b, hg))
-            nc.sync.dma_start(out=k_sb[b, hg][:], in_=k[b][:, cols].rearrange("(t p) d -> p t d", p=P))
-            q_sb[b, hg] = raw.tile([P, NT, W], BF16, name="q_sb%d%d" % (b, hg))
-            nc.sync.dma_start(out=q_sb[b, hg][:], in_=q[b][:, cols].rearrange("(p t) d -> p t d", t=NT))
-
-        def load_pvk(b):
-            pvk_sb[b] = raw.tile([P, NT, D], BF16, name="pvk_sb%d" % b)
+        pvk_sb = [raw.tile([P, NT, D], BF16, name="pvk_sb%d" % b) for b in range(B)]
+        k_sb = [raw.tile([P, NT, D], BF16, name="k_sb%d" % b) for b in range(B)]
+        q_sb = [raw.tile([P, NT, D], BF16, name="q_sb%d" % b) for b in range(B)]
+        pq_sb = [raw.tile([P, NT, DQ], BF16, name="pq_sb%d" % b) for b in range(B)]
+        out_view = [out[b].rearrange("(p t) c -> p t c", t=NT) for b in range(B)]
+        for b in range(B):
             nc.sync.dma_start(
                 out=pvk_sb[b][:].rearrange("p (u e) d -> p u (e d)", e=2),
                 in_=pre_value_key[b].rearrange("(u p e) d -> p u (e d)", u=2, e=2),
             )
-
-        def load_pq(b):
-            pq_sb[b] = raw.tile([P, NT, DQ], BF16, name="pq_sb%d" % b)
+        for b in range(B):
+            nc.sync.dma_start(out=k_sb[b][:], in_=k[b].rearrange("(t p) d -> p t d", p=P))
+            nc.sync.dma_start(out=q_sb[b][:], in_=q[b].rearrange("(p t) d -> p t d", t=NT))
+        for b in range(B):
             nc.sync.dma_start(out=pq_sb[b][:], in_=pre_query[b].rearrange("(p t) c -> p t c", t=NT))
-
-        load_wv(0)
-        load_k_q(0, 0)
-        load_wv(1)
-        load_pvk(0)
-        load_k_q(0, 1)
-        load_pq(0)
-        load_k_q(1, 0)
-        load_pvk(1)
-        load_k_q(1, 1)
-        load_pq(1)
 
         ident_bf = const.tile([P, P], BF16)
         make_identity(nc, ident_bf[:])
@@ -134,8 +116,6 @@ def tile_multiheadedselfattention_pa_kernel(
                 out=bc_ps[:, 0:width], lhsT=ones_bf[:], rhs=small_row[:, first : first + width], start=True, stop=True
             )
             nc.scalar.copy(out=small_bc[:, first : first + width], in_=bc_ps[:, 0:width])
-        inv_count = const.tile([P, B], F32)
-        nc.vector.reciprocal(out=inv_count[:], in_=small_bc[:, COUNT0 : COUNT0 + B])
 
         wv_codes = keep.tile([P, PASSES, D], U32, align_bytes=64)
         wv_scales = keep.tile([P, PASSES, D], U8, align_bytes=64)
@@ -158,17 +138,26 @@ def tile_multiheadedselfattention_pa_kernel(
                     in_=grouped[:].rearrange("p c t -> p (c t)"),
                 )
 
+        inv_count = const.tile([P, B], F32)
+        nc.vector.reciprocal(out=inv_count[:], in_=small_bc[:, COUNT0 : COUNT0 + B])
+        gate_scale = const.tile([P, B, H], F32)
+        for b in range(B):
+            nc.vector.tensor_scalar(
+                out=gate_scale[:, b, :], in0=small_bc[:, GAIN0 : GAIN0 + H], scalar1=inv_count[:, b : b + 1],
+                scalar2=SCALE, op0=ALU.mult, op1=ALU.mult,
+            )
+
         pvk_codes = keep.tile([P, PASSES, B * S], U32, align_bytes=64)
         pvk_scales = keep.tile([P, PASSES, B * S], U8, align_bytes=64)
         v_codes = keep.tile([P, B, D], U32, align_bytes=64)
         v_scales = keep.tile([P, B, D], U8, align_bytes=64)
         kqT = [keep.tile([P, H, 2, S], BF16, name="kqT%d" % b) for b in range(B)]
-        gate = {}
-        one_minus_gate = {}
+        gate = [keep.tile([P, NT, H], F32, name="gate%d" % b) for b in range(B)]
+        one_minus_gate = [keep.tile([P, NT, H], F32, name="one_minus_gate%d" % b) for b in range(B)]
 
         def prepare_tokens(b):
             pvk_words = pvk_sb[b][:].bitcast(F32)
-            pvk_grouped = stage.tile([P, PASSES, S, 4], BF16, align_bytes=64, bufs=1)
+            pvk_grouped = stage.tile([P, PASSES, S, 4], BF16, align_bytes=64)
             pvk_grouped_words = pvk_grouped[:].bitcast(F32)
             for t in range(NT):
                 w_bank = psum_b.tile([P, PASSES, 2, P], F32, tag="b")
@@ -186,20 +175,8 @@ def tile_multiheadedselfattention_pa_kernel(
                     scales=pvk_scales[:, g, b * S : (b + 1) * S],
                     in_=pvk_grouped[:, g].rearrange("p r t -> p (r t)"),
                 )
-            tail = stage.tile([P, NT, DQ - D], F32, bufs=1)
-            nc.gpsimd.tensor_scalar(
-                out=tail[:], in0=pq_sb[b][:, :, D:DQ], scalar1=1.0, scalar2=0.0, op0=ALU.mult, op1=ALU.add
-            )
-            nc.sync.dma_start(out=out[b].rearrange("(p t) c -> p t c", t=NT)[:, :, D:DQ], in_=tail[:])
 
-        def prepare_head(b, h, banks, tag):
-            hg, hh = divmod(h, HG)
-            t_bank = banks.tile([P, 2, NT, P], BF16, tag=tag)
-            for side, x_sb in enumerate((k_sb[b, hg], q_sb[b, hg])):
-                for t in range(NT):
-                    nc.tensor.transpose(t_bank[:, side, t, :], x_sb[:, t, hh * P : (hh + 1) * P], ident_bf[:])
-            nc.scalar.copy(out=kqT[b][:, h], in_=t_bank[:].rearrange("p a t r -> p a (t r)"))
-
+        def prepare_values(b, h, banks, tag):
             cols = slice(h * P, (h + 1) * P)
             v_bank = banks.tile([P, NT, P], F32, tag=tag)
             for t in range(NT):
@@ -227,73 +204,81 @@ def tile_multiheadedselfattention_pa_kernel(
                 in_=v_grouped[:].rearrange("p c t -> p (c t)"),
             )
 
-        def prepare_gate(b, hg):
-            ksum_ps = psum_c.tile([P, HG], F32, tag="c")
-            for hh in range(HG):
+        def prepare_scores(b, h, banks, tag):
+            t_bank = banks.tile([P, 2, NT, P], BF16, tag=tag)
+            for side, x_sb in enumerate((k_sb[b], q_sb[b])):
+                for t in range(NT):
+                    nc.tensor.transpose(t_bank[:, side, t, :], x_sb[:, t, h * P : (h + 1) * P], ident_bf[:])
+            nc.scalar.copy(out=kqT[b][:, h], in_=t_bank[:].rearrange("p a t r -> p a (t r)"))
+
+        def prepare_gate(b):
+            ksum_ps = psum_c.tile([P, H], F32, tag="c")
+            for h in range(H):
                 for t in range(NT):
                     nc.tensor.matmul(
-                        out=ksum_ps[:, hh : hh + 1],
-                        lhsT=k_sb[b, hg][:, t, hh * P : (hh + 1) * P],
+                        out=ksum_ps[:, h : h + 1],
+                        lhsT=k_sb[b][:, t, h * P : (h + 1) * P],
                         rhs=mask_t[:, b * NT + t : b * NT + t + 1],
                         start=(t == 0),
                         stop=(t == NT - 1),
                     )
-            ksum_terms = small.tile([P, HG, 2], BF16)
+            ksum_terms = small.tile([P, H, 2], BF16)
             nc.vector.tensor_copy(out=ksum_terms[:, :, 0], in_=ksum_ps[:])
-            ksum_rest = small.tile([P, HG], F32)
-            nc.vector.tensor_tensor(out=ksum_rest[:], in0=ksum_ps[:], in1=ksum_terms[:, :, 0], op=ALU.subtract)
-            nc.vector.tensor_copy(out=ksum_terms[:, :, 1], in_=ksum_rest[:])
-            pooled_ps = psum_c.tile([P, NT, HG, 2], F32, tag="c")
+            nc.vector.tensor_tensor(
+                out=ksum_terms[:, :, 1], in0=ksum_ps[:], in1=ksum_terms[:, :, 0], op=ALU.subtract
+            )
+            pooled_ps = psum_c.tile([P, NT, H, 2], F32, tag="c")
             for it in range(NT):
-                for hh in range(HG):
+                for h in range(H):
                     nc.tensor.matmul(
-                        out=pooled_ps[:, it, hh, :],
-                        lhsT=kqT[b][:, hg * HG + hh, 1, it * P : (it + 1) * P],
-                        rhs=ksum_terms[:, hh, :],
+                        out=pooled_ps[:, it, h, :],
+                        lhsT=kqT[b][:, h, 1, it * P : (it + 1) * P],
+                        rhs=ksum_terms[:, h, :],
                         start=True,
                         stop=True,
                     )
-            heads = slice(hg * HG, (hg + 1) * HG)
-            pooled = small.tile([P, NT, HG], F32)
+            pooled = small.tile([P, NT, H], F32)
             nc.vector.tensor_reduce(out=pooled[:], in_=pooled_ps[:], axis=AX.X, op=ALU.add)
-            nc.vector.tensor_scalar(
-                out=pooled[:], in0=pooled[:], scalar1=inv_count[:, b : b + 1], scalar2=SCALE,
-                op0=ALU.mult, op1=ALU.mult,
+            nc.vector.tensor_tensor(
+                out=pooled[:], in0=pooled[:], in1=gate_scale[:, b, :].unsqueeze(1).to_broadcast([P, NT, H]),
+                op=ALU.mult,
             )
-            gain = small_bc[:, GAIN0:GATE_BIAS0][:, heads].unsqueeze(1).to_broadcast([P, NT, HG])
-            nc.vector.tensor_tensor(out=pooled[:], in0=pooled[:], in1=gain, op=ALU.mult)
-            gate_bias = small_bc[:, GATE_BIAS0:COUNT0][:, heads].unsqueeze(1).to_broadcast([P, NT, HG])
-            nc.vector.tensor_tensor(out=pooled[:], in0=pooled[:], in1=gate_bias, op=ALU.add)
-            exp_neg = small.tile([P, NT, HG], F32)
+            nc.vector.tensor_tensor(
+                out=pooled[:], in0=pooled[:],
+                in1=small_bc[:, GATE_BIAS0 : GATE_BIAS0 + H].unsqueeze(1).to_broadcast([P, NT, H]), op=ALU.add,
+            )
+            exp_neg = small.tile([P, NT, H], F32)
             nc.scalar.activation(out=exp_neg[:], in_=pooled[:], func=ACT.Exp, scale=-1.0)
             nc.vector.tensor_scalar_add(out=exp_neg[:], in0=exp_neg[:], scalar1=1.0)
-            gate[b, hg] = keep.tile([P, NT, HG], F32, name="gate%d%d" % (b, hg))
-            nc.vector.reciprocal(out=gate[b, hg][:], in_=exp_neg[:])
-            one_minus_gate[b, hg] = keep.tile([P, NT, HG], F32, name="one_minus_gate%d%d" % (b, hg))
+            nc.vector.reciprocal(out=gate[b][:], in_=exp_neg[:])
             nc.vector.tensor_scalar(
-                out=one_minus_gate[b, hg][:], in0=gate[b, hg][:], scalar1=-1.0, scalar2=1.0,
-                op0=ALU.mult, op1=ALU.add,
+                out=one_minus_gate[b][:], in0=gate[b][:], scalar1=-1.0, scalar2=1.0, op0=ALU.mult, op1=ALU.add
             )
+            tail = stage.tile([P, NT, DQ - D], F32, bufs=1)
+            nc.gpsimd.tensor_scalar(
+                out=tail[:], in0=pq_sb[b][:, :, D:DQ], scalar1=1.0, scalar2=0.0, op0=ALU.mult, op1=ALU.add
+            )
+            nc.sync.dma_start(out=out_view[b][:, :, D:DQ], in_=tail[:])
 
-        def attention(b, hg, it):
+        units = [(b, hg, it) for b in range(B) for hg in range(H // HG) for it in range(NT)]
+        e_bf = {}
+        row_sum = {}
+        e_grouped = {}
+        e_codes = {}
+        e_scales = {}
+        h_bank = {}
+        result = {}
+
+        def scores_and_exp(n):
+            b, hg, it = units[n]
             rows = slice(it * P, (it + 1) * P)
-            result = stage.tile([P, W], F32, bufs=3)
-            for hh in range(HG):
-                nc.gpsimd.tensor_scalar(
-                    out=result[:, hh * P : (hh + 1) * P],
-                    in0=pq_sb[b][:, it, (hg * HG + hh) * P : (hg * HG + hh + 1) * P],
-                    scalar1=one_minus_gate[b, hg][:, it, hh : hh + 1],
-                    scalar2=0.0,
-                    op0=ALU.mult,
-                    op1=ALU.add,
-                )
             row_max = small.tile([P, HG], F32)
             exp_bias = small.tile([P, HG], F32)
-            e_bf = stage.tile([P, HG, S], BF16, bufs=3)
-            row_sum = small.tile([P, HG], F32)
+            e_bf[n] = stage.tile([P, HG, S], BF16, name="e_bf")
+            row_sum[n] = small.tile([P, HG], F32, name="row_sum", bufs=5)
             for hh in range(HG):
                 h = hg * HG + hh
-                s_bank = psum_s.tile([P, S], F32, tag="s", name="s_bank%d" % hh)
+                s_bank = psum_s.tile([P, S], F32, tag="s")
                 for t in range(NT):
                     nc.tensor.matmul(
                         out=s_bank[:, t * P : (t + 1) * P], lhsT=mask_bias_t[:, b * NT + t, :], rhs=ident_f32[:],
@@ -308,16 +293,18 @@ def tile_multiheadedselfattention_pa_kernel(
                     op0=ALU.mult, op1=ALU.add,
                 )
                 nc.scalar.activation(
-                    out=e_bf[:, hh, :],
+                    out=e_bf[n][:, hh, :],
                     in_=s_bank[:],
                     func=ACT.Exp,
                     bias=exp_bias[:, hh : hh + 1],
                     scale=SCALE,
-                    accum_out=row_sum[:, hh : hh + 1],
+                    accum_out=row_sum[n][:, hh : hh + 1],
                 )
-            e_words = e_bf[:].bitcast(F32)
-            e_grouped = stage.tile([P, HG, P, 4], BF16, align_bytes=64)
-            e_grouped_words = e_grouped[:].bitcast(F32)
+
+        def transpose_e(n):
+            e_words = e_bf[n][:].bitcast(F32)
+            e_grouped[n] = stage.tile([P, HG, P, 4], BF16, align_bytes=64, name="e_grouped")
+            e_grouped_words = e_grouped[n][:].bitcast(F32)
             for pair in range(HG // 2):
                 e_bank = psum_b.tile([P, 2, 2, P], F32, tag="b")
                 for h2 in range(2):
@@ -329,54 +316,83 @@ def tile_multiheadedselfattention_pa_kernel(
                     out=e_grouped_words[:, 2 * pair : 2 * pair + 2, :, :],
                     in_=e_bank[:].rearrange("p h u i -> p h i u"),
                 )
-            e_codes = stage.tile([P, W], U32, align_bytes=64, bufs=3)
-            e_scales = stage.tile([P, W], U8, align_bytes=64, bufs=3)
+
+        def quantise_e(n):
+            b, hg, it = units[n]
+            e_codes[n] = stage.tile([P, W], U32, align_bytes=64, name="e_codes")
+            e_scales[n] = stage.tile([P, W], U8, align_bytes=64, name="e_scales")
             nc.vector.quantize_mx(
-                out=e_codes[:].bitcast(FP8X4),
-                scales=e_scales[:],
-                in_=e_grouped[:].rearrange("p h i t -> p (h i t)"),
+                out=e_codes[n][:].bitcast(FP8X4),
+                scales=e_scales[n][:],
+                in_=e_grouped[n][:].rearrange("p h i t -> p (h i t)"),
             )
-            h_bank = psum_h.tile([P, HG, P], F32, tag="h")
+            result[n] = stage.tile([P, W], F32, name="result", bufs=3)
+            for hh in range(HG):
+                h = hg * HG + hh
+                nc.gpsimd.tensor_scalar(
+                    out=result[n][:, hh * P : (hh + 1) * P],
+                    in0=pq_sb[b][:, it, h * P : (h + 1) * P],
+                    scalar1=one_minus_gate[b][:, it, h : h + 1],
+                    scalar2=0.0,
+                    op0=ALU.mult,
+                    op1=ALU.add,
+                )
+
+        def e_times_v(n):
+            b, hg, it = units[n]
+            h_bank[n] = psum_h.tile([P, HG, P], F32, tag="h", name="h_bank")
             for hh in range(HG):
                 h = hg * HG + hh
                 nc.tensor.matmul_mx(
-                    out=h_bank[:, hh, :],
-                    lhsT=e_codes[:, hh * P : (hh + 1) * P].bitcast(FP8X4),
-                    lhsT_scale=e_scales[:, hh * P : (hh + 1) * P],
+                    out=h_bank[n][:, hh, :],
+                    lhsT=e_codes[n][:, hh * P : (hh + 1) * P].bitcast(FP8X4),
+                    lhsT_scale=e_scales[n][:, hh * P : (hh + 1) * P],
                     rhs=v_codes[:, b, h * P : (h + 1) * P].bitcast(FP8X4),
                     rhs_scale=v_scales[:, b, h * P : (h + 1) * P],
                     start=True,
                     stop=True,
                 )
+
+        def blend(n):
+            b, hg, it = units[n]
             weight = small.tile([P, HG], F32)
-            nc.vector.reciprocal(out=weight[:], in_=row_sum[:])
-            nc.vector.tensor_tensor(out=weight[:], in0=weight[:], in1=gate[b, hg][:, it, :], op=ALU.mult)
+            nc.vector.reciprocal(out=weight[:], in_=row_sum[n][:])
+            nc.vector.tensor_tensor(
+                out=weight[:], in0=weight[:], in1=gate[b][:, it, hg * HG : (hg + 1) * HG], op=ALU.mult
+            )
             for hh in range(HG):
                 cols = slice(hh * P, (hh + 1) * P)
                 nc.vector.scalar_tensor_tensor(
-                    out=result[:, cols],
-                    in0=h_bank[:, hh, :],
+                    out=result[n][:, cols],
+                    in0=h_bank[n][:, hh, :],
                     scalar=weight[:, hh : hh + 1],
-                    in1=result[:, cols],
+                    in1=result[n][:, cols],
                     op0=ALU.mult,
                     op1=ALU.add,
                 )
-            nc.sync.dma_start(
-                out=out[b].rearrange("(p t) c -> p t c", t=NT)[:, it, hg * W : (hg + 1) * W], in_=result[:]
-            )
+            nc.sync.dma_start(out=out_view[b][:, it, hg * W : (hg + 1) * W], in_=result[n][:])
 
-        groups = [(b, hg) for b in range(B) for hg in range(H // HG)]
-        prepare_tokens(0)
-        for hh in range(HG):
-            prepare_head(0, hh, psum_s, "s")
-        prepare_gate(0, 0)
-        for n, (b, hg) in enumerate(groups):
-            following = groups[n + 1] if n + 1 < len(groups) else None
-            if following is not None and following[0] != b:
-                prepare_tokens(following[0])
-            for it in range(NT):
-                attention(b, hg, it)
-                if following is not None:
-                    prepare_head(following[0], following[1] * HG + it, psum_c, "c")
-            if following is not None:
-                prepare_gate(following[0], following[1])
+        for b in range(B):
+            prepare_tokens(b)
+        for h in range(H):
+            prepare_values(0, h, psum_s, "s")
+        for h in range(H):
+            prepare_scores(0, h, psum_s, "s")
+        per_batch = len(units) // B
+        for step in range(len(units) + 3):
+            if step < len(units):
+                scores_and_exp(step)
+            if step < H:
+                prepare_values(1, step, psum_c, "c")
+            if 3 <= step:
+                e_times_v(step - 3)
+            if 1 <= step <= len(units):
+                transpose_e(step - 1)
+            if step < H:
+                prepare_scores(1, step, psum_c, "c")
+            if step % per_batch == 0 and step < len(units):
+                prepare_gate(step // per_batch)
+            if 2 <= step <= len(units) + 1:
+                quantise_e(step - 2)
+            if 3 <= step:
+                blend(step - 3)

@@ -152,8 +152,6 @@ def tile_multiheadedselfattention_pa_kernel(
         v_codes = keep.tile([P, B, D], U32, align_bytes=64)
         v_scales = keep.tile([P, B, D], U8, align_bytes=64)
         kqT = [keep.tile([P, H, 2, S], BF16, name="kqT%d" % b) for b in range(B)]
-        gate = [keep.tile([P, NT, H], F32, name="gate%d" % b) for b in range(B)]
-        one_minus_gate = [keep.tile([P, NT, H], F32, name="one_minus_gate%d" % b) for b in range(B)]
 
         def prepare_tokens(b):
             pvk_words = pvk_sb[b][:].bitcast(F32)
@@ -176,7 +174,9 @@ def tile_multiheadedselfattention_pa_kernel(
                     in_=pvk_grouped[:, g].rearrange("p r t -> p (r t)"),
                 )
 
-        def prepare_values(b, h, banks, tag):
+        v_grouped = {}
+
+        def values_matmul(b, h, banks, tag):
             cols = slice(h * P, (h + 1) * P)
             v_bank = banks.tile([P, NT, P], F32, tag=tag)
             for t in range(NT):
@@ -191,17 +191,20 @@ def tile_multiheadedselfattention_pa_kernel(
                         start=(g == 0),
                         stop=(g == PASSES - 1),
                     )
-            v_grouped = stage.tile([P, P, NT], BF16, align_bytes=64)
+            v_grouped[b, h] = stage.tile([P, P, NT], BF16, align_bytes=64, name="v_grouped")
             nc.vector.tensor_tensor(
-                out=v_grouped[:],
+                out=v_grouped[b, h][:],
                 in0=v_bank[:].rearrange("p t c -> p c t"),
                 in1=small_bc[:, cols].unsqueeze(2).to_broadcast([P, P, NT]),
                 op=ALU.add,
             )
+
+        def values_quantise(b, h):
+            cols = slice(h * P, (h + 1) * P)
             nc.vector.quantize_mx(
                 out=v_codes[:, b, cols].bitcast(FP8X4),
                 scales=v_scales[:, b, cols],
-                in_=v_grouped[:].rearrange("p c t -> p (c t)"),
+                in_=v_grouped[b, h][:].rearrange("p c t -> p (c t)"),
             )
 
         def prepare_scores(b, h, banks, tag):
@@ -211,49 +214,65 @@ def tile_multiheadedselfattention_pa_kernel(
                     nc.tensor.transpose(t_bank[:, side, t, :], x_sb[:, t, h * P : (h + 1) * P], ident_bf[:])
             nc.scalar.copy(out=kqT[b][:, h], in_=t_bank[:].rearrange("p a t r -> p a (t r)"))
 
-        def prepare_gate(b):
-            ksum_ps = psum_c.tile([P, H], F32, tag="c")
-            for h in range(H):
+        ksum_terms = {}
+        gate = {}
+        one_minus_gate = {}
+
+        def gate_keys(b, hg):
+            ksum_ps = psum_b.tile([P, HG], F32, tag="b")
+            for hh in range(HG):
+                h = hg * HG + hh
                 for t in range(NT):
                     nc.tensor.matmul(
-                        out=ksum_ps[:, h : h + 1],
+                        out=ksum_ps[:, hh : hh + 1],
                         lhsT=k_sb[b][:, t, h * P : (h + 1) * P],
                         rhs=mask_t[:, b * NT + t : b * NT + t + 1],
                         start=(t == 0),
                         stop=(t == NT - 1),
                     )
-            ksum_terms = small.tile([P, H, 2], BF16)
-            nc.vector.tensor_copy(out=ksum_terms[:, :, 0], in_=ksum_ps[:])
+            ksum_terms[b, hg] = small.tile([P, HG, 2], BF16, name="ksum_terms")
+            nc.vector.tensor_copy(out=ksum_terms[b, hg][:, :, 0], in_=ksum_ps[:])
             nc.vector.tensor_tensor(
-                out=ksum_terms[:, :, 1], in0=ksum_ps[:], in1=ksum_terms[:, :, 0], op=ALU.subtract
+                out=ksum_terms[b, hg][:, :, 1], in0=ksum_ps[:], in1=ksum_terms[b, hg][:, :, 0], op=ALU.subtract
             )
-            pooled_ps = psum_c.tile([P, NT, H, 2], F32, tag="c")
+
+        def gate_queries(b, hg):
+            heads = slice(hg * HG, (hg + 1) * HG)
+            pooled_ps = psum_b.tile([P, NT, HG, 2], F32, tag="b")
             for it in range(NT):
-                for h in range(H):
+                for hh in range(HG):
                     nc.tensor.matmul(
-                        out=pooled_ps[:, it, h, :],
-                        lhsT=kqT[b][:, h, 1, it * P : (it + 1) * P],
-                        rhs=ksum_terms[:, h, :],
+                        out=pooled_ps[:, it, hh, :],
+                        lhsT=kqT[b][:, hg * HG + hh, 1, it * P : (it + 1) * P],
+                        rhs=ksum_terms[b, hg][:, hh, :],
                         start=True,
                         stop=True,
                     )
-            pooled = small.tile([P, NT, H], F32)
+            pooled = small.tile([P, NT, HG], F32)
             nc.vector.tensor_reduce(out=pooled[:], in_=pooled_ps[:], axis=AX.X, op=ALU.add)
-            nc.vector.tensor_tensor(
-                out=pooled[:], in0=pooled[:], in1=gate_scale[:, b, :].unsqueeze(1).to_broadcast([P, NT, H]),
+            scaled = small.tile([P, NT, HG], F32)
+            nc.gpsimd.tensor_tensor(
+                out=scaled[:], in0=pooled[:], in1=gate_scale[:, b, heads].unsqueeze(1).to_broadcast([P, NT, HG]),
                 op=ALU.mult,
             )
-            nc.vector.tensor_tensor(
-                out=pooled[:], in0=pooled[:],
-                in1=small_bc[:, GATE_BIAS0 : GATE_BIAS0 + H].unsqueeze(1).to_broadcast([P, NT, H]), op=ALU.add,
+            shifted = small.tile([P, NT, HG], F32)
+            nc.gpsimd.tensor_tensor(
+                out=shifted[:], in0=scaled[:],
+                in1=small_bc[:, GATE_BIAS0 : GATE_BIAS0 + H][:, heads].unsqueeze(1).to_broadcast([P, NT, HG]),
+                op=ALU.add,
             )
-            exp_neg = small.tile([P, NT, H], F32)
-            nc.scalar.activation(out=exp_neg[:], in_=pooled[:], func=ACT.Exp, scale=-1.0)
-            nc.vector.tensor_scalar_add(out=exp_neg[:], in0=exp_neg[:], scalar1=1.0)
-            nc.vector.reciprocal(out=gate[b][:], in_=exp_neg[:])
-            nc.vector.tensor_scalar(
-                out=one_minus_gate[b][:], in0=gate[b][:], scalar1=-1.0, scalar2=1.0, op0=ALU.mult, op1=ALU.add
+            tanh_half = small.tile([P, NT, HG], F32)
+            nc.scalar.activation(out=tanh_half[:], in_=shifted[:], func=ACT.Tanh, scale=0.5)
+            gate[b, hg] = keep.tile([P, NT, HG], F32, name="gate%d%d" % (b, hg))
+            nc.gpsimd.tensor_scalar(
+                out=gate[b, hg][:], in0=tanh_half[:], scalar1=0.5, scalar2=0.5, op0=ALU.mult, op1=ALU.add
             )
+            one_minus_gate[b, hg] = keep.tile([P, NT, HG], F32, name="one_minus_gate%d%d" % (b, hg))
+            nc.gpsimd.tensor_scalar(
+                out=one_minus_gate[b, hg][:], in0=tanh_half[:], scalar1=-0.5, scalar2=0.5, op0=ALU.mult, op1=ALU.add
+            )
+
+        def copy_tail(b):
             tail = stage.tile([P, NT, DQ - D], F32, bufs=1)
             nc.gpsimd.tensor_scalar(
                 out=tail[:], in0=pq_sb[b][:, :, D:DQ], scalar1=1.0, scalar2=0.0, op0=ALU.mult, op1=ALU.add
@@ -261,13 +280,25 @@ def tile_multiheadedselfattention_pa_kernel(
             nc.sync.dma_start(out=out_view[b][:, :, D:DQ], in_=tail[:])
 
         units = [(b, hg, it) for b in range(B) for hg in range(H // HG) for it in range(NT)]
+        s_banks = {}
         e_bf = {}
         row_sum = {}
         e_grouped = {}
         e_codes = {}
         e_scales = {}
+        weight = {}
         h_bank = {}
         result = {}
+
+        def fill_mask_bias(n):
+            b, hg, it = units[n]
+            s_banks[n] = [psum_s.tile([P, S], F32, tag="s", name="s_bank") for hh in range(HG)]
+            for hh in range(HG):
+                for t in range(NT):
+                    nc.tensor.matmul(
+                        out=s_banks[n][hh][:, t * P : (t + 1) * P], lhsT=mask_bias_t[:, b * NT + t, :],
+                        rhs=ident_f32[:], is_transpose=True, start=(t == 0), stop=False,
+                    )
 
         def scores_and_exp(n):
             b, hg, it = units[n]
@@ -275,15 +306,10 @@ def tile_multiheadedselfattention_pa_kernel(
             row_max = small.tile([P, HG], F32)
             exp_bias = small.tile([P, HG], F32)
             e_bf[n] = stage.tile([P, HG, S], BF16, name="e_bf")
-            row_sum[n] = small.tile([P, HG], F32, name="row_sum", bufs=5)
+            row_sum[n] = small.tile([P, HG], F32, name="row_sum", bufs=4)
             for hh in range(HG):
                 h = hg * HG + hh
-                s_bank = psum_s.tile([P, S], F32, tag="s")
-                for t in range(NT):
-                    nc.tensor.matmul(
-                        out=s_bank[:, t * P : (t + 1) * P], lhsT=mask_bias_t[:, b * NT + t, :], rhs=ident_f32[:],
-                        is_transpose=True, start=(t == 0), stop=False,
-                    )
+                s_bank = s_banks[n][hh]
                 nc.tensor.matmul(
                     out=s_bank[:], lhsT=kqT[b][:, h, 1, rows], rhs=kqT[b][:, h, 0, :], start=False, stop=True
                 )
@@ -317,8 +343,25 @@ def tile_multiheadedselfattention_pa_kernel(
                     in_=e_bank[:].rearrange("p h u i -> p h i u"),
                 )
 
-        def quantise_e(n):
+        def blend_weights(n):
             b, hg, it = units[n]
+            inv_sum = small.tile([P, HG], F32)
+            nc.vector.reciprocal(out=inv_sum[:], in_=row_sum[n][:])
+            weight[n] = small.tile([P, HG], F32, name="weight", bufs=3)
+            nc.gpsimd.tensor_tensor(out=weight[n][:], in0=inv_sum[:], in1=gate[b, hg][:, it, :], op=ALU.mult)
+            result[n] = stage.tile([P, W], F32, name="result", bufs=3)
+            for hh in range(HG):
+                h = hg * HG + hh
+                nc.gpsimd.tensor_scalar(
+                    out=result[n][:, hh * P : (hh + 1) * P],
+                    in0=pq_sb[b][:, it, h * P : (h + 1) * P],
+                    scalar1=one_minus_gate[b, hg][:, it, hh : hh + 1],
+                    scalar2=0.0,
+                    op0=ALU.mult,
+                    op1=ALU.add,
+                )
+
+        def quantise_e(n):
             e_codes[n] = stage.tile([P, W], U32, align_bytes=64, name="e_codes")
             e_scales[n] = stage.tile([P, W], U8, align_bytes=64, name="e_scales")
             nc.vector.quantize_mx(
@@ -326,17 +369,6 @@ def tile_multiheadedselfattention_pa_kernel(
                 scales=e_scales[n][:],
                 in_=e_grouped[n][:].rearrange("p h i t -> p (h i t)"),
             )
-            result[n] = stage.tile([P, W], F32, name="result", bufs=3)
-            for hh in range(HG):
-                h = hg * HG + hh
-                nc.gpsimd.tensor_scalar(
-                    out=result[n][:, hh * P : (hh + 1) * P],
-                    in0=pq_sb[b][:, it, h * P : (h + 1) * P],
-                    scalar1=one_minus_gate[b][:, it, h : h + 1],
-                    scalar2=0.0,
-                    op0=ALU.mult,
-                    op1=ALU.add,
-                )
 
         def e_times_v(n):
             b, hg, it = units[n]
@@ -355,44 +387,59 @@ def tile_multiheadedselfattention_pa_kernel(
 
         def blend(n):
             b, hg, it = units[n]
-            weight = small.tile([P, HG], F32)
-            nc.vector.reciprocal(out=weight[:], in_=row_sum[n][:])
-            nc.vector.tensor_tensor(
-                out=weight[:], in0=weight[:], in1=gate[b][:, it, hg * HG : (hg + 1) * HG], op=ALU.mult
-            )
             for hh in range(HG):
                 cols = slice(hh * P, (hh + 1) * P)
                 nc.vector.scalar_tensor_tensor(
                     out=result[n][:, cols],
                     in0=h_bank[n][:, hh, :],
-                    scalar=weight[:, hh : hh + 1],
+                    scalar=weight[n][:, hh : hh + 1],
                     in1=result[n][:, cols],
                     op0=ALU.mult,
                     op1=ALU.add,
                 )
             nc.sync.dma_start(out=out_view[b][:, it, hg * W : (hg + 1) * W], in_=result[n][:])
 
+        heads = [(b, h) for b in range(B) for h in range(H)]
+        groups = [(b, hg) for b in range(B) for hg in range(H // HG)]
         for b in range(B):
             prepare_tokens(b)
-        for h in range(H):
-            prepare_values(0, h, psum_s, "s")
-        for h in range(H):
-            prepare_scores(0, h, psum_s, "s")
-        per_batch = len(units) // B
+        for n in range(HG):
+            values_matmul(heads[n][0], heads[n][1], psum_s, "s")
+            if n > 0:
+                values_quantise(heads[n - 1][0], heads[n - 1][1])
+        values_quantise(heads[HG - 1][0], heads[HG - 1][1])
+        gate_keys(0, 0)
+        for n in range(HG):
+            prepare_scores(heads[n][0], heads[n][1], psum_s, "s")
+        gate_queries(0, 0)
+        fill_mask_bias(0)
+        last = len(units) - 1
         for step in range(len(units) + 3):
-            if step < len(units):
+            coming = heads[step + HG] if step + HG < len(heads) else None
+            next_group = groups[step // NT + 1] if step // NT + 1 < len(groups) else None
+            if step <= last:
                 scores_and_exp(step)
-            if step < H:
-                prepare_values(1, step, psum_c, "c")
+            if 2 <= step <= last + 2:
+                blend_weights(step - 2)
+            if coming is not None:
+                values_matmul(coming[0], coming[1], psum_c, "c")
             if 3 <= step:
                 e_times_v(step - 3)
-            if 1 <= step <= len(units):
+            if coming is not None:
+                prepare_scores(coming[0], coming[1], psum_c, "c")
+            if 1 <= step <= last + 1:
                 transpose_e(step - 1)
-            if step < H:
-                prepare_scores(1, step, psum_c, "c")
-            if step % per_batch == 0 and step < len(units):
-                prepare_gate(step // per_batch)
-            if 2 <= step <= len(units) + 1:
+            if step + 1 <= last:
+                fill_mask_bias(step + 1)
+            if 2 <= step <= last + 2:
                 quantise_e(step - 2)
+            if coming is not None:
+                values_quantise(coming[0], coming[1])
             if 3 <= step:
                 blend(step - 3)
+            if next_group is not None and step % NT == 1:
+                gate_keys(next_group[0], next_group[1])
+            if next_group is not None and step % NT == 3:
+                gate_queries(next_group[0], next_group[1])
+            if step <= last and units[step][1:] == (0, NT - 1):
+                copy_tail(units[step][0])

@@ -53,19 +53,19 @@ def tile_multiheadedselfattention_pa_kernel(
 
         mask_rows = const.tile([P, P], BF16)
         nc.vector.memset(mask_rows[:], 0.0)
-        nc.scalar.dma_start(
+        nc.sync.dma_start(
             out=mask_rows[0 : B * NT, :], in_=value_key_masks.rearrange("b (t p) -> (b t) p", p=P)
         )
         small_row = const.tile([P, ROW_W], BF16)
         nc.vector.memset(small_row[:], 0.0)
-        nc.scalar.dma_start(out=small_row[0:1, 0:D], in_=bv.rearrange("(o n) -> o n", o=1))
-        nc.scalar.dma_start(
+        nc.sync.dma_start(out=small_row[0:1, 0:D], in_=bv.rearrange("(o n) -> o n", o=1))
+        nc.sync.dma_start(
             out=small_row[0:1, GAIN0 : GAIN0 + H], in_=overall_gain.rearrange("a h b c -> a (h b c)")
         )
-        nc.scalar.dma_start(
+        nc.sync.dma_start(
             out=small_row[0:1, GATE_BIAS0 : GATE_BIAS0 + H], in_=overall_bias.rearrange("a h b c -> a (h b c)")
         )
-        nc.scalar.dma_start(
+        nc.sync.dma_start(
             out=small_row[0:1, COUNT0 : COUNT0 + B], in_=value_key_counts.rearrange("(o n) -> o n", o=1)
         )
 
@@ -106,6 +106,12 @@ def tile_multiheadedselfattention_pa_kernel(
         nc.vector.tensor_scalar(
             out=mask_bias_t[:], in0=mask_t[:].unsqueeze(2).to_broadcast([P, B * NT, P]),
             scalar1=1.0, scalar2=MASKED, op0=ALU.subtract, op1=ALU.mult,
+        )
+
+        mask_diag = const.tile([P, B * NT, P], BF16)
+        nc.vector.tensor_tensor(
+            out=mask_diag[:], in0=ident_bf[:].unsqueeze(1).to_broadcast([P, B * NT, P]),
+            in1=mask_t[:].unsqueeze(2).to_broadcast([P, B * NT, P]), op=ALU.mult,
         )
 
         small_bc = const.tile([P, ROW_W], F32)
@@ -207,33 +213,32 @@ def tile_multiheadedselfattention_pa_kernel(
                 in_=v_grouped[b, h][:].rearrange("p c t -> p (c t)"),
             )
 
+        ksum = [keep.tile([P, H], F32, name="ksum%d" % b) for b in range(B)]
+
         def prepare_scores(b, h, banks, tag):
+            cols = slice(h * P, (h + 1) * P)
             t_bank = banks.tile([P, 2, NT, P], BF16, tag=tag)
-            for side, x_sb in enumerate((k_sb[b], q_sb[b])):
-                for t in range(NT):
-                    nc.tensor.transpose(t_bank[:, side, t, :], x_sb[:, t, h * P : (h + 1) * P], ident_bf[:])
-            nc.scalar.copy(out=kqT[b][:, h], in_=t_bank[:].rearrange("p a t r -> p a (t r)"))
+            for t in range(NT):
+                nc.tensor.transpose(t_bank[:, 0, t, :], k_sb[b][:, t, cols], mask_diag[:, b * NT + t, :])
+            for t in range(NT):
+                nc.tensor.transpose(t_bank[:, 1, t, :], q_sb[b][:, t, cols], ident_bf[:])
+            nc.scalar.activation(
+                out=kqT[b][:, h, 0, :], in_=t_bank[:, 0].rearrange("p t r -> p (t r)"), func=ACT.Copy,
+                accum_out=ksum[b][:, h : h + 1],
+            )
+            nc.scalar.copy(out=kqT[b][:, h, 1, :], in_=t_bank[:, 1].rearrange("p t r -> p (t r)"))
 
         ksum_terms = {}
         gate = {}
         one_minus_gate = {}
 
         def gate_keys(b, hg):
-            ksum_ps = psum_b.tile([P, HG], F32, tag="b")
-            for hh in range(HG):
-                h = hg * HG + hh
-                for t in range(NT):
-                    nc.tensor.matmul(
-                        out=ksum_ps[:, hh : hh + 1],
-                        lhsT=k_sb[b][:, t, h * P : (h + 1) * P],
-                        rhs=mask_t[:, b * NT + t : b * NT + t + 1],
-                        start=(t == 0),
-                        stop=(t == NT - 1),
-                    )
+            heads = slice(hg * HG, (hg + 1) * HG)
             ksum_terms[b, hg] = small.tile([P, HG, 2], BF16, name="ksum_terms")
-            nc.vector.tensor_copy(out=ksum_terms[b, hg][:, :, 0], in_=ksum_ps[:])
-            nc.vector.tensor_tensor(
-                out=ksum_terms[b, hg][:, :, 1], in0=ksum_ps[:], in1=ksum_terms[b, hg][:, :, 0], op=ALU.subtract
+            nc.gpsimd.tensor_copy(out=ksum_terms[b, hg][:, :, 0], in_=ksum[b][:, heads])
+            nc.gpsimd.tensor_tensor(
+                out=ksum_terms[b, hg][:, :, 1], in0=ksum[b][:, heads], in1=ksum_terms[b, hg][:, :, 0],
+                op=ALU.subtract,
             )
 
         def gate_queries(b, hg):
@@ -280,7 +285,6 @@ def tile_multiheadedselfattention_pa_kernel(
             nc.sync.dma_start(out=out_view[b][:, :, D:DQ], in_=tail[:])
 
         units = [(b, hg, it) for b in range(B) for hg in range(H // HG) for it in range(NT)]
-        s_banks = {}
         e_bf = {}
         row_sum = {}
         e_grouped = {}
@@ -289,16 +293,6 @@ def tile_multiheadedselfattention_pa_kernel(
         weight = {}
         h_bank = {}
         result = {}
-
-        def fill_mask_bias(n):
-            b, hg, it = units[n]
-            s_banks[n] = [psum_s.tile([P, S], F32, tag="s", name="s_bank") for hh in range(HG)]
-            for hh in range(HG):
-                for t in range(NT):
-                    nc.tensor.matmul(
-                        out=s_banks[n][hh][:, t * P : (t + 1) * P], lhsT=mask_bias_t[:, b * NT + t, :],
-                        rhs=ident_f32[:], is_transpose=True, start=(t == 0), stop=False,
-                    )
 
         def scores_and_exp(n):
             b, hg, it = units[n]
@@ -309,7 +303,12 @@ def tile_multiheadedselfattention_pa_kernel(
             row_sum[n] = small.tile([P, HG], F32, name="row_sum", bufs=4)
             for hh in range(HG):
                 h = hg * HG + hh
-                s_bank = s_banks[n][hh]
+                s_bank = psum_s.tile([P, S], F32, tag="s")
+                for t in range(NT):
+                    nc.tensor.matmul(
+                        out=s_bank[:, t * P : (t + 1) * P], lhsT=mask_bias_t[:, b * NT + t, :], rhs=ident_f32[:],
+                        is_transpose=True, start=(t == 0), stop=False,
+                    )
                 nc.tensor.matmul(
                     out=s_bank[:], lhsT=kqT[b][:, h, 1, rows], rhs=kqT[b][:, h, 0, :], start=False, stop=True
                 )
@@ -408,38 +407,33 @@ def tile_multiheadedselfattention_pa_kernel(
             if n > 0:
                 values_quantise(heads[n - 1][0], heads[n - 1][1])
         values_quantise(heads[HG - 1][0], heads[HG - 1][1])
-        gate_keys(0, 0)
         for n in range(HG):
             prepare_scores(heads[n][0], heads[n][1], psum_s, "s")
-        gate_queries(0, 0)
-        fill_mask_bias(0)
+        gate_keys(0, 0)
         last = len(units) - 1
         for step in range(len(units) + 3):
             coming = heads[step + HG] if step + HG < len(heads) else None
-            next_group = groups[step // NT + 1] if step // NT + 1 < len(groups) else None
             if step <= last:
                 scores_and_exp(step)
+            if step <= last and step % NT == 0:
+                gate_queries(groups[step // NT][0], groups[step // NT][1])
             if 2 <= step <= last + 2:
                 blend_weights(step - 2)
             if coming is not None:
                 values_matmul(coming[0], coming[1], psum_c, "c")
             if 3 <= step:
                 e_times_v(step - 3)
-            if coming is not None:
-                prepare_scores(coming[0], coming[1], psum_c, "c")
             if 1 <= step <= last + 1:
                 transpose_e(step - 1)
-            if step + 1 <= last:
-                fill_mask_bias(step + 1)
+            if coming is not None:
+                prepare_scores(coming[0], coming[1], psum_c, "c")
             if 2 <= step <= last + 2:
                 quantise_e(step - 2)
             if coming is not None:
                 values_quantise(coming[0], coming[1])
             if 3 <= step:
                 blend(step - 3)
-            if next_group is not None and step % NT == 1:
-                gate_keys(next_group[0], next_group[1])
-            if next_group is not None and step % NT == 3:
-                gate_queries(next_group[0], next_group[1])
+            if coming is not None and step % NT == NT - 1:
+                gate_keys(groups[step // NT + 1][0], groups[step // NT + 1][1])
             if step <= last and units[step][1:] == (0, NT - 1):
                 copy_tail(units[step][0])

@@ -25,6 +25,7 @@ HG = 4
 W = HG * P
 SCALE = 1.0 / math.sqrt(P)
 MASKED = 1.0e30
+MASKED_BY_VECTOR = 1
 
 GAIN0 = D
 GATE_BIAS0 = D + 16
@@ -108,6 +109,12 @@ def tile_multiheadedselfattention_pa_kernel(
             scalar1=1.0, scalar2=MASKED, op0=ALU.subtract, op1=ALU.mult,
         )
 
+        mask_bias_bc = const.tile([P, B, S], BF16)
+        for b in range(B):
+            bias_ps = psum_s.tile([P, S], F32, tag="s")
+            for t in range(NT):
+                nc.tensor.transpose(bias_ps[:, t * P : (t + 1) * P], mask_bias_t[:, b * NT + t, :], ident_f32[:])
+            nc.scalar.copy(out=mask_bias_bc[:, b, :], in_=bias_ps[:])
         mask_diag = const.tile([P, B * NT, P], BF16)
         nc.vector.tensor_tensor(
             out=mask_diag[:], in0=ident_bf[:].unsqueeze(1).to_broadcast([P, B * NT, P]),
@@ -126,12 +133,12 @@ def tile_multiheadedselfattention_pa_kernel(
         wv_codes = keep.tile([P, PASSES, D], U32, align_bytes=64)
         wv_scales = keep.tile([P, PASSES, D], U8, align_bytes=64)
         for g in range(PASSES):
-            grouped_v = stage.tile([P, S, 4], BF16, align_bytes=64)
+            grouped_v = stage.tile([P, S, 4], BF16, align_bytes=64, tag="e_bf")
             nc.vector.tensor_copy(
                 out=grouped_v[:].rearrange("p (c i) t -> p c t i", i=4),
                 in_=wv_raw[:, g, :, 0:S].rearrange("p t (c i) -> p c t i", i=4),
             )
-            grouped_s = stage.tile([P, S, 4], BF16, align_bytes=64)
+            grouped_s = stage.tile([P, S, 4], BF16, align_bytes=64, tag="e_grouped")
             nc.scalar.copy(
                 out=grouped_s[:].rearrange("p (c i) t -> p c t i", i=4),
                 in_=wv_raw[:, g, :, S:D].rearrange("p t (c i) -> p c t i", i=4),
@@ -299,27 +306,35 @@ def tile_multiheadedselfattention_pa_kernel(
             rows = slice(it * P, (it + 1) * P)
             row_max = small.tile([P, HG], F32)
             exp_bias = small.tile([P, HG], F32)
-            e_bf[n] = stage.tile([P, HG, S], BF16, name="e_bf")
+            e_bf[n] = stage.tile([P, HG, S], BF16, align_bytes=64, name="e_bf")
             row_sum[n] = small.tile([P, HG], F32, name="row_sum", bufs=4)
             for hh in range(HG):
                 h = hg * HG + hh
                 s_bank = psum_s.tile([P, S], F32, tag="s")
-                for t in range(NT):
+                if hh >= MASKED_BY_VECTOR:
+                    for t in range(NT):
+                        nc.tensor.matmul(
+                            out=s_bank[:, t * P : (t + 1) * P], lhsT=mask_bias_t[:, b * NT + t, :], rhs=ident_f32[:],
+                            is_transpose=True, start=(t == 0), stop=False,
+                        )
                     nc.tensor.matmul(
-                        out=s_bank[:, t * P : (t + 1) * P], lhsT=mask_bias_t[:, b * NT + t, :], rhs=ident_f32[:],
-                        is_transpose=True, start=(t == 0), stop=False,
+                        out=s_bank[:], lhsT=kqT[b][:, h, 1, rows], rhs=kqT[b][:, h, 0, :], start=False, stop=True
                     )
-                nc.tensor.matmul(
-                    out=s_bank[:], lhsT=kqT[b][:, h, 1, rows], rhs=kqT[b][:, h, 0, :], start=False, stop=True
-                )
-                nc.vector.tensor_reduce(out=row_max[:, hh : hh + 1], in_=s_bank[:], axis=AX.X, op=ALU.max)
+                    scores = s_bank
+                else:
+                    nc.tensor.matmul(
+                        out=s_bank[:], lhsT=kqT[b][:, h, 1, rows], rhs=kqT[b][:, h, 0, :], start=True, stop=True
+                    )
+                    scores = stage.tile([P, S], F32, name="masked_scores")
+                    nc.vector.tensor_tensor(out=scores[:], in0=s_bank[:], in1=mask_bias_bc[:, b, :], op=ALU.add)
+                nc.vector.tensor_reduce(out=row_max[:, hh : hh + 1], in_=scores[:], axis=AX.X, op=ALU.max)
                 nc.gpsimd.tensor_scalar(
                     out=exp_bias[:, hh : hh + 1], in0=row_max[:, hh : hh + 1], scalar1=-SCALE, scalar2=0.0,
                     op0=ALU.mult, op1=ALU.add,
                 )
                 nc.scalar.activation(
                     out=e_bf[n][:, hh, :],
-                    in_=s_bank[:],
+                    in_=scores[:],
                     func=ACT.Exp,
                     bias=exp_bias[:, hh : hh + 1],
                     scale=SCALE,

@@ -25,7 +25,6 @@ HG = 4
 W = HG * P
 SCALE = 1.0 / math.sqrt(P)
 MASKED = 1.0e30
-MASKED_BY_VECTOR = 1
 
 GAIN0 = D
 GATE_BIAS0 = D + 16
@@ -109,12 +108,6 @@ def tile_multiheadedselfattention_pa_kernel(
             scalar1=1.0, scalar2=MASKED, op0=ALU.subtract, op1=ALU.mult,
         )
 
-        mask_bias_bc = const.tile([P, B, S], BF16)
-        for b in range(B):
-            bias_ps = psum_s.tile([P, S], F32, tag="s")
-            for t in range(NT):
-                nc.tensor.transpose(bias_ps[:, t * P : (t + 1) * P], mask_bias_t[:, b * NT + t, :], ident_f32[:])
-            nc.scalar.copy(out=mask_bias_bc[:, b, :], in_=bias_ps[:])
         mask_diag = const.tile([P, B * NT, P], BF16)
         nc.vector.tensor_tensor(
             out=mask_diag[:], in0=ident_bf[:].unsqueeze(1).to_broadcast([P, B * NT, P]),
@@ -133,12 +126,12 @@ def tile_multiheadedselfattention_pa_kernel(
         wv_codes = keep.tile([P, PASSES, D], U32, align_bytes=64)
         wv_scales = keep.tile([P, PASSES, D], U8, align_bytes=64)
         for g in range(PASSES):
-            grouped_v = stage.tile([P, S, 4], BF16, align_bytes=64, tag="e_bf")
+            grouped_v = stage.tile([P, S, 4], BF16, align_bytes=64)
             nc.vector.tensor_copy(
                 out=grouped_v[:].rearrange("p (c i) t -> p c t i", i=4),
                 in_=wv_raw[:, g, :, 0:S].rearrange("p t (c i) -> p c t i", i=4),
             )
-            grouped_s = stage.tile([P, S, 4], BF16, align_bytes=64, tag="e_grouped")
+            grouped_s = stage.tile([P, S, 4], BF16, align_bytes=64)
             nc.scalar.copy(
                 out=grouped_s[:].rearrange("p (c i) t -> p c t i", i=4),
                 in_=wv_raw[:, g, :, S:D].rearrange("p t (c i) -> p c t i", i=4),
@@ -304,37 +297,28 @@ def tile_multiheadedselfattention_pa_kernel(
         def scores_and_exp(n):
             b, hg, it = units[n]
             rows = slice(it * P, (it + 1) * P)
-            row_max = small.tile([P, HG], F32)
             exp_bias = small.tile([P, HG], F32)
-            e_bf[n] = stage.tile([P, HG, S], BF16, align_bytes=64, name="e_bf")
+            e_bf[n] = stage.tile([P, HG, S], BF16, name="e_bf")
             row_sum[n] = small.tile([P, HG], F32, name="row_sum", bufs=4)
             for hh in range(HG):
                 h = hg * HG + hh
                 s_bank = psum_s.tile([P, S], F32, tag="s")
-                if hh >= MASKED_BY_VECTOR:
-                    for t in range(NT):
-                        nc.tensor.matmul(
-                            out=s_bank[:, t * P : (t + 1) * P], lhsT=mask_bias_t[:, b * NT + t, :], rhs=ident_f32[:],
-                            is_transpose=True, start=(t == 0), stop=False,
-                        )
+                for t in range(NT):
                     nc.tensor.matmul(
-                        out=s_bank[:], lhsT=kqT[b][:, h, 1, rows], rhs=kqT[b][:, h, 0, :], start=False, stop=True
+                        out=s_bank[:, t * P : (t + 1) * P], lhsT=mask_bias_t[:, b * NT + t, :], rhs=ident_f32[:],
+                        is_transpose=True, start=(t == 0), stop=False,
                     )
-                    scores = s_bank
-                else:
-                    nc.tensor.matmul(
-                        out=s_bank[:], lhsT=kqT[b][:, h, 1, rows], rhs=kqT[b][:, h, 0, :], start=True, stop=True
-                    )
-                    scores = stage.tile([P, S], F32, name="masked_scores")
-                    nc.vector.tensor_tensor(out=scores[:], in0=s_bank[:], in1=mask_bias_bc[:, b, :], op=ALU.add)
-                nc.vector.tensor_reduce(out=row_max[:, hh : hh + 1], in_=scores[:], axis=AX.X, op=ALU.max)
-                nc.gpsimd.tensor_scalar(
-                    out=exp_bias[:, hh : hh + 1], in0=row_max[:, hh : hh + 1], scalar1=-SCALE, scalar2=0.0,
-                    op0=ALU.mult, op1=ALU.add,
+                nc.tensor.matmul(
+                    out=s_bank[:], lhsT=kqT[b][:, h, 1, rows], rhs=kqT[b][:, h, 0, :], start=False, stop=True
+                )
+                products = stage.tile([P, S], BF16, bufs=4)
+                nc.vector.tensor_scalar(
+                    out=products[:], in0=s_bank[:], scalar1=-SCALE, scalar2=None, op0=ALU.mult, op1=ALU.min,
+                    accum_out=exp_bias[:, hh : hh + 1],
                 )
                 nc.scalar.activation(
                     out=e_bf[n][:, hh, :],
-                    in_=scores[:],
+                    in_=s_bank[:],
                     func=ACT.Exp,
                     bias=exp_bias[:, hh : hh + 1],
                     scale=SCALE,

@@ -24,12 +24,16 @@ PASSES = D // (4 * P)
 HG = 4
 W = HG * P
 SCALE = 1.0 / math.sqrt(P)
-MASKED = 1.0e30
+WV_PART = D // 4
+LAG = 5
 
-GAIN0 = D
-GATE_BIAS0 = D + 16
-COUNT0 = D + 32
-ROW_W = D + 48
+MASK0 = 0
+BV0 = B * S
+GAIN0 = BV0 + D
+GATE_BIAS0 = GAIN0 + 16
+COUNT0 = GAIN0 + 32
+ROW_W = GAIN0 + 48
+SMALL_W = ROW_W - BV0
 
 FLOPS = 2 * B * S * D * D + 2 * 2 * B * H * S * S * P
 
@@ -48,148 +52,308 @@ def tile_multiheadedselfattention_pa_kernel(
         small = ctx.enter_context(tc.tile_pool(name="small", bufs=2))
         psum_s = ctx.enter_context(tc.psum_pool(name="psum_s", bufs=4))
         psum_b = ctx.enter_context(tc.psum_pool(name="psum_b", bufs=2))
-        psum_h = ctx.enter_context(tc.psum_pool(name="psum_h", bufs=1))
-        psum_c = ctx.enter_context(tc.psum_pool(name="psum_c", bufs=1))
+        psum_c = ctx.enter_context(tc.psum_pool(name="psum_c", bufs=2))
 
-        mask_rows = const.tile([P, P], BF16)
+        mask_rows = const.tile([P, 2 * P], BF16)
         nc.vector.memset(mask_rows[:], 0.0)
-        nc.sync.dma_start(
-            out=mask_rows[0 : B * NT, :], in_=value_key_masks.rearrange("b (t p) -> (b t) p", p=P)
-        )
+        nc.sync.dma_start(out=mask_rows[0 : B * 2, :], in_=value_key_masks.rearrange("b (u w) -> (b u) w", u=2))
         small_row = const.tile([P, ROW_W], BF16)
         nc.vector.memset(small_row[:], 0.0)
-        nc.sync.dma_start(out=small_row[0:1, 0:D], in_=bv.rearrange("(o n) -> o n", o=1))
         nc.sync.dma_start(
-            out=small_row[0:1, GAIN0 : GAIN0 + H], in_=overall_gain.rearrange("a h b c -> a (h b c)")
-        )
-        nc.sync.dma_start(
-            out=small_row[0:1, GATE_BIAS0 : GATE_BIAS0 + H], in_=overall_bias.rearrange("a h b c -> a (h b c)")
-        )
-        nc.sync.dma_start(
-            out=small_row[0:1, COUNT0 : COUNT0 + B], in_=value_key_counts.rearrange("(o n) -> o n", o=1)
+            out=small_row[0:1, MASK0 : MASK0 + B * S], in_=value_key_masks.rearrange("(o b) s -> o (b s)", o=1)
         )
 
-        wv_raw = raw.tile([P, PASSES, 4, D], BF16)
+        k_sb = {}
+        q_sb = {}
+        pq_sb = {}
+        pvk_sb = {}
+        out_view = [out[b].rearrange("(p t) c -> p t c", t=NT) for b in range(B)]
+
+        def load_k(b, hg):
+            cols = slice(hg * W, (hg + 1) * W)
+            nc.sync.dma_start(out=k_sb[b][:, :, cols], in_=k[b].rearrange("(t p) d -> p t d", p=P)[:, :, cols])
+
+        def load_q(b, hg):
+            cols = slice(hg * W, (hg + 1) * W)
+            nc.sync.dma_start(out=q_sb[b][:, :, cols], in_=q[b].rearrange("(p t) d -> p t d", t=NT)[:, :, cols])
+
+        def load_pvk(b):
+            nc.sync.dma_start(
+                out=pvk_sb[b].rearrange("p (u e) d -> p u (e d)", e=2),
+                in_=pre_value_key[b].rearrange("(u p e) d -> p u (e d)", u=2, e=2),
+            )
+
+        def load_pq(b):
+            pq_sb[b] = raw.tile([P, NT, DQ], BF16, name="pq_sb%d" % b)
+            nc.sync.dma_start(out=pq_sb[b][:], in_=pre_query[b].rearrange("(p t) c -> p t c", t=NT))
+
+        k_sb[0] = raw.tile([P, NT, D], BF16, name="k_sb0")
+        q_sb[0] = raw.tile([P, NT, D], BF16, name="q_sb0")
+        load_k(0, 0)
+        load_q(0, 0)
+        for first, width, vector in (
+            (BV0, D, bv.rearrange("(o n) -> o n", o=1)),
+            (GAIN0, H, overall_gain.rearrange("a h b c -> a (h b c)")),
+            (GATE_BIAS0, H, overall_bias.rearrange("a h b c -> a (h b c)")),
+            (COUNT0, B, value_key_counts.rearrange("(o n) -> o n", o=1)),
+        ):
+            nc.sync.dma_start(out=small_row[0:1, first : first + width], in_=vector)
+        load_k(0, 1)
+        load_q(0, 1)
+        wv_raw = raw.tile([P, PASSES, 4, D], BF16, name="wv_raw", tag="wide")
         for g in range(PASSES):
             nc.sync.dma_start(
                 out=wv_raw[:, g].rearrange("p (u e) n -> p u (e n)", e=2),
                 in_=Wv[g * 4 * P : (g + 1) * 4 * P, :].rearrange("(u p e) n -> p u (e n)", u=2, e=2),
             )
-        pvk_sb = [raw.tile([P, NT, D], BF16, name="pvk_sb%d" % b) for b in range(B)]
-        k_sb = [raw.tile([P, NT, D], BF16, name="k_sb%d" % b) for b in range(B)]
-        q_sb = [raw.tile([P, NT, D], BF16, name="q_sb%d" % b) for b in range(B)]
-        pq_sb = [raw.tile([P, NT, DQ], BF16, name="pq_sb%d" % b) for b in range(B)]
-        out_view = [out[b].rearrange("(p t) c -> p t c", t=NT) for b in range(B)]
-        for b in range(B):
-            nc.sync.dma_start(
-                out=pvk_sb[b][:].rearrange("p (u e) d -> p u (e d)", e=2),
-                in_=pre_value_key[b].rearrange("(u p e) d -> p u (e d)", u=2, e=2),
-            )
-        for b in range(B):
-            nc.sync.dma_start(out=k_sb[b][:], in_=k[b].rearrange("(t p) d -> p t d", p=P))
-            nc.sync.dma_start(out=q_sb[b][:], in_=q[b].rearrange("(p t) d -> p t d", t=NT))
-        for b in range(B):
-            nc.sync.dma_start(out=pq_sb[b][:], in_=pre_query[b].rearrange("(p t) c -> p t c", t=NT))
+        pvk_first = raw.tile([P, NT, D], BF16, name="pvk_first")
+        pvk_sb[0] = pvk_first[:]
+        load_pvk(0)
+        load_pq(0)
+
+        k_sb[1] = raw.tile([P, NT, D], BF16, name="k_sb1")
+        for hg in range(2):
+            load_k(1, hg)
+
+        def load_second_batch():
+            wide = raw.tile([P, PASSES, 4, D], BF16, name="wide", tag="wide")
+            pvk_sb[1] = wide[:, 0]
+            q_sb[1] = wide[:, 1]
+            load_q(1, 0)
+            load_pvk(1)
+            load_q(1, 1)
+            load_pq(1)
 
         ident_bf = const.tile([P, P], BF16)
         make_identity(nc, ident_bf[:])
         ident_f32 = const.tile([P, P], F32)
         make_identity(nc, ident_f32[:])
+        before = const.tile([P, P], BF16)
+        nc.gpsimd.memset(before[:], 1.0)
+        nc.gpsimd.affine_select(
+            out=before[:], in_=before[:], compare_op=ALU.is_gt, fill=0.0, base=0, pattern=[[1, P]],
+            channel_multiplier=-1,
+        )
         ones_bf = const.tile([P, P], BF16)
         nc.vector.memset(ones_bf[:], 1.0)
+        warm = const.tile([P, 1], F32)
+        nc.scalar.activation(out=warm[:], in_=ones_bf[:, 0:1], func=ACT.Exp)
 
-        mask_t_ps = psum_c.tile([P, P], BF16, tag="c")
-        nc.tensor.transpose(mask_t_ps[:], mask_rows[:], ident_bf[:])
-        mask_t = const.tile([P, B * NT], BF16)
-        nc.vector.tensor_copy(out=mask_t[:], in_=mask_t_ps[:, 0 : B * NT])
-        mask_bias_t = const.tile([P, B * NT, P], F32)
-        nc.vector.tensor_scalar(
-            out=mask_bias_t[:], in0=mask_t[:].unsqueeze(2).to_broadcast([P, B * NT, P]),
-            scalar1=1.0, scalar2=MASKED, op0=ALU.subtract, op1=ALU.mult,
+        mask_ps = psum_c.tile([P, 2, P], BF16, tag="c", name="mask_ps")
+        for f in range(2):
+            nc.tensor.transpose(mask_ps[:, f, :], mask_rows[:, f * P : (f + 1) * P], ident_bf[:])
+        pair_ps = psum_c.tile([P, P], F32, tag="c", name="pair_ps")
+        nc.tensor.transpose(pair_ps[:], mask_rows[:].bitcast(F32), ident_f32[:])
+        mask_t = const.tile([P, NT * B], BF16)
+        nc.vector.tensor_copy(
+            out=mask_t[:].rearrange("p (u f b) -> p u f b", u=2, f=2),
+            in_=mask_ps[:, :, 0 : B * 2].rearrange("p f (b u) -> p u f b", u=2),
         )
+        mask_pair = const.tile([P, B * NT], BF16)
+        nc.vector.tensor_copy(out=mask_pair[:].bitcast(F32), in_=pair_ps[:, 0 : B * 2])
 
-        mask_diag = const.tile([P, B * NT, P], BF16)
-        nc.vector.tensor_tensor(
-            out=mask_diag[:], in0=ident_bf[:].unsqueeze(1).to_broadcast([P, B * NT, P]),
-            in1=mask_t[:].unsqueeze(2).to_broadcast([P, B * NT, P]), op=ALU.mult,
-        )
-
-        small_bc = const.tile([P, ROW_W], F32)
-        for first in range(0, ROW_W, S):
-            width = min(S, ROW_W - first)
-            bc_ps = psum_s.tile([P, S], F32, tag="s")
+        kept_ps = psum_b.tile([P, S], F32, tag="b", name="kept_ps")
+        nc.tensor.matmul(out=kept_ps[:, 0 : NT * B], lhsT=before[:], rhs=mask_t[:], start=True, stop=False)
+        for t in range(1, NT):
             nc.tensor.matmul(
-                out=bc_ps[:, 0:width], lhsT=ones_bf[:], rhs=small_row[:, first : first + width], start=True, stop=True
+                out=kept_ps[:, t * B : NT * B], lhsT=ones_bf[:], rhs=mask_t[:, 0 : (NT - t) * B], start=False,
+                stop=(t == NT - 1),
             )
-            nc.scalar.copy(out=small_bc[:, first : first + width], in_=bc_ps[:, 0:width])
+        for t in range(NT):
+            nc.tensor.matmul(
+                out=kept_ps[:, NT * B : NT * B + B], lhsT=ones_bf[:], rhs=mask_t[:, t * B : (t + 1) * B],
+                start=(t == 0), stop=(t == NT - 1),
+            )
+        select = const.tile([P, NT * B, 2], BF16)
+        nc.vector.tensor_copy(out=select[:, :, 0], in_=mask_t[:])
+        nc.vector.scalar_tensor_tensor(
+            out=select[:, :, 1], in0=kept_ps[:, 0 : NT * B], scalar=0.0, in1=mask_t[:], op0=ALU.is_equal, op1=ALU.mult
+        )
+        minus_masked = const.tile([P, B], F32)
+        nc.vector.tensor_scalar(
+            out=minus_masked[:], in0=kept_ps[:, NT * B : NT * B + B], scalar1=float(S), scalar2=None, op0=ALU.subtract
+        )
+
+        mask_diag = const.tile([P, NT * B, P], BF16)
+        nc.vector.tensor_tensor(
+            out=mask_diag[:], in0=ident_bf[:].unsqueeze(1).to_broadcast([P, NT * B, P]),
+            in1=mask_t[:].unsqueeze(2).to_broadcast([P, NT * B, P]), op=ALU.mult,
+        )
+        pair_diag = const.tile([P, B * NT, P], F32)
+        nc.gpsimd.tensor_tensor(
+            out=pair_diag[:], in0=ident_f32[:].unsqueeze(1).to_broadcast([P, B * NT, P]),
+            in1=mask_pair[:].unsqueeze(2).to_broadcast([P, B * NT, P]), op=ALU.mult,
+        )
+
+        not_mask = const.tile([P, B, S], BF16)
+        for b in range(B):
+            bc_ps = psum_s.tile([P, S], F32, tag="s", name="bc_ps")
+            nc.tensor.matmul(
+                out=bc_ps[:], lhsT=ones_bf[:], rhs=small_row[:, MASK0 + b * S : MASK0 + (b + 1) * S], start=True, stop=True
+            )
+            nc.scalar.activation(out=not_mask[:, b, :], in_=bc_ps[:], func=ACT.Copy, scale=-1.0, bias=1.0)
+
+        ks_bank = {}
+        ks = {}
+        ksum_terms = {}
+
+        def key_sums(b, hg, hh):
+            h = hg * HG + hh
+            if hh == 0:
+                ks_bank[b, hg] = psum_c.tile([P, HG, 2], F32, tag="c", name="ks_bank")
+            for t in range(NT):
+                nc.tensor.matmul(
+                    out=ks_bank[b, hg][:, hh, :], lhsT=k_sb[b][:, t, h * P : (h + 1) * P], rhs=select[:, t * B + b, :],
+                    start=(t == 0), stop=(t == NT - 1),
+                )
+
+        def key_sums_copy(b, hg):
+            ks[b, hg] = small.tile([P, HG, 2], F32, name="ks")
+            nc.vector.tensor_copy(out=ks[b, hg][:], in_=ks_bank[b, hg][:])
+
+        def key_terms(b, hg):
+            terms = small.tile([P, HG, 3], BF16, name="ksum_terms")
+            nc.gpsimd.tensor_copy(out=terms[:, :, 0], in_=ks[b, hg][:, :, 0])
+            nc.gpsimd.tensor_tensor(
+                out=terms[:, :, 1], in0=ks[b, hg][:, :, 0], in1=terms[:, :, 0], op=ALU.subtract
+            )
+            nc.gpsimd.tensor_copy(out=terms[:, :, 2], in_=ks[b, hg][:, :, 1])
+            ksum_terms[b, hg] = terms
+
+        kT = [keep.tile([P, H, S], BF16, name="kT%d" % b) for b in range(B)]
+        qT = [keep.tile([P, H, S], BF16, name="qT%d" % b) for b in range(B)]
+
+        k_bank = {}
+        q_bank = {}
+
+        def transpose_keys(b, h):
+            k_bank[b, h] = psum_c.tile([P, NT, P], BF16, tag="c", name="k_bank")
+            for t in range(NT):
+                nc.tensor.transpose(
+                    k_bank[b, h][:, t, :], k_sb[b][:, t, h * P : (h + 1) * P], mask_diag[:, t * B + b, :]
+                )
+
+        def fill_keys(b, h):
+            nc.vector.scalar_tensor_tensor(
+                out=kT[b][:, h, :], in0=not_mask[:, b, :], scalar=ks[b, h // HG][:, h % HG, 1:2],
+                in1=k_bank[b, h][:].rearrange("p t r -> p (t r)"), op0=ALU.mult, op1=ALU.add,
+            )
+
+        def transpose_queries(b, h):
+            q_bank[b, h] = psum_c.tile([P, 2, NT, P], BF16, tag="c", name="q_bank")
+            for h2 in range(2):
+                cols = slice((h + h2) * P, (h + h2 + 1) * P)
+                for t in range(NT):
+                    nc.tensor.transpose(q_bank[b, h][:, h2, t, :], q_sb[b][:, t, cols], ident_bf[:])
+
+        def copy_queries(b, h):
+            nc.scalar.copy(out=qT[b][:, h : h + 2, :], in_=q_bank[b, h][:].rearrange("p h t r -> p h (t r)"))
+
+        small_bc = const.tile([P, SMALL_W], F32)
+        small_bank = {}
+
+        def small_spread(first):
+            width = min(S, SMALL_W - first)
+            small_bank[first] = psum_c.tile([P, S], F32, tag="c", name="small_bank")
+            nc.tensor.matmul(
+                out=small_bank[first][:, 0:width], lhsT=ones_bf[:], rhs=small_row[:, BV0 + first : BV0 + first + width],
+                start=True, stop=True,
+            )
+
+        def small_copy(first):
+            width = min(S, SMALL_W - first)
+            nc.scalar.copy(out=small_bc[:, first : first + width], in_=small_bank[first][:, 0:width])
+
+        gain_bc = small_bc[:, GAIN0 - BV0 : GAIN0 - BV0 + H]
+        gate_bias_bc = small_bc[:, GATE_BIAS0 - BV0 : GATE_BIAS0 - BV0 + H]
+        count_bc = small_bc[:, COUNT0 - BV0 : COUNT0 - BV0 + B]
+        inv_count = const.tile([P, B], F32)
+        gate_scale = const.tile([P, B, H], F32)
+
+        def gate_scales():
+            nc.vector.reciprocal(out=inv_count[:], in_=count_bc)
+            for b in range(B):
+                nc.gpsimd.tensor_scalar(
+                    out=gate_scale[:, b, :], in0=gain_bc, scalar1=inv_count[:, b : b + 1], scalar2=SCALE, op0=ALU.mult,
+                    op1=ALU.mult,
+                )
 
         wv_codes = keep.tile([P, PASSES, D], U32, align_bytes=64)
         wv_scales = keep.tile([P, PASSES, D], U8, align_bytes=64)
-        for g in range(PASSES):
-            grouped_v = stage.tile([P, S, 4], BF16, align_bytes=64)
-            nc.vector.tensor_copy(
-                out=grouped_v[:].rearrange("p (c i) t -> p c t i", i=4),
-                in_=wv_raw[:, g, :, 0:S].rearrange("p t (c i) -> p c t i", i=4),
-            )
-            grouped_s = stage.tile([P, S, 4], BF16, align_bytes=64)
-            nc.scalar.copy(
-                out=grouped_s[:].rearrange("p (c i) t -> p c t i", i=4),
-                in_=wv_raw[:, g, :, S:D].rearrange("p t (c i) -> p c t i", i=4),
-            )
-            for half, grouped in enumerate((grouped_v, grouped_s)):
-                cols = slice(half * S, (half + 1) * S)
-                nc.vector.quantize_mx(
-                    out=wv_codes[:, g, cols].bitcast(FP8X4),
-                    scales=wv_scales[:, g, cols],
-                    in_=grouped[:].rearrange("p c t -> p (c t)"),
-                )
+        wv_grouped = {}
 
-        inv_count = const.tile([P, B], F32)
-        nc.vector.reciprocal(out=inv_count[:], in_=small_bc[:, COUNT0 : COUNT0 + B])
-        gate_scale = const.tile([P, B, H], F32)
-        for b in range(B):
-            nc.vector.tensor_scalar(
-                out=gate_scale[:, b, :], in0=small_bc[:, GAIN0 : GAIN0 + H], scalar1=inv_count[:, b : b + 1],
-                scalar2=SCALE, op0=ALU.mult, op1=ALU.mult,
+        def weights_regroup(g, part):
+            cols = slice(part * WV_PART, (part + 1) * WV_PART)
+            grouped = stage.tile([P, WV_PART, 4], BF16, align_bytes=64, name="wv_grouped", bufs=4)
+            out_cols = grouped[:].rearrange("p (c i) t -> p c t i", i=4)
+            in_cols = wv_raw[:, g, :, cols].rearrange("p t (c i) -> p c t i", i=4)
+            if part % 2 == 0:
+                nc.vector.tensor_copy(out=out_cols, in_=in_cols)
+            else:
+                nc.scalar.copy(out=out_cols, in_=in_cols)
+            wv_grouped[g, part] = grouped
+
+        def weights_quantise(g, part):
+            cols = slice(part * WV_PART, (part + 1) * WV_PART)
+            nc.vector.quantize_mx(
+                out=wv_codes[:, g, cols].bitcast(FP8X4),
+                scales=wv_scales[:, g, cols],
+                in_=wv_grouped[g, part][:].rearrange("p c t -> p (c t)"),
             )
 
         pvk_codes = keep.tile([P, PASSES, B * S], U32, align_bytes=64)
         pvk_scales = keep.tile([P, PASSES, B * S], U8, align_bytes=64)
         v_codes = keep.tile([P, B, D], U32, align_bytes=64)
         v_scales = keep.tile([P, B, D], U8, align_bytes=64)
-        kqT = [keep.tile([P, H, 2, S], BF16, name="kqT%d" % b) for b in range(B)]
+        pvk_grouped = {}
+        bias_kept = {}
 
-        def prepare_tokens(b):
-            pvk_words = pvk_sb[b][:].bitcast(F32)
-            pvk_grouped = stage.tile([P, PASSES, S, 4], BF16, align_bytes=64)
-            pvk_grouped_words = pvk_grouped[:].bitcast(F32)
+        def spread_bias(b):
+            bias_kept[b] = stage.tile([P, NT, D], BF16, name="bias_kept")
             for t in range(NT):
-                w_bank = psum_b.tile([P, PASSES, 2, P], F32, tag="b")
-                for g in range(PASSES):
-                    for u in range(2):
-                        first = (2 * g + u) * P
-                        nc.tensor.transpose(w_bank[:, g, u, :], pvk_words[:, t, first : first + P], ident_f32[:])
-                nc.scalar.copy(
-                    out=pvk_grouped_words[:, :, t * P : (t + 1) * P, :],
-                    in_=w_bank[:].rearrange("p g u r -> p g r u"),
-                )
-            for g in range(PASSES):
-                nc.vector.quantize_mx(
-                    out=pvk_codes[:, g, b * S : (b + 1) * S].bitcast(FP8X4),
-                    scales=pvk_scales[:, g, b * S : (b + 1) * S],
-                    in_=pvk_grouped[:, g].rearrange("p r t -> p (r t)"),
+                nc.gpsimd.tensor_scalar(
+                    out=bias_kept[b][:, t, :], in0=small_bc[:, 0:D], scalar1=mask_pair[:, b * NT + t : b * NT + t + 1],
+                    scalar2=0.0, op0=ALU.mult, op1=ALU.add,
                 )
 
+        w_bank = {}
+
+        def tokens_transpose(b, t):
+            pvk_words = pvk_sb[b].bitcast(F32)
+            w_bank[b, t] = psum_c.tile([P, PASSES, 2, P], F32, tag="c", name="w_bank")
+            for g in range(PASSES):
+                for u in range(2):
+                    first = (2 * g + u) * P
+                    nc.tensor.transpose(
+                        w_bank[b, t][:, g, u, :], pvk_words[:, t, first : first + P], pair_diag[:, b * NT + t, :]
+                    )
+
+        def tokens_group(b, t):
+            if t == 0:
+                pvk_grouped[b] = stage.tile([P, PASSES, S, 4], BF16, align_bytes=64, name="pvk_grouped", bufs=1)
+            nc.scalar.copy(
+                out=pvk_grouped[b][:].bitcast(F32)[:, :, t * P : (t + 1) * P, :],
+                in_=w_bank[b, t][:].rearrange("p g u r -> p g r u"),
+            )
+
+        def tokens_quantise(b, g):
+                nc.vector.quantize_mx(
+             out=pvk_codes[:, g, b * S : (b + 1) * S].bitcast(FP8X4),
+             scales=pvk_scales[:, g, b * S : (b + 1) * S],
+             in_=pvk_grouped[b][:, g].rearrange("p r t -> p (r t)"),
+                )
+
+        v_bank = {}
         v_grouped = {}
 
-        def values_matmul(b, h, banks, tag):
+        def values_matmul(b, h):
             cols = slice(h * P, (h + 1) * P)
-            v_bank = banks.tile([P, NT, P], F32, tag=tag)
+            v_bank[b, h] = psum_c.tile([P, NT, P], F32, tag="c", name="v_bank")
             for t in range(NT):
                 toks = slice(b * S + t * P, b * S + (t + 1) * P)
                 for g in range(PASSES):
                     nc.tensor.matmul_mx(
-                        out=v_bank[:, t, :],
+                        out=v_bank[b, h][:, t, :],
                         lhsT=pvk_codes[:, g, toks].bitcast(FP8X4),
                         lhsT_scale=pvk_scales[:, g, toks],
                         rhs=wv_codes[:, g, cols].bitcast(FP8X4),
@@ -197,11 +361,14 @@ def tile_multiheadedselfattention_pa_kernel(
                         start=(g == 0),
                         stop=(g == PASSES - 1),
                     )
-            v_grouped[b, h] = stage.tile([P, P, NT], BF16, align_bytes=64, name="v_grouped")
+
+        def values_add(b, h):
+            cols = slice(h * P, (h + 1) * P)
+            v_grouped[b, h] = stage.tile([P, P, NT], BF16, align_bytes=64, name="v_grouped", bufs=3)
             nc.vector.tensor_tensor(
                 out=v_grouped[b, h][:],
-                in0=v_bank[:].rearrange("p t c -> p c t"),
-                in1=small_bc[:, cols].unsqueeze(2).to_broadcast([P, P, NT]),
+                in0=v_bank[b, h][:].rearrange("p t c -> p c t"),
+                in1=bias_kept[b][:, :, cols].rearrange("p t c -> p c t"),
                 op=ALU.add,
             )
 
@@ -213,48 +380,33 @@ def tile_multiheadedselfattention_pa_kernel(
                 in_=v_grouped[b, h][:].rearrange("p c t -> p (c t)"),
             )
 
-        ksum = [keep.tile([P, H], F32, name="ksum%d" % b) for b in range(B)]
-
-        def prepare_scores(b, h, banks, tag):
-            cols = slice(h * P, (h + 1) * P)
-            t_bank = banks.tile([P, 2, NT, P], BF16, tag=tag)
-            for t in range(NT):
-                nc.tensor.transpose(t_bank[:, 0, t, :], k_sb[b][:, t, cols], mask_diag[:, b * NT + t, :])
-            for t in range(NT):
-                nc.tensor.transpose(t_bank[:, 1, t, :], q_sb[b][:, t, cols], ident_bf[:])
-            nc.scalar.activation(
-                out=kqT[b][:, h, 0, :], in_=t_bank[:, 0].rearrange("p t r -> p (t r)"), func=ACT.Copy,
-                accum_out=ksum[b][:, h : h + 1],
-            )
-            nc.scalar.copy(out=kqT[b][:, h, 1, :], in_=t_bank[:, 1].rearrange("p t r -> p (t r)"))
-
-        ksum_terms = {}
         gate = {}
         one_minus_gate = {}
+        copy_score = {}
+        pooled_bank = {}
+        shifted_score = {}
 
-        def gate_keys(b, hg):
-            heads = slice(hg * HG, (hg + 1) * HG)
-            ksum_terms[b, hg] = small.tile([P, HG, 2], BF16, name="ksum_terms")
-            nc.gpsimd.tensor_copy(out=ksum_terms[b, hg][:, :, 0], in_=ksum[b][:, heads])
-            nc.gpsimd.tensor_tensor(
-                out=ksum_terms[b, hg][:, :, 1], in0=ksum[b][:, heads], in1=ksum_terms[b, hg][:, :, 0],
-                op=ALU.subtract,
-            )
-
-        def gate_queries(b, hg):
-            heads = slice(hg * HG, (hg + 1) * HG)
-            pooled_ps = psum_b.tile([P, NT, HG, 2], F32, tag="b")
+        def pool_scores(b, hg):
+            pooled_bank[b, hg] = psum_c.tile([P, NT, HG, 3], F32, tag="c", name="pooled_bank")
             for it in range(NT):
                 for hh in range(HG):
                     nc.tensor.matmul(
-                        out=pooled_ps[:, it, hh, :],
-                        lhsT=kqT[b][:, hg * HG + hh, 1, it * P : (it + 1) * P],
+                        out=pooled_bank[b, hg][:, it, hh, :],
+                        lhsT=qT[b][:, hg * HG + hh, it * P : (it + 1) * P],
                         rhs=ksum_terms[b, hg][:, hh, :],
                         start=True,
                         stop=True,
                     )
+
+        def gates(b, hg):
+            heads = slice(hg * HG, (hg + 1) * HG)
+            pooled_ps = pooled_bank[b, hg]
             pooled = small.tile([P, NT, HG], F32)
-            nc.vector.tensor_reduce(out=pooled[:], in_=pooled_ps[:], axis=AX.X, op=ALU.add)
+            nc.vector.tensor_reduce(out=pooled[:], in_=pooled_ps[:, :, :, 0:2], axis=AX.X, op=ALU.add)
+            copy_score[b, hg] = small.tile([P, NT, HG], F32, name="copy_score")
+            nc.vector.tensor_scalar(
+                out=copy_score[b, hg][:], in0=pooled_ps[:, :, :, 2], scalar1=SCALE, scalar2=None, op0=ALU.mult
+            )
             scaled = small.tile([P, NT, HG], F32)
             nc.gpsimd.tensor_tensor(
                 out=scaled[:], in0=pooled[:], in1=gate_scale[:, b, heads].unsqueeze(1).to_broadcast([P, NT, HG]),
@@ -262,12 +414,14 @@ def tile_multiheadedselfattention_pa_kernel(
             )
             shifted = small.tile([P, NT, HG], F32)
             nc.gpsimd.tensor_tensor(
-                out=shifted[:], in0=scaled[:],
-                in1=small_bc[:, GATE_BIAS0 : GATE_BIAS0 + H][:, heads].unsqueeze(1).to_broadcast([P, NT, HG]),
+                out=shifted[:], in0=scaled[:], in1=gate_bias_bc[:, heads].unsqueeze(1).to_broadcast([P, NT, HG]),
                 op=ALU.add,
             )
+            shifted_score[b, hg] = shifted
+
+        def sigmoids(b, hg):
             tanh_half = small.tile([P, NT, HG], F32)
-            nc.scalar.activation(out=tanh_half[:], in_=shifted[:], func=ACT.Tanh, scale=0.5)
+            nc.scalar.activation(out=tanh_half[:], in_=shifted_score[b, hg][:], func=ACT.Tanh, scale=0.5)
             gate[b, hg] = keep.tile([P, NT, HG], F32, name="gate%d%d" % (b, hg))
             nc.gpsimd.tensor_scalar(
                 out=gate[b, hg][:], in0=tanh_half[:], scalar1=0.5, scalar2=0.5, op0=ALU.mult, op1=ALU.add
@@ -278,15 +432,20 @@ def tile_multiheadedselfattention_pa_kernel(
             )
 
         def copy_tail(b):
-            tail = stage.tile([P, NT, DQ - D], F32, bufs=1)
+            tail = stage.tile([P, NT, DQ - D], F32, bufs=1, name="tail")
             nc.gpsimd.tensor_scalar(
                 out=tail[:], in0=pq_sb[b][:, :, D:DQ], scalar1=1.0, scalar2=0.0, op0=ALU.mult, op1=ALU.add
             )
             nc.sync.dma_start(out=out_view[b][:, :, D:DQ], in_=tail[:])
 
         units = [(b, hg, it) for b in range(B) for hg in range(H // HG) for it in range(NT)]
+        exp_bias = {}
         e_bf = {}
         row_sum = {}
+        copy_arg = {}
+        copy_e = {}
+        kept_sum = {}
+        inv_sum = {}
         e_grouped = {}
         e_codes = {}
         e_scales = {}
@@ -294,60 +453,88 @@ def tile_multiheadedselfattention_pa_kernel(
         h_bank = {}
         result = {}
 
-        def scores_and_exp(n):
-            b, hg, it = units[n]
-            rows = slice(it * P, (it + 1) * P)
-            exp_bias = small.tile([P, HG], F32)
-            e_bf[n] = stage.tile([P, HG, S], BF16, name="e_bf")
-            row_sum[n] = small.tile([P, HG], F32, name="row_sum", bufs=4)
-            for hh in range(HG):
-                h = hg * HG + hh
-                s_bank = psum_s.tile([P, S], F32, tag="s")
-                for t in range(NT):
-                    nc.tensor.matmul(
-                        out=s_bank[:, t * P : (t + 1) * P], lhsT=mask_bias_t[:, b * NT + t, :], rhs=ident_f32[:],
-                        is_transpose=True, start=(t == 0), stop=False,
-                    )
-                nc.tensor.matmul(
-                    out=s_bank[:], lhsT=kqT[b][:, h, 1, rows], rhs=kqT[b][:, h, 0, :], start=False, stop=True
-                )
-                products = stage.tile([P, S], BF16, bufs=4)
-                nc.vector.tensor_scalar(
-                    out=products[:], in0=s_bank[:], scalar1=-SCALE, scalar2=None, op0=ALU.mult, op1=ALU.min,
-                    accum_out=exp_bias[:, hh : hh + 1],
-                )
-                nc.scalar.activation(
-                    out=e_bf[n][:, hh, :],
-                    in_=s_bank[:],
-                    func=ACT.Exp,
-                    bias=exp_bias[:, hh : hh + 1],
-                    scale=SCALE,
-                    accum_out=row_sum[n][:, hh : hh + 1],
-                )
+        s_bank = {}
 
-        def transpose_e(n):
+        def scores(i):
+            n, hh = divmod(i, HG)
+            b, hg, it = units[n]
+            h = hg * HG + hh
+            s_bank[i] = psum_s.tile([P, S], F32, tag="s", name="s_bank")
+            nc.tensor.matmul(
+                out=s_bank[i][:], lhsT=qT[b][:, h, it * P : (it + 1) * P], rhs=kT[b][:, h, :], start=True, stop=True
+            )
+
+        def maximum_and_exp(i):
+            n, hh = divmod(i, HG)
+            if hh == 0:
+                exp_bias[n] = small.tile([P, HG], F32, name="exp_bias", bufs=3)
+                e_bf[n] = stage.tile([P, HG, S], BF16, name="e_bf", bufs=3)
+                row_sum[n] = small.tile([P, HG], F32, name="row_sum", bufs=4)
+            products = stage.tile([P, S], BF16, bufs=1, name="products")
+            nc.vector.tensor_scalar(
+                out=products[:], in0=s_bank[i][:], scalar1=-SCALE, scalar2=None, op0=ALU.mult, op1=ALU.min,
+                accum_out=exp_bias[n][:, hh : hh + 1],
+            )
+            nc.scalar.activation(
+                out=e_bf[n][:, hh, :],
+                in_=s_bank[i][:],
+                func=ACT.Exp,
+                bias=exp_bias[n][:, hh : hh + 1],
+                scale=SCALE,
+                accum_out=row_sum[n][:, hh : hh + 1],
+            )
+
+        def copies_argument(n):
+            b, hg, it = units[n]
+            copy_arg[n] = small.tile([P, HG], F32, name="copy_arg")
+            nc.gpsimd.tensor_tensor(
+                out=copy_arg[n][:], in0=copy_score[b, hg][:, it, :], in1=exp_bias[n][:], op=ALU.add
+            )
+
+        def copies_exp(n):
+            copy_e[n] = small.tile([P, HG], F32, name="copy_e")
+            nc.scalar.activation(out=copy_e[n][:], in_=copy_arg[n][:], func=ACT.Exp)
+
+        e_bank = {}
+
+        def transpose_e(n, pair):
             e_words = e_bf[n][:].bitcast(F32)
-            e_grouped[n] = stage.tile([P, HG, P, 4], BF16, align_bytes=64, name="e_grouped")
-            e_grouped_words = e_grouped[n][:].bitcast(F32)
-            for pair in range(HG // 2):
-                e_bank = psum_b.tile([P, 2, 2, P], F32, tag="b")
-                for h2 in range(2):
-                    for u in range(2):
-                        nc.tensor.transpose(
-                            e_bank[:, h2, u, :], e_words[:, 2 * pair + h2, u * P : (u + 1) * P], ident_f32[:]
-                        )
-                nc.scalar.copy(
-                    out=e_grouped_words[:, 2 * pair : 2 * pair + 2, :, :],
-                    in_=e_bank[:].rearrange("p h u i -> p h i u"),
-                )
+            e_bank[n, pair] = psum_b.tile([P, 2, 2, P], F32, tag="b", name="e_bank")
+            for h2 in range(2):
+                for u in range(2):
+                    nc.tensor.transpose(
+                        e_bank[n, pair][:, h2, u, :], e_words[:, 2 * pair + h2, u * P : (u + 1) * P], ident_f32[:]
+                    )
+
+        def group_e(n, pair):
+            if pair == 0:
+                e_grouped[n] = stage.tile([P, HG, P, 4], BF16, align_bytes=64, name="e_grouped", bufs=2)
+            nc.scalar.copy(
+                out=e_grouped[n][:].bitcast(F32)[:, 2 * pair : 2 * pair + 2, :, :],
+                in_=e_bank[n, pair][:].rearrange("p h u i -> p h i u"),
+            )
+
+        def kept_sums(n):
+            b, hg, it = units[n]
+            part = small.tile([P, HG], F32, name="part")
+            nc.gpsimd.tensor_scalar(
+                out=part[:], in0=copy_e[n][:], scalar1=minus_masked[:, b : b + 1], scalar2=0.0, op0=ALU.mult, op1=ALU.add
+            )
+            kept_sum[n] = small.tile([P, HG], F32, name="kept_sum")
+            nc.gpsimd.tensor_tensor(out=kept_sum[n][:], in0=row_sum[n][:], in1=part[:], op=ALU.add)
+
+        def invert_sums(n):
+            inv_sum[n] = small.tile([P, HG], F32, name="inv_sum")
+            nc.vector.reciprocal(out=inv_sum[n][:], in_=kept_sum[n][:])
 
         def blend_weights(n):
             b, hg, it = units[n]
-            inv_sum = small.tile([P, HG], F32)
-            nc.vector.reciprocal(out=inv_sum[:], in_=row_sum[n][:])
-            weight[n] = small.tile([P, HG], F32, name="weight", bufs=3)
-            nc.gpsimd.tensor_tensor(out=weight[n][:], in0=inv_sum[:], in1=gate[b, hg][:, it, :], op=ALU.mult)
-            result[n] = stage.tile([P, W], F32, name="result", bufs=3)
+            weight[n] = small.tile([P, HG], F32, name="weight", bufs=LAG)
+            nc.gpsimd.tensor_tensor(out=weight[n][:], in0=inv_sum[n][:], in1=gate[b, hg][:, it, :], op=ALU.mult)
+
+        def blend_rest(n):
+            b, hg, it = units[n]
+            result[n] = stage.tile([P, W], F32, name="result", bufs=LAG)
             for hh in range(HG):
                 h = hg * HG + hh
                 nc.gpsimd.tensor_scalar(
@@ -360,8 +547,8 @@ def tile_multiheadedselfattention_pa_kernel(
                 )
 
         def quantise_e(n):
-            e_codes[n] = stage.tile([P, W], U32, align_bytes=64, name="e_codes")
-            e_scales[n] = stage.tile([P, W], U8, align_bytes=64, name="e_scales")
+            e_codes[n] = stage.tile([P, W], U32, align_bytes=64, name="e_codes", bufs=LAG)
+            e_scales[n] = stage.tile([P, W], U8, align_bytes=64, name="e_scales", bufs=LAG)
             nc.vector.quantize_mx(
                 out=e_codes[n][:].bitcast(FP8X4),
                 scales=e_scales[n][:],
@@ -370,7 +557,7 @@ def tile_multiheadedselfattention_pa_kernel(
 
         def e_times_v(n):
             b, hg, it = units[n]
-            h_bank[n] = psum_h.tile([P, HG, P], F32, tag="h", name="h_bank")
+            h_bank[n] = psum_c.tile([P, HG, P], F32, tag="c", name="h_bank")
             for hh in range(HG):
                 h = hg * HG + hh
                 nc.tensor.matmul_mx(
@@ -397,42 +584,101 @@ def tile_multiheadedselfattention_pa_kernel(
                 )
             nc.sync.dma_start(out=out_view[b][:, it, hg * W : (hg + 1) * W], in_=result[n][:])
 
+        def blend_by_scalar(n):
+            b, hg, it = units[n]
+            product = stage.tile([P, W], F32, name="product")
+            for hh in range(HG):
+                nc.scalar.activation(
+                    out=product[:, hh * P : (hh + 1) * P], in_=h_bank[n][:, hh, :], func=ACT.Copy,
+                    scale=weight[n][:, hh : hh + 1],
+                )
+            nc.gpsimd.tensor_tensor(out=result[n][:], in0=product[:], in1=result[n][:], op=ALU.add)
+            nc.sync.dma_start(out=out_view[b][:, it, hg * W : (hg + 1) * W], in_=result[n][:])
+
         heads = [(b, h) for b in range(B) for h in range(H)]
         groups = [(b, hg) for b in range(B) for hg in range(H // HG)]
-        for b in range(B):
-            prepare_tokens(b)
-        for n in range(HG):
-            values_matmul(heads[n][0], heads[n][1], psum_s, "s")
-            if n > 0:
-                values_quantise(heads[n - 1][0], heads[n - 1][1])
-        values_quantise(heads[HG - 1][0], heads[HG - 1][1])
-        for n in range(HG):
-            prepare_scores(heads[n][0], heads[n][1], psum_s, "s")
-        gate_keys(0, 0)
         last = len(units) - 1
-        for step in range(len(units) + 3):
-            coming = heads[step + HG] if step + HG < len(heads) else None
-            if step <= last:
-                scores_and_exp(step)
-            if step <= last and step % NT == 0:
-                gate_queries(groups[step // NT][0], groups[step // NT][1])
-            if 2 <= step <= last + 2:
-                blend_weights(step - 2)
-            if coming is not None:
-                values_matmul(coming[0], coming[1], psum_c, "c")
-            if 3 <= step:
-                e_times_v(step - 3)
-            if 1 <= step <= last + 1:
-                transpose_e(step - 1)
-            if coming is not None:
-                prepare_scores(coming[0], coming[1], psum_c, "c")
-            if 2 <= step <= last + 2:
-                quantise_e(step - 2)
-            if coming is not None:
-                values_quantise(coming[0], coming[1])
-            if 3 <= step:
-                blend(step - 3)
-            if coming is not None and step % NT == NT - 1:
-                gate_keys(groups[step // NT + 1][0], groups[step // NT + 1][1])
-            if step <= last and units[step][1:] == (0, NT - 1):
-                copy_tail(units[step][0])
+        plan = {}
+        for hh in range(HG):
+            key_sums(0, 0, hh)
+        transpose_keys(0, 0)
+        key_sums_copy(0, 0)
+        key_terms(0, 0)
+        fill_keys(0, 0)
+        transpose_queries(0, 0)
+        copy_queries(0, 0)
+        transpose_keys(0, 1)
+        fill_keys(0, 1)
+
+        def at(n, hh, tensor, rest):
+            plan.setdefault(n * HG + hh, []).append((tensor, rest))
+
+        def nothing():
+            pass
+
+        for n in range(len(units)):
+            at(n, 3, lambda n=n: transpose_e(n, 0), lambda n=n: group_e(n, 0))
+            at(n + 1, 1, lambda n=n: transpose_e(n, 1), lambda n=n: group_e(n, 1))
+            at(n + 1, 0, nothing, lambda n=n: copies_argument(n))
+            at(n + 1, 2, nothing, lambda n=n: copies_exp(n))
+            at(n + 1, 3, nothing, lambda n=n: (quantise_e(n), kept_sums(n), blend_rest(n)))
+            at(n + 2, 1, nothing, lambda n=n: (invert_sums(n), blend_weights(n)))
+        at(0, 0, lambda: transpose_queries(0, 2), lambda: copy_queries(0, 2))
+        at(0, 0, lambda: transpose_keys(0, 2), lambda: fill_keys(0, 2))
+        at(0, 1, lambda: transpose_keys(0, 3), lambda: fill_keys(0, 3))
+        for i, first in enumerate((D, 0, S)):
+            at(0, i, lambda first=first: small_spread(first), lambda first=first: small_copy(first))
+        at(0, 2, nothing, gate_scales)
+        for c in range(HG, len(heads)):
+            b, h = heads[c]
+            if h % 2 == 0:
+                at(c - HG, 0, lambda b=b, h=h: transpose_queries(b, h), lambda b=b, h=h: copy_queries(b, h))
+            at(c - HG, 3 if c == HG else 1, lambda b=b, h=h: transpose_keys(b, h), lambda b=b, h=h: fill_keys(b, h))
+        for g, (b, hg) in enumerate(groups):
+            slot = g * NT * HG - 2 if g > 0 else HG - 1
+            at(slot // HG, slot % HG, lambda b=b, hg=hg: pool_scores(b, hg), lambda b=b, hg=hg: gates(b, hg))
+            at((slot + 2) // HG, (slot + 2) % HG, nothing, lambda b=b, hg=hg: sigmoids(b, hg))
+            if g >= 1:
+                slot = (g - 1) * NT * HG - 2 if g > 1 else 2
+                at(slot // HG, slot % HG, lambda b=b, hg=hg: [key_sums(b, hg, hh) for hh in range(HG)],
+                   lambda b=b, hg=hg: (key_sums_copy(b, hg), key_terms(b, hg)))
+        at(1, 0, nothing, lambda: spread_bias(0))
+        for w in range(PASSES * 4):
+            at(1 + w // NT, w % NT, nothing, lambda w=w: weights_regroup(w // 4, w % 4))
+            at(1 + (w + 2) // NT, (w + 2) % NT, nothing, lambda w=w: weights_quantise(w // 4, w % 4))
+        for t in range(NT):
+            at(2 + (t + 2) // NT, (t + 2) % NT, lambda t=t: tokens_transpose(0, t), lambda t=t: tokens_group(0, t))
+            at(5 + t // 2, 2 * (t % 2), lambda t=t: tokens_transpose(1, t), lambda t=t: tokens_group(1, t))
+        at(3, 0, nothing, load_second_batch)
+        for g in range(PASSES):
+            at(3, 2 + g, nothing, lambda g=g: tokens_quantise(0, g))
+            at(7, g, nothing, lambda g=g: tokens_quantise(1, g))
+        v_ready = {}
+        for c, (b, h) in enumerate(heads):
+            slot = (4 * HG + 1 + 2 * c) if b == 0 else (8 * HG + HG * h)
+            v_ready[b, h // HG] = slot + 3
+            at(slot // HG, slot % HG, lambda b=b, h=h: values_matmul(b, h), lambda b=b, h=h: values_add(b, h))
+            at((slot + 1) // HG, (slot + 1) % HG, nothing, lambda b=b, h=h: values_quantise(b, h))
+        at(6, 0, nothing, lambda: spread_bias(1))
+        free_slot = 0
+        for n in range(len(units)):
+            slot = max((n + 2) * HG + 2, v_ready[units[n][0], units[n][1]], free_slot)
+            at(slot // HG, slot % HG, lambda n=n: e_times_v(n), lambda n=n: blend_by_scalar(n) if n in () else blend(n))
+            free_slot = slot + 2
+        at(3, 3, nothing, lambda: copy_tail(0))
+        at(11, 3, nothing, lambda: copy_tail(1))
+
+        slots = len(units) * HG
+        scores(0)
+        scores(1)
+        for tensor, rest in plan[0]:
+            tensor()
+        for i in range(max(plan) + 1):
+            for tensor, rest in plan.get(i + 1, []):
+                tensor()
+            if i < slots:
+                maximum_and_exp(i)
+            for tensor, rest in plan.get(i, []):
+                rest()
+            if i + 2 < slots:
+                scores(i + 2)

@@ -24,11 +24,11 @@ PASSES = D // (4 * P)
 HG = 4
 W = HG * P
 SCALE = 1.0 / math.sqrt(P)
+MASKED = 1.0e30
 WV_PART = D // 4
-LAG = 5
+LAG = 7
 
-MASK0 = 0
-BV0 = B * S
+BV0 = 0
 GAIN0 = BV0 + D
 GATE_BIAS0 = GAIN0 + 16
 COUNT0 = GAIN0 + 32
@@ -54,14 +54,13 @@ def tile_multiheadedselfattention_pa_kernel(
         psum_b = ctx.enter_context(tc.psum_pool(name="psum_b", bufs=2))
         psum_c = ctx.enter_context(tc.psum_pool(name="psum_c", bufs=2))
 
-        mask_rows = const.tile([P, 2 * P], BF16)
+        mask_rows = const.tile([P, P], BF16)
         nc.vector.memset(mask_rows[:], 0.0)
-        nc.sync.dma_start(out=mask_rows[0 : B * 2, :], in_=value_key_masks.rearrange("b (u w) -> (b u) w", u=2))
+        nc.sync.dma_start(
+            out=mask_rows[0 : B * NT, :], in_=value_key_masks.rearrange("b (t p) -> (b t) p", p=P)
+        )
         small_row = const.tile([P, ROW_W], BF16)
         nc.vector.memset(small_row[:], 0.0)
-        nc.sync.dma_start(
-            out=small_row[0:1, MASK0 : MASK0 + B * S], in_=value_key_masks.rearrange("(o b) s -> o (b s)", o=1)
-        )
 
         k_sb = {}
         q_sb = {}
@@ -128,126 +127,57 @@ def tile_multiheadedselfattention_pa_kernel(
         make_identity(nc, ident_bf[:])
         ident_f32 = const.tile([P, P], F32)
         make_identity(nc, ident_f32[:])
-        before = const.tile([P, P], BF16)
-        nc.gpsimd.memset(before[:], 1.0)
-        nc.gpsimd.affine_select(
-            out=before[:], in_=before[:], compare_op=ALU.is_gt, fill=0.0, base=0, pattern=[[1, P]],
-            channel_multiplier=-1,
-        )
         ones_bf = const.tile([P, P], BF16)
         nc.vector.memset(ones_bf[:], 1.0)
         warm = const.tile([P, 1], F32)
         nc.scalar.activation(out=warm[:], in_=ones_bf[:, 0:1], func=ACT.Exp)
 
-        mask_ps = psum_c.tile([P, 2, P], BF16, tag="c", name="mask_ps")
-        for f in range(2):
-            nc.tensor.transpose(mask_ps[:, f, :], mask_rows[:, f * P : (f + 1) * P], ident_bf[:])
-        pair_ps = psum_c.tile([P, P], F32, tag="c", name="pair_ps")
-        nc.tensor.transpose(pair_ps[:], mask_rows[:].bitcast(F32), ident_f32[:])
-        mask_t = const.tile([P, NT * B], BF16)
-        nc.vector.tensor_copy(
-            out=mask_t[:].rearrange("p (u f b) -> p u f b", u=2, f=2),
-            in_=mask_ps[:, :, 0 : B * 2].rearrange("p f (b u) -> p u f b", u=2),
-        )
-        mask_pair = const.tile([P, B * NT], BF16)
-        nc.vector.tensor_copy(out=mask_pair[:].bitcast(F32), in_=pair_ps[:, 0 : B * 2])
-
-        kept_ps = psum_b.tile([P, S], F32, tag="b", name="kept_ps")
-        nc.tensor.matmul(out=kept_ps[:, 0 : NT * B], lhsT=before[:], rhs=mask_t[:], start=True, stop=False)
-        for t in range(1, NT):
-            nc.tensor.matmul(
-                out=kept_ps[:, t * B : NT * B], lhsT=ones_bf[:], rhs=mask_t[:, 0 : (NT - t) * B], start=False,
-                stop=(t == NT - 1),
-            )
-        for t in range(NT):
-            nc.tensor.matmul(
-                out=kept_ps[:, NT * B : NT * B + B], lhsT=ones_bf[:], rhs=mask_t[:, t * B : (t + 1) * B],
-                start=(t == 0), stop=(t == NT - 1),
-            )
-        select = const.tile([P, NT * B, 2], BF16)
-        nc.vector.tensor_copy(out=select[:, :, 0], in_=mask_t[:])
-        nc.vector.scalar_tensor_tensor(
-            out=select[:, :, 1], in0=kept_ps[:, 0 : NT * B], scalar=0.0, in1=mask_t[:], op0=ALU.is_equal, op1=ALU.mult
-        )
-        minus_masked = const.tile([P, B], F32)
-        nc.vector.tensor_scalar(
-            out=minus_masked[:], in0=kept_ps[:, NT * B : NT * B + B], scalar1=float(S), scalar2=None, op0=ALU.subtract
-        )
-
-        mask_diag = const.tile([P, NT * B, P], BF16)
-        nc.vector.tensor_tensor(
-            out=mask_diag[:], in0=ident_bf[:].unsqueeze(1).to_broadcast([P, NT * B, P]),
-            in1=mask_t[:].unsqueeze(2).to_broadcast([P, NT * B, P]), op=ALU.mult,
-        )
-        pair_diag = const.tile([P, B * NT, P], F32)
-        nc.gpsimd.tensor_tensor(
-            out=pair_diag[:], in0=ident_f32[:].unsqueeze(1).to_broadcast([P, B * NT, P]),
-            in1=mask_pair[:].unsqueeze(2).to_broadcast([P, B * NT, P]), op=ALU.mult,
-        )
-
-        not_mask = const.tile([P, B, S], BF16)
+        mask_ps = psum_c.tile([P, P], BF16, tag="c", name="mask_ps")
+        nc.tensor.transpose(mask_ps[:], mask_rows[:], ident_bf[:])
+        mask_t = const.tile([P, B * NT], BF16)
+        nc.vector.tensor_copy(out=mask_t[:], in_=mask_ps[:, 0 : B * NT])
+        mask_bias_t = const.tile([P, B * NT, P], F32)
         for b in range(B):
-            bc_ps = psum_s.tile([P, S], F32, tag="s", name="bc_ps")
-            nc.tensor.matmul(
-                out=bc_ps[:], lhsT=ones_bf[:], rhs=small_row[:, MASK0 + b * S : MASK0 + (b + 1) * S], start=True, stop=True
+            tiles = slice(b * NT, (b + 1) * NT)
+            nc.vector.tensor_scalar(
+                out=mask_bias_t[:, tiles, :], in0=mask_t[:, tiles].unsqueeze(2).to_broadcast([P, NT, P]),
+                scalar1=1.0, scalar2=MASKED, op0=ALU.subtract, op1=ALU.mult,
             )
-            nc.scalar.activation(out=not_mask[:, b, :], in_=bc_ps[:], func=ACT.Copy, scale=-1.0, bias=1.0)
 
         ks_bank = {}
         ks = {}
         ksum_terms = {}
 
-        def key_sums(b, hg, hh):
-            h = hg * HG + hh
-            if hh == 0:
-                ks_bank[b, hg] = psum_c.tile([P, HG, 2], F32, tag="c", name="ks_bank")
-            for t in range(NT):
-                nc.tensor.matmul(
-                    out=ks_bank[b, hg][:, hh, :], lhsT=k_sb[b][:, t, h * P : (h + 1) * P], rhs=select[:, t * B + b, :],
-                    start=(t == 0), stop=(t == NT - 1),
-                )
-
-        def key_sums_copy(b, hg):
-            ks[b, hg] = small.tile([P, HG, 2], F32, name="ks")
-            nc.vector.tensor_copy(out=ks[b, hg][:], in_=ks_bank[b, hg][:])
+        def key_sums(b, hg):
+            ks_bank[b, hg] = psum_c.tile([P, HG], F32, tag="c", name="ks_bank")
+            for hh in range(HG):
+                h = hg * HG + hh
+                for t in range(NT):
+                    nc.tensor.matmul(
+                        out=ks_bank[b, hg][:, hh : hh + 1], lhsT=k_sb[b][:, t, h * P : (h + 1) * P],
+                        rhs=mask_t[:, b * NT + t : b * NT + t + 1], start=(t == 0), stop=(t == NT - 1),
+                    )
 
         def key_terms(b, hg):
-            terms = small.tile([P, HG, 3], BF16, name="ksum_terms")
-            nc.gpsimd.tensor_copy(out=terms[:, :, 0], in_=ks[b, hg][:, :, 0])
-            nc.gpsimd.tensor_tensor(
-                out=terms[:, :, 1], in0=ks[b, hg][:, :, 0], in1=terms[:, :, 0], op=ALU.subtract
-            )
-            nc.gpsimd.tensor_copy(out=terms[:, :, 2], in_=ks[b, hg][:, :, 1])
+            ks[b, hg] = small.tile([P, HG], F32, name="ks")
+            nc.vector.tensor_copy(out=ks[b, hg][:], in_=ks_bank[b, hg][:])
+            terms = small.tile([P, HG, 2], BF16, name="ksum_terms")
+            nc.gpsimd.tensor_copy(out=terms[:, :, 0], in_=ks[b, hg][:])
+            nc.gpsimd.tensor_tensor(out=terms[:, :, 1], in0=ks[b, hg][:], in1=terms[:, :, 0], op=ALU.subtract)
             ksum_terms[b, hg] = terms
 
-        kT = [keep.tile([P, H, S], BF16, name="kT%d" % b) for b in range(B)]
-        qT = [keep.tile([P, H, S], BF16, name="qT%d" % b) for b in range(B)]
+        kqT = [keep.tile([P, H, 2, S], BF16, name="kqT%d" % b) for b in range(B)]
+        kq_bank = {}
 
-        k_bank = {}
-        q_bank = {}
-
-        def transpose_keys(b, h):
-            k_bank[b, h] = psum_c.tile([P, NT, P], BF16, tag="c", name="k_bank")
-            for t in range(NT):
-                nc.tensor.transpose(
-                    k_bank[b, h][:, t, :], k_sb[b][:, t, h * P : (h + 1) * P], mask_diag[:, t * B + b, :]
-                )
-
-        def fill_keys(b, h):
-            nc.vector.scalar_tensor_tensor(
-                out=kT[b][:, h, :], in0=not_mask[:, b, :], scalar=ks[b, h // HG][:, h % HG, 1:2],
-                in1=k_bank[b, h][:].rearrange("p t r -> p (t r)"), op0=ALU.mult, op1=ALU.add,
-            )
-
-        def transpose_queries(b, h):
-            q_bank[b, h] = psum_c.tile([P, 2, NT, P], BF16, tag="c", name="q_bank")
-            for h2 in range(2):
-                cols = slice((h + h2) * P, (h + h2 + 1) * P)
+        def transpose_kq(b, h):
+            cols = slice(h * P, (h + 1) * P)
+            kq_bank[b, h] = psum_c.tile([P, 2, NT, P], BF16, tag="c", name="kq_bank")
+            for i, tokens in enumerate((k_sb[b], q_sb[b])):
                 for t in range(NT):
-                    nc.tensor.transpose(q_bank[b, h][:, h2, t, :], q_sb[b][:, t, cols], ident_bf[:])
+                    nc.tensor.transpose(kq_bank[b, h][:, i, t, :], tokens[:, t, cols], ident_bf[:])
 
-        def copy_queries(b, h):
-            nc.scalar.copy(out=qT[b][:, h : h + 2, :], in_=q_bank[b, h][:].rearrange("p h t r -> p h (t r)"))
+        def copy_kq(b, h):
+            nc.scalar.copy(out=kqT[b][:, h, :, :], in_=kq_bank[b, h][:].rearrange("p i t r -> p i (t r)"))
 
         small_bc = const.tile([P, SMALL_W], F32)
         small_bank = {}
@@ -287,10 +217,7 @@ def tile_multiheadedselfattention_pa_kernel(
             grouped = stage.tile([P, WV_PART, 4], BF16, align_bytes=64, name="wv_grouped", bufs=4)
             out_cols = grouped[:].rearrange("p (c i) t -> p c t i", i=4)
             in_cols = wv_raw[:, g, :, cols].rearrange("p t (c i) -> p c t i", i=4)
-            if part % 2 == 0:
-                nc.vector.tensor_copy(out=out_cols, in_=in_cols)
-            else:
-                nc.scalar.copy(out=out_cols, in_=in_cols)
+            nc.vector.tensor_copy(out=out_cols, in_=in_cols)
             wv_grouped[g, part] = grouped
 
         def weights_quantise(g, part):
@@ -306,15 +233,6 @@ def tile_multiheadedselfattention_pa_kernel(
         v_codes = keep.tile([P, B, D], U32, align_bytes=64)
         v_scales = keep.tile([P, B, D], U8, align_bytes=64)
         pvk_grouped = {}
-        bias_kept = {}
-
-        def spread_bias(b):
-            bias_kept[b] = stage.tile([P, NT, D], BF16, name="bias_kept")
-            for t in range(NT):
-                nc.gpsimd.tensor_scalar(
-                    out=bias_kept[b][:, t, :], in0=small_bc[:, 0:D], scalar1=mask_pair[:, b * NT + t : b * NT + t + 1],
-                    scalar2=0.0, op0=ALU.mult, op1=ALU.add,
-                )
 
         w_bank = {}
 
@@ -325,7 +243,7 @@ def tile_multiheadedselfattention_pa_kernel(
                 for u in range(2):
                     first = (2 * g + u) * P
                     nc.tensor.transpose(
-                        w_bank[b, t][:, g, u, :], pvk_words[:, t, first : first + P], pair_diag[:, b * NT + t, :]
+                        w_bank[b, t][:, g, u, :], pvk_words[:, t, first : first + P], ident_f32[:]
                     )
 
         def tokens_group(b, t):
@@ -368,7 +286,7 @@ def tile_multiheadedselfattention_pa_kernel(
             nc.vector.tensor_tensor(
                 out=v_grouped[b, h][:],
                 in0=v_bank[b, h][:].rearrange("p t c -> p c t"),
-                in1=bias_kept[b][:, :, cols].rearrange("p t c -> p c t"),
+                in1=small_bc[:, cols].unsqueeze(2).to_broadcast([P, P, NT]),
                 op=ALU.add,
             )
 
@@ -382,17 +300,16 @@ def tile_multiheadedselfattention_pa_kernel(
 
         gate = {}
         one_minus_gate = {}
-        copy_score = {}
         pooled_bank = {}
         shifted_score = {}
 
         def pool_scores(b, hg):
-            pooled_bank[b, hg] = psum_c.tile([P, NT, HG, 3], F32, tag="c", name="pooled_bank")
+            pooled_bank[b, hg] = psum_c.tile([P, NT, HG, 2], F32, tag="c", name="pooled_bank")
             for it in range(NT):
                 for hh in range(HG):
                     nc.tensor.matmul(
                         out=pooled_bank[b, hg][:, it, hh, :],
-                        lhsT=qT[b][:, hg * HG + hh, it * P : (it + 1) * P],
+                        lhsT=kqT[b][:, hg * HG + hh, 1, it * P : (it + 1) * P],
                         rhs=ksum_terms[b, hg][:, hh, :],
                         start=True,
                         stop=True,
@@ -402,11 +319,7 @@ def tile_multiheadedselfattention_pa_kernel(
             heads = slice(hg * HG, (hg + 1) * HG)
             pooled_ps = pooled_bank[b, hg]
             pooled = small.tile([P, NT, HG], F32)
-            nc.vector.tensor_reduce(out=pooled[:], in_=pooled_ps[:, :, :, 0:2], axis=AX.X, op=ALU.add)
-            copy_score[b, hg] = small.tile([P, NT, HG], F32, name="copy_score")
-            nc.vector.tensor_scalar(
-                out=copy_score[b, hg][:], in0=pooled_ps[:, :, :, 2], scalar1=SCALE, scalar2=None, op0=ALU.mult
-            )
+            nc.vector.tensor_reduce(out=pooled[:], in_=pooled_ps[:], axis=AX.X, op=ALU.add)
             scaled = small.tile([P, NT, HG], F32)
             nc.gpsimd.tensor_tensor(
                 out=scaled[:], in0=pooled[:], in1=gate_scale[:, b, heads].unsqueeze(1).to_broadcast([P, NT, HG]),
@@ -442,9 +355,6 @@ def tile_multiheadedselfattention_pa_kernel(
         exp_bias = {}
         e_bf = {}
         row_sum = {}
-        copy_arg = {}
-        copy_e = {}
-        kept_sum = {}
         inv_sum = {}
         e_grouped = {}
         e_codes = {}
@@ -460,21 +370,36 @@ def tile_multiheadedselfattention_pa_kernel(
             b, hg, it = units[n]
             h = hg * HG + hh
             s_bank[i] = psum_s.tile([P, S], F32, tag="s", name="s_bank")
+            for t in range(NT):
+                nc.tensor.matmul(
+                    out=s_bank[i][:, t * P : (t + 1) * P], lhsT=mask_bias_t[:, b * NT + t, :], rhs=ident_f32[:],
+                    is_transpose=True, start=(t == 0), stop=False,
+                )
             nc.tensor.matmul(
-                out=s_bank[i][:], lhsT=qT[b][:, h, it * P : (it + 1) * P], rhs=kT[b][:, h, :], start=True, stop=True
+                out=s_bank[i][:], lhsT=kqT[b][:, h, 1, it * P : (it + 1) * P], rhs=kqT[b][:, h, 0, :], start=False,
+                stop=True,
             )
 
-        def maximum_and_exp(i):
+        highest = {}
+
+        def maximum(i):
+            n, hh = divmod(i, HG)
+            if hh == 0:
+                highest[n] = small.tile([P, HG], F32, name="highest", bufs=3)
+                e_bf[n] = stage.tile([P, HG, S], BF16, name="e_bf", bufs=3)
+                row_sum[n] = small.tile([P, HG], F32, name="row_sum", bufs=4)
+            nc.vector.tensor_reduce(out=highest[n][:, hh : hh + 1], in_=s_bank[i][:], axis=AX.X, op=ALU.max)
+
+        def scale_maximum(i):
             n, hh = divmod(i, HG)
             if hh == 0:
                 exp_bias[n] = small.tile([P, HG], F32, name="exp_bias", bufs=3)
-                e_bf[n] = stage.tile([P, HG, S], BF16, name="e_bf", bufs=3)
-                row_sum[n] = small.tile([P, HG], F32, name="row_sum", bufs=4)
-            products = stage.tile([P, S], BF16, bufs=1, name="products")
-            nc.vector.tensor_scalar(
-                out=products[:], in0=s_bank[i][:], scalar1=-SCALE, scalar2=None, op0=ALU.mult, op1=ALU.min,
-                accum_out=exp_bias[n][:, hh : hh + 1],
+            nc.scalar.activation(
+                out=exp_bias[n][:, hh : hh + 1], in_=highest[n][:, hh : hh + 1], func=ACT.Copy, scale=-SCALE
             )
+
+        def exponential(i):
+            n, hh = divmod(i, HG)
             nc.scalar.activation(
                 out=e_bf[n][:, hh, :],
                 in_=s_bank[i][:],
@@ -483,17 +408,6 @@ def tile_multiheadedselfattention_pa_kernel(
                 scale=SCALE,
                 accum_out=row_sum[n][:, hh : hh + 1],
             )
-
-        def copies_argument(n):
-            b, hg, it = units[n]
-            copy_arg[n] = small.tile([P, HG], F32, name="copy_arg")
-            nc.gpsimd.tensor_tensor(
-                out=copy_arg[n][:], in0=copy_score[b, hg][:, it, :], in1=exp_bias[n][:], op=ALU.add
-            )
-
-        def copies_exp(n):
-            copy_e[n] = small.tile([P, HG], F32, name="copy_e")
-            nc.scalar.activation(out=copy_e[n][:], in_=copy_arg[n][:], func=ACT.Exp)
 
         e_bank = {}
 
@@ -514,18 +428,9 @@ def tile_multiheadedselfattention_pa_kernel(
                 in_=e_bank[n, pair][:].rearrange("p h u i -> p h i u"),
             )
 
-        def kept_sums(n):
-            b, hg, it = units[n]
-            part = small.tile([P, HG], F32, name="part")
-            nc.gpsimd.tensor_scalar(
-                out=part[:], in0=copy_e[n][:], scalar1=minus_masked[:, b : b + 1], scalar2=0.0, op0=ALU.mult, op1=ALU.add
-            )
-            kept_sum[n] = small.tile([P, HG], F32, name="kept_sum")
-            nc.gpsimd.tensor_tensor(out=kept_sum[n][:], in0=row_sum[n][:], in1=part[:], op=ALU.add)
-
         def invert_sums(n):
             inv_sum[n] = small.tile([P, HG], F32, name="inv_sum")
-            nc.vector.reciprocal(out=inv_sum[n][:], in_=kept_sum[n][:])
+            nc.vector.reciprocal(out=inv_sum[n][:], in_=row_sum[n][:])
 
         def blend_weights(n):
             b, hg, it = units[n]
@@ -572,43 +477,19 @@ def tile_multiheadedselfattention_pa_kernel(
 
         def blend(n):
             b, hg, it = units[n]
-            for hh in range(HG):
-                cols = slice(hh * P, (hh + 1) * P)
-                nc.vector.scalar_tensor_tensor(
-                    out=result[n][:, cols],
-                    in0=h_bank[n][:, hh, :],
-                    scalar=weight[n][:, hh : hh + 1],
-                    in1=result[n][:, cols],
-                    op0=ALU.mult,
-                    op1=ALU.add,
-                )
-            nc.sync.dma_start(out=out_view[b][:, it, hg * W : (hg + 1) * W], in_=result[n][:])
-
-        def blend_by_scalar(n):
-            b, hg, it = units[n]
-            product = stage.tile([P, W], F32, name="product")
-            for hh in range(HG):
-                nc.scalar.activation(
-                    out=product[:, hh * P : (hh + 1) * P], in_=h_bank[n][:, hh, :], func=ACT.Copy,
-                    scale=weight[n][:, hh : hh + 1],
-                )
-            nc.gpsimd.tensor_tensor(out=result[n][:], in0=product[:], in1=result[n][:], op=ALU.add)
+            product = stage.tile([P, HG, P], F32, name="product")
+            nc.vector.tensor_tensor(
+                out=product[:], in0=h_bank[n][:], in1=weight[n][:].unsqueeze(2).to_broadcast([P, HG, P]), op=ALU.mult
+            )
+            nc.gpsimd.tensor_tensor(
+                out=result[n][:], in0=product[:].rearrange("p h c -> p (h c)"), in1=result[n][:], op=ALU.add
+            )
             nc.sync.dma_start(out=out_view[b][:, it, hg * W : (hg + 1) * W], in_=result[n][:])
 
         heads = [(b, h) for b in range(B) for h in range(H)]
         groups = [(b, hg) for b in range(B) for hg in range(H // HG)]
         last = len(units) - 1
         plan = {}
-        for hh in range(HG):
-            key_sums(0, 0, hh)
-        transpose_keys(0, 0)
-        key_sums_copy(0, 0)
-        key_terms(0, 0)
-        fill_keys(0, 0)
-        transpose_queries(0, 0)
-        copy_queries(0, 0)
-        transpose_keys(0, 1)
-        fill_keys(0, 1)
 
         def at(n, hh, tensor, rest):
             plan.setdefault(n * HG + hh, []).append((tensor, rest))
@@ -616,33 +497,30 @@ def tile_multiheadedselfattention_pa_kernel(
         def nothing():
             pass
 
-        for n in range(len(units)):
-            at(n, 3, lambda n=n: transpose_e(n, 0), lambda n=n: group_e(n, 0))
-            at(n + 1, 1, lambda n=n: transpose_e(n, 1), lambda n=n: group_e(n, 1))
-            at(n + 1, 0, nothing, lambda n=n: copies_argument(n))
-            at(n + 1, 2, nothing, lambda n=n: copies_exp(n))
-            at(n + 1, 3, nothing, lambda n=n: (quantise_e(n), kept_sums(n), blend_rest(n)))
-            at(n + 2, 1, nothing, lambda n=n: (invert_sums(n), blend_weights(n)))
-        at(0, 0, lambda: transpose_queries(0, 2), lambda: copy_queries(0, 2))
-        at(0, 0, lambda: transpose_keys(0, 2), lambda: fill_keys(0, 2))
-        at(0, 1, lambda: transpose_keys(0, 3), lambda: fill_keys(0, 3))
+        for h in range(3):
+            transpose_kq(0, h)
+            copy_kq(0, h)
+        at(0, 0, lambda: transpose_kq(0, 3), lambda: copy_kq(0, 3))
+        at(0, 0, lambda: key_sums(0, 0), lambda: key_terms(0, 0))
         for i, first in enumerate((D, 0, S)):
             at(0, i, lambda first=first: small_spread(first), lambda first=first: small_copy(first))
         at(0, 2, nothing, gate_scales)
+        for n in range(len(units)):
+            at(n, 3, lambda n=n: transpose_e(n, 0), lambda n=n: group_e(n, 0))
+            at(n + 1, 1, lambda n=n: transpose_e(n, 1), lambda n=n: group_e(n, 1))
+            at(n + 1, 0, nothing, lambda n=n: invert_sums(n))
+            at(n + 1, 2, nothing, lambda n=n: blend_rest(n))
+            at(n + 1, 3, nothing, lambda n=n: quantise_e(n))
+            at(n + 2, 1, nothing, lambda n=n: blend_weights(n))
         for c in range(HG, len(heads)):
             b, h = heads[c]
-            if h % 2 == 0:
-                at(c - HG, 0, lambda b=b, h=h: transpose_queries(b, h), lambda b=b, h=h: copy_queries(b, h))
-            at(c - HG, 3 if c == HG else 1, lambda b=b, h=h: transpose_keys(b, h), lambda b=b, h=h: fill_keys(b, h))
+            at(c - HG, 3 if c == HG else 1, lambda b=b, h=h: transpose_kq(b, h), lambda b=b, h=h: copy_kq(b, h))
         for g, (b, hg) in enumerate(groups):
-            slot = g * NT * HG - 2 if g > 0 else HG - 1
+            slot = g * NT * HG - 1 if g > 0 else HG - 1
             at(slot // HG, slot % HG, lambda b=b, hg=hg: pool_scores(b, hg), lambda b=b, hg=hg: gates(b, hg))
             at((slot + 2) // HG, (slot + 2) % HG, nothing, lambda b=b, hg=hg: sigmoids(b, hg))
             if g >= 1:
-                slot = (g - 1) * NT * HG - 2 if g > 1 else 2
-                at(slot // HG, slot % HG, lambda b=b, hg=hg: [key_sums(b, hg, hh) for hh in range(HG)],
-                   lambda b=b, hg=hg: (key_sums_copy(b, hg), key_terms(b, hg)))
-        at(1, 0, nothing, lambda: spread_bias(0))
+                at(g * NT - 2, 3, lambda b=b, hg=hg: key_sums(b, hg), lambda b=b, hg=hg: key_terms(b, hg))
         for w in range(PASSES * 4):
             at(1 + w // NT, w % NT, nothing, lambda w=w: weights_regroup(w // 4, w % 4))
             at(1 + (w + 2) // NT, (w + 2) % NT, nothing, lambda w=w: weights_quantise(w // 4, w % 4))
@@ -659,11 +537,10 @@ def tile_multiheadedselfattention_pa_kernel(
             v_ready[b, h // HG] = slot + 3
             at(slot // HG, slot % HG, lambda b=b, h=h: values_matmul(b, h), lambda b=b, h=h: values_add(b, h))
             at((slot + 1) // HG, (slot + 1) % HG, nothing, lambda b=b, h=h: values_quantise(b, h))
-        at(6, 0, nothing, lambda: spread_bias(1))
         free_slot = 0
         for n in range(len(units)):
             slot = max((n + 2) * HG + 2, v_ready[units[n][0], units[n][1]], free_slot)
-            at(slot // HG, slot % HG, lambda n=n: e_times_v(n), lambda n=n: blend_by_scalar(n) if n in () else blend(n))
+            at(slot // HG, slot % HG, lambda n=n: e_times_v(n), lambda n=n: blend(n))
             free_slot = slot + 2
         at(3, 3, nothing, lambda: copy_tail(0))
         at(11, 3, nothing, lambda: copy_tail(1))
@@ -671,14 +548,21 @@ def tile_multiheadedselfattention_pa_kernel(
         slots = len(units) * HG
         scores(0)
         scores(1)
+        scores(2)
+        maximum(0)
+        scale_maximum(0)
         for tensor, rest in plan[0]:
             tensor()
         for i in range(max(plan) + 1):
             for tensor, rest in plan.get(i + 1, []):
                 tensor()
+            if i + 1 < slots:
+                maximum(i + 1)
             if i < slots:
-                maximum_and_exp(i)
+                exponential(i)
+            if i + 1 < slots:
+                scale_maximum(i + 1)
             for tensor, rest in plan.get(i, []):
                 rest()
-            if i + 2 < slots:
-                scores(i + 2)
+            if i + 3 < slots:
+                scores(i + 3)

@@ -388,15 +388,17 @@ def tile_multiheadedselfattention_pa_kernel(
                 highest[n] = small.tile([P, HG], F32, name="highest", bufs=3)
                 e_bf[n] = stage.tile([P, HG, S], BF16, name="e_bf", bufs=3)
                 row_sum[n] = small.tile([P, HG], F32, name="row_sum", bufs=4)
-            nc.vector.tensor_reduce(out=highest[n][:, hh : hh + 1], in_=s_bank[i][:], axis=AX.X, op=ALU.max)
+            products = stage.tile([P, S], BF16, bufs=4, name="products")
+            nc.vector.tensor_scalar(
+                out=products[:], in0=s_bank[i][:], scalar1=-SCALE, scalar2=None, op0=ALU.mult, op1=ALU.min,
+                accum_out=highest[n][:, hh : hh + 1],
+            )
 
         def scale_maximum(i):
             n, hh = divmod(i, HG)
             if hh == 0:
                 exp_bias[n] = small.tile([P, HG], F32, name="exp_bias", bufs=3)
-            nc.scalar.activation(
-                out=exp_bias[n][:, hh : hh + 1], in_=highest[n][:, hh : hh + 1], func=ACT.Copy, scale=-SCALE
-            )
+            pass
 
         def exponential(i):
             n, hh = divmod(i, HG)
@@ -404,7 +406,7 @@ def tile_multiheadedselfattention_pa_kernel(
                 out=e_bf[n][:, hh, :],
                 in_=s_bank[i][:],
                 func=ACT.Exp,
-                bias=exp_bias[n][:, hh : hh + 1],
+                bias=highest[n][:, hh : hh + 1],
                 scale=SCALE,
                 accum_out=row_sum[n][:, hh : hh + 1],
             )
@@ -477,13 +479,16 @@ def tile_multiheadedselfattention_pa_kernel(
 
         def blend(n):
             b, hg, it = units[n]
-            product = stage.tile([P, HG, P], F32, name="product")
-            nc.vector.tensor_tensor(
-                out=product[:], in0=h_bank[n][:], in1=weight[n][:].unsqueeze(2).to_broadcast([P, HG, P]), op=ALU.mult
-            )
-            nc.gpsimd.tensor_tensor(
-                out=result[n][:], in0=product[:].rearrange("p h c -> p (h c)"), in1=result[n][:], op=ALU.add
-            )
+            for hh in range(HG):
+                cols = slice(hh * P, (hh + 1) * P)
+                nc.vector.scalar_tensor_tensor(
+                    out=result[n][:, cols],
+                    in0=h_bank[n][:, hh, :],
+                    scalar=weight[n][:, hh : hh + 1],
+                    in1=result[n][:, cols],
+                    op0=ALU.mult,
+                    op1=ALU.add,
+                )
             nc.sync.dma_start(out=out_view[b][:, it, hg * W : (hg + 1) * W], in_=result[n][:])
 
         heads = [(b, h) for b in range(B) for h in range(H)]

@@ -25,7 +25,8 @@ HG = 4
 W = HG * P
 SCALE = 1.0 / math.sqrt(P)
 MASKED = 1.0e30
-WV_PART = D // 4
+WV_PARTS = 4
+WV_PART = D // WV_PARTS
 LAG = 7
 
 BV0 = 0
@@ -50,9 +51,9 @@ def tile_multiheadedselfattention_pa_kernel(
         keep = ctx.enter_context(tc.tile_pool(name="keep", bufs=1))
         stage = ctx.enter_context(tc.tile_pool(name="stage", bufs=2))
         small = ctx.enter_context(tc.tile_pool(name="small", bufs=2))
-        psum_s = ctx.enter_context(tc.psum_pool(name="psum_s", bufs=4))
+        psum_s = ctx.enter_context(tc.psum_pool(name="psum_s", bufs=3))
         psum_b = ctx.enter_context(tc.psum_pool(name="psum_b", bufs=2))
-        psum_c = ctx.enter_context(tc.psum_pool(name="psum_c", bufs=2))
+        psum_c = ctx.enter_context(tc.psum_pool(name="psum_c", bufs=3))
 
         mask_rows = const.tile([P, P], BF16)
         nc.vector.memset(mask_rows[:], 0.0)
@@ -78,7 +79,7 @@ def tile_multiheadedselfattention_pa_kernel(
 
         def load_pvk(b):
             nc.sync.dma_start(
-                out=pvk_sb[b].rearrange("p (u e) d -> p u (e d)", e=2),
+                out=pvk_sb[b][:].rearrange("p (u e) d -> p u (e d)", e=2),
                 in_=pre_value_key[b].rearrange("(u p e) d -> p u (e d)", u=2, e=2),
             )
 
@@ -86,10 +87,22 @@ def tile_multiheadedselfattention_pa_kernel(
             pq_sb[b] = raw.tile([P, NT, DQ], BF16, name="pq_sb%d" % b)
             nc.sync.dma_start(out=pq_sb[b][:], in_=pre_query[b].rearrange("(p t) c -> p t c", t=NT))
 
+        wv_raw = raw.tile([P, PASSES, 4, D], BF16, name="wv_raw")
+
+        def load_wv(g, half):
+            cols = slice(half * S, (half + 1) * S)
+            for u in range(2):
+                rows = slice((2 * g + u) * 2 * P, (2 * g + u + 1) * 2 * P)
+                nc.sync.dma_start(
+                    out=wv_raw[:, g, 2 * u : 2 * u + 2, cols], in_=Wv[rows, cols].rearrange("(p e) n -> p e n", e=2)
+                )
+
         k_sb[0] = raw.tile([P, NT, D], BF16, name="k_sb0")
         q_sb[0] = raw.tile([P, NT, D], BF16, name="q_sb0")
+        load_wv(0, 0)
         load_k(0, 0)
         load_q(0, 0)
+        load_wv(0, 1)
         for first, width, vector in (
             (BV0, D, bv.rearrange("(o n) -> o n", o=1)),
             (GAIN0, H, overall_gain.rearrange("a h b c -> a (h b c)")),
@@ -99,29 +112,20 @@ def tile_multiheadedselfattention_pa_kernel(
             nc.sync.dma_start(out=small_row[0:1, first : first + width], in_=vector)
         load_k(0, 1)
         load_q(0, 1)
-        wv_raw = raw.tile([P, PASSES, 4, D], BF16, name="wv_raw", tag="wide")
-        for g in range(PASSES):
-            nc.sync.dma_start(
-                out=wv_raw[:, g].rearrange("p (u e) n -> p u (e n)", e=2),
-                in_=Wv[g * 4 * P : (g + 1) * 4 * P, :].rearrange("(u p e) n -> p u (e n)", u=2, e=2),
-            )
-        pvk_first = raw.tile([P, NT, D], BF16, name="pvk_first")
-        pvk_sb[0] = pvk_first[:]
+        load_wv(1, 0)
+        load_wv(1, 1)
+        pvk_sb[0] = raw.tile([P, NT, D], BF16, name="pvk_sb0")
         load_pvk(0)
         load_pq(0)
 
         k_sb[1] = raw.tile([P, NT, D], BF16, name="k_sb1")
+        q_sb[1] = raw.tile([P, NT, D], BF16, name="q_sb1")
         for hg in range(2):
             load_k(1, hg)
-
-        def load_second_batch():
-            wide = raw.tile([P, PASSES, 4, D], BF16, name="wide", tag="wide")
-            pvk_sb[1] = wide[:, 0]
-            q_sb[1] = wide[:, 1]
-            load_q(1, 0)
-            load_pvk(1)
-            load_q(1, 1)
-            load_pq(1)
+            load_q(1, hg)
+        pvk_sb[1] = raw.tile([P, NT, D], BF16, name="pvk_sb1")
+        load_pvk(1)
+        load_pq(1)
 
         ident_bf = const.tile([P, P], BF16)
         make_identity(nc, ident_bf[:])
@@ -237,7 +241,7 @@ def tile_multiheadedselfattention_pa_kernel(
         w_bank = {}
 
         def tokens_transpose(b, t):
-            pvk_words = pvk_sb[b].bitcast(F32)
+            pvk_words = pvk_sb[b][:].bitcast(F32)
             w_bank[b, t] = psum_c.tile([P, PASSES, 2, P], F32, tag="c", name="w_bank")
             for g in range(PASSES):
                 for u in range(2):
@@ -380,25 +384,17 @@ def tile_multiheadedselfattention_pa_kernel(
                 stop=True,
             )
 
-        highest = {}
-
         def maximum(i):
             n, hh = divmod(i, HG)
             if hh == 0:
-                highest[n] = small.tile([P, HG], F32, name="highest", bufs=3)
+                exp_bias[n] = small.tile([P, HG], F32, name="exp_bias", bufs=3)
                 e_bf[n] = stage.tile([P, HG, S], BF16, name="e_bf", bufs=3)
                 row_sum[n] = small.tile([P, HG], F32, name="row_sum", bufs=4)
-            products = stage.tile([P, S], BF16, bufs=4, name="products")
+            products = stage.tile([P, S], BF16, bufs=2, name="products")
             nc.vector.tensor_scalar(
                 out=products[:], in0=s_bank[i][:], scalar1=-SCALE, scalar2=None, op0=ALU.mult, op1=ALU.min,
-                accum_out=highest[n][:, hh : hh + 1],
+                accum_out=exp_bias[n][:, hh : hh + 1],
             )
-
-        def scale_maximum(i):
-            n, hh = divmod(i, HG)
-            if hh == 0:
-                exp_bias[n] = small.tile([P, HG], F32, name="exp_bias", bufs=3)
-            pass
 
         def exponential(i):
             n, hh = divmod(i, HG)
@@ -406,7 +402,7 @@ def tile_multiheadedselfattention_pa_kernel(
                 out=e_bf[n][:, hh, :],
                 in_=s_bank[i][:],
                 func=ACT.Exp,
-                bias=highest[n][:, hh : hh + 1],
+                bias=exp_bias[n][:, hh : hh + 1],
                 scale=SCALE,
                 accum_out=row_sum[n][:, hh : hh + 1],
             )
@@ -493,81 +489,79 @@ def tile_multiheadedselfattention_pa_kernel(
 
         heads = [(b, h) for b in range(B) for h in range(H)]
         groups = [(b, hg) for b in range(B) for hg in range(H // HG)]
-        last = len(units) - 1
+        slots = len(units) * HG
+        mx_plan = {}
+        tensor_plan = {}
         plan = {}
 
-        def at(n, hh, tensor, rest):
-            plan.setdefault(n * HG + hh, []).append((tensor, rest))
+        def at(slot, rest, tensor=None, mx=None):
+            plan.setdefault(slot, []).append(rest)
+            if tensor is not None:
+                tensor_plan.setdefault(slot, []).append(tensor)
+            if mx is not None:
+                mx_plan.setdefault(slot, []).append(mx)
 
-        def nothing():
-            pass
-
-        for h in range(3):
-            transpose_kq(0, h)
-            copy_kq(0, h)
-        at(0, 0, lambda: transpose_kq(0, 3), lambda: copy_kq(0, 3))
-        at(0, 0, lambda: key_sums(0, 0), lambda: key_terms(0, 0))
+        at(1, lambda: key_terms(0, 0), tensor=lambda: key_sums(0, 0))
         for i, first in enumerate((D, 0, S)):
-            at(0, i, lambda first=first: small_spread(first), lambda first=first: small_copy(first))
-        at(0, 2, nothing, gate_scales)
+            at(1 + i, lambda first=first: small_copy(first), tensor=lambda first=first: small_spread(first))
+        at(3, gate_scales)
         for n in range(len(units)):
-            at(n, 3, lambda n=n: transpose_e(n, 0), lambda n=n: group_e(n, 0))
-            at(n + 1, 1, lambda n=n: transpose_e(n, 1), lambda n=n: group_e(n, 1))
-            at(n + 1, 0, nothing, lambda n=n: invert_sums(n))
-            at(n + 1, 2, nothing, lambda n=n: blend_rest(n))
-            at(n + 1, 3, nothing, lambda n=n: quantise_e(n))
-            at(n + 2, 1, nothing, lambda n=n: blend_weights(n))
+            start = n * HG
+            at(start + 3, lambda n=n: group_e(n, 0), tensor=lambda n=n: transpose_e(n, 0))
+            at(start + 5, lambda n=n: group_e(n, 1), tensor=lambda n=n: transpose_e(n, 1))
+            at(start + 5, lambda n=n: invert_sums(n))
+            at(start + 6, lambda n=n: blend_rest(n))
+            at(start + 7, lambda n=n: quantise_e(n))
+            at(start + 9, lambda n=n: blend_weights(n))
         for c in range(HG, len(heads)):
             b, h = heads[c]
-            at(c - HG, 3 if c == HG else 1, lambda b=b, h=h: transpose_kq(b, h), lambda b=b, h=h: copy_kq(b, h))
+            at((c - HG) * HG + 1, lambda b=b, h=h: copy_kq(b, h), tensor=lambda b=b, h=h: transpose_kq(b, h))
         for g, (b, hg) in enumerate(groups):
-            slot = g * NT * HG - 1 if g > 0 else HG - 1
-            at(slot // HG, slot % HG, lambda b=b, hg=hg: pool_scores(b, hg), lambda b=b, hg=hg: gates(b, hg))
-            at((slot + 2) // HG, (slot + 2) % HG, nothing, lambda b=b, hg=hg: sigmoids(b, hg))
-            if g >= 1:
-                at(g * NT - 2, 3, lambda b=b, hg=hg: key_sums(b, hg), lambda b=b, hg=hg: key_terms(b, hg))
-        for w in range(PASSES * 4):
-            at(1 + w // NT, w % NT, nothing, lambda w=w: weights_regroup(w // 4, w % 4))
-            at(1 + (w + 2) // NT, (w + 2) % NT, nothing, lambda w=w: weights_quantise(w // 4, w % 4))
-        for t in range(NT):
-            at(2 + (t + 2) // NT, (t + 2) % NT, lambda t=t: tokens_transpose(0, t), lambda t=t: tokens_group(0, t))
-            at(5 + t // 2, 2 * (t % 2), lambda t=t: tokens_transpose(1, t), lambda t=t: tokens_group(1, t))
-        at(3, 0, nothing, load_second_batch)
-        for g in range(PASSES):
-            at(3, 2 + g, nothing, lambda g=g: tokens_quantise(0, g))
-            at(7, g, nothing, lambda g=g: tokens_quantise(1, g))
-        v_ready = {}
+            slot = g * NT * HG if g > 0 else 3
+            if g > 0:
+                at(slot - 2 * HG, lambda b=b, hg=hg: key_terms(b, hg), tensor=lambda b=b, hg=hg: key_sums(b, hg))
+            at(slot, lambda b=b, hg=hg: gates(b, hg), tensor=lambda b=b, hg=hg: pool_scores(b, hg))
+            at(slot + 2, lambda b=b, hg=hg: sigmoids(b, hg))
+        for w in range(1, PASSES * WV_PARTS):
+            at(w - 1, lambda w=w: weights_regroup(w // WV_PARTS, w % WV_PARTS))
+        for w in range(PASSES * WV_PARTS):
+            at(w + 1, lambda w=w: weights_quantise(w // WV_PARTS, w % WV_PARTS))
+        for b, slot, stride in ((0, 5, 1), (1, 10, 2)):
+            for t in range(NT):
+                at(
+                    slot + t * stride, lambda b=b, t=t: tokens_group(b, t),
+                    tensor=lambda b=b, t=t: tokens_transpose(b, t),
+                )
+            for g in range(PASSES):
+                at(slot + (NT - 1) * stride + 1 + g, lambda b=b, g=g: tokens_quantise(b, g))
+        v_slot = {}
         for c, (b, h) in enumerate(heads):
-            slot = (4 * HG + 1 + 2 * c) if b == 0 else (8 * HG + HG * h)
-            v_ready[b, h // HG] = slot + 3
-            at(slot // HG, slot % HG, lambda b=b, h=h: values_matmul(b, h), lambda b=b, h=h: values_add(b, h))
-            at((slot + 1) // HG, (slot + 1) % HG, nothing, lambda b=b, h=h: values_quantise(b, h))
+            slot = 4 * HG + 2 * c if b == 0 else (4 + h) * HG + 4 * HG
+            v_slot[b, h // HG] = slot + 1
+            at(slot, lambda b=b, h=h: values_add(b, h), mx=lambda b=b, h=h: values_matmul(b, h))
+            at(slot + 1, lambda b=b, h=h: values_quantise(b, h))
         free_slot = 0
         for n in range(len(units)):
-            slot = max((n + 2) * HG + 2, v_ready[units[n][0], units[n][1]], free_slot)
-            at(slot // HG, slot % HG, lambda n=n: e_times_v(n), lambda n=n: blend(n))
+            b, hg, it = units[n]
+            slot = max(n * HG + 10, v_slot[b, hg] + 2, free_slot)
+            at(slot, lambda n=n: blend(n), mx=lambda n=n: e_times_v(n))
             free_slot = slot + 2
-        at(3, 3, nothing, lambda: copy_tail(0))
-        at(11, 3, nothing, lambda: copy_tail(1))
+        for b in range(B):
+            at(15 + b * 29, lambda b=b: copy_tail(b))
 
-        slots = len(units) * HG
-        scores(0)
-        scores(1)
-        scores(2)
-        maximum(0)
-        scale_maximum(0)
-        for tensor, rest in plan[0]:
-            tensor()
+        for h in range(HG):
+            transpose_kq(0, h)
+            copy_kq(0, h)
+        weights_regroup(0, 0)
+        for i in range(2):
+            scores(i)
         for i in range(max(plan) + 1):
-            for tensor, rest in plan.get(i + 1, []):
-                tensor()
-            if i + 1 < slots:
-                maximum(i + 1)
+            for work in mx_plan.get(i + 1, []) + tensor_plan.get(i + 1, []):
+                work()
             if i < slots:
+                maximum(i)
                 exponential(i)
-            if i + 1 < slots:
-                scale_maximum(i + 1)
-            for tensor, rest in plan.get(i, []):
-                rest()
-            if i + 3 < slots:
-                scores(i + 3)
+            for work in plan.get(i, []):
+                work()
+            if i + 2 < slots:
+                scores(i + 2)

@@ -51,8 +51,8 @@ def tile_multiheadedselfattention_pa_kernel(
         keep = ctx.enter_context(tc.tile_pool(name="keep", bufs=1))
         stage = ctx.enter_context(tc.tile_pool(name="stage", bufs=2))
         small = ctx.enter_context(tc.tile_pool(name="small", bufs=2))
-        psum_s = ctx.enter_context(tc.psum_pool(name="psum_s", bufs=3))
-        psum_b = ctx.enter_context(tc.psum_pool(name="psum_b", bufs=2))
+        psum_s = ctx.enter_context(tc.psum_pool(name="psum_s", bufs=4))
+        psum_b = ctx.enter_context(tc.psum_pool(name="psum_b", bufs=1))
         psum_c = ctx.enter_context(tc.psum_pool(name="psum_c", bufs=3))
 
         mask_rows = const.tile([P, P], BF16)
@@ -87,14 +87,15 @@ def tile_multiheadedselfattention_pa_kernel(
             pq_sb[b] = raw.tile([P, NT, DQ], BF16, name="pq_sb%d" % b)
             nc.sync.dma_start(out=pq_sb[b][:], in_=pre_query[b].rearrange("(p t) c -> p t c", t=NT))
 
-        wv_raw = raw.tile([P, PASSES, 4, D], BF16, name="wv_raw")
+        wv_raw = {}
 
         def load_wv(g, half):
             cols = slice(half * S, (half + 1) * S)
+            wv_raw[g, half] = raw.tile([P, 4, S], BF16, name="wv_raw%d%d" % (g, half))
             for u in range(2):
                 rows = slice((2 * g + u) * 2 * P, (2 * g + u + 1) * 2 * P)
                 nc.sync.dma_start(
-                    out=wv_raw[:, g, 2 * u : 2 * u + 2, cols], in_=Wv[rows, cols].rearrange("(p e) n -> p e n", e=2)
+                    out=wv_raw[g, half][:, 2 * u : 2 * u + 2, :], in_=Wv[rows, cols].rearrange("(p e) n -> p e n", e=2)
                 )
 
         k_sb[0] = raw.tile([P, NT, D], BF16, name="k_sb0")
@@ -217,10 +218,10 @@ def tile_multiheadedselfattention_pa_kernel(
         wv_grouped = {}
 
         def weights_regroup(g, part):
-            cols = slice(part * WV_PART, (part + 1) * WV_PART)
+            half, first = divmod(part * WV_PART, S)
             grouped = stage.tile([P, WV_PART, 4], BF16, align_bytes=64, name="wv_grouped", bufs=4)
             out_cols = grouped[:].rearrange("p (c i) t -> p c t i", i=4)
-            in_cols = wv_raw[:, g, :, cols].rearrange("p t (c i) -> p c t i", i=4)
+            in_cols = wv_raw[g, half][:, :, first : first + WV_PART].rearrange("p t (c i) -> p c t i", i=4)
             nc.vector.tensor_copy(out=out_cols, in_=in_cols)
             wv_grouped[g, part] = grouped
 
@@ -286,20 +287,21 @@ def tile_multiheadedselfattention_pa_kernel(
 
         def values_add(b, h):
             cols = slice(h * P, (h + 1) * P)
-            v_grouped[b, h] = stage.tile([P, P, NT], BF16, align_bytes=64, name="v_grouped", bufs=3)
+            if h % 2 == 0:
+                v_grouped[b, h // 2] = stage.tile([P, 2, P, NT], BF16, align_bytes=64, name="v_grouped", bufs=2)
             nc.vector.tensor_tensor(
-                out=v_grouped[b, h][:],
+                out=v_grouped[b, h // 2][:, h % 2],
                 in0=v_bank[b, h][:].rearrange("p t c -> p c t"),
                 in1=small_bc[:, cols].unsqueeze(2).to_broadcast([P, P, NT]),
                 op=ALU.add,
             )
 
-        def values_quantise(b, h):
-            cols = slice(h * P, (h + 1) * P)
+        def values_quantise(b, pair):
+            cols = slice(pair * 2 * P, (pair + 1) * 2 * P)
             nc.vector.quantize_mx(
                 out=v_codes[:, b, cols].bitcast(FP8X4),
                 scales=v_scales[:, b, cols],
-                in_=v_grouped[b, h][:].rearrange("p c t -> p (c t)"),
+                in_=v_grouped[b, pair][:].rearrange("p h c t -> p (h c t)"),
             )
 
         gate = {}
@@ -366,6 +368,7 @@ def tile_multiheadedselfattention_pa_kernel(
         weight = {}
         h_bank = {}
         result = {}
+        ALL = range(HG)
 
         s_bank = {}
 
@@ -384,16 +387,19 @@ def tile_multiheadedselfattention_pa_kernel(
                 stop=True,
             )
 
+        highest = {}
+
         def maximum(i):
             n, hh = divmod(i, HG)
             if hh == 0:
+                highest[n] = small.tile([P, HG], F32, name="highest", bufs=3)
                 exp_bias[n] = small.tile([P, HG], F32, name="exp_bias", bufs=3)
                 e_bf[n] = stage.tile([P, HG, S], BF16, name="e_bf", bufs=3)
                 row_sum[n] = small.tile([P, HG], F32, name="row_sum", bufs=4)
-            products = stage.tile([P, S], BF16, bufs=2, name="products")
-            nc.vector.tensor_scalar(
-                out=products[:], in0=s_bank[i][:], scalar1=-SCALE, scalar2=None, op0=ALU.mult, op1=ALU.min,
-                accum_out=exp_bias[n][:, hh : hh + 1],
+            nc.vector.tensor_reduce(out=highest[n][:, hh : hh + 1], in_=s_bank[i][:], axis=AX.X, op=ALU.max)
+            nc.gpsimd.tensor_scalar(
+                out=exp_bias[n][:, hh : hh + 1], in0=highest[n][:, hh : hh + 1], scalar1=-SCALE, scalar2=0.0,
+                op0=ALU.mult, op1=ALU.add,
             )
 
         def exponential(i):
@@ -449,22 +455,24 @@ def tile_multiheadedselfattention_pa_kernel(
                     op1=ALU.add,
                 )
 
-        def quantise_e(n):
-            e_codes[n] = stage.tile([P, W], U32, align_bytes=64, name="e_codes", bufs=LAG)
-            e_scales[n] = stage.tile([P, W], U8, align_bytes=64, name="e_scales", bufs=LAG)
+        def quantise_e(n, heads=ALL):
+            if heads[0] == 0:
+                e_codes[n] = stage.tile([P, W], U32, align_bytes=64, name="e_codes", bufs=LAG)
+                e_scales[n] = stage.tile([P, W], U8, align_bytes=64, name="e_scales", bufs=LAG)
+            cols = slice(heads[0] * P, (heads[-1] + 1) * P)
             nc.vector.quantize_mx(
-                out=e_codes[n][:].bitcast(FP8X4),
-                scales=e_scales[n][:],
-                in_=e_grouped[n][:].rearrange("p h i t -> p (h i t)"),
+                out=e_codes[n][:, cols].bitcast(FP8X4),
+                scales=e_scales[n][:, cols],
+                in_=e_grouped[n][:, heads[0] : heads[-1] + 1].rearrange("p h i t -> p (h i t)"),
             )
 
-        def e_times_v(n):
+        def e_times_v(n, heads=ALL):
             b, hg, it = units[n]
-            h_bank[n] = psum_c.tile([P, HG, P], F32, tag="c", name="h_bank")
-            for hh in range(HG):
+            h_bank[n, heads[0]] = psum_c.tile([P, HG, P], F32, tag="c", name="h_bank")
+            for hh in heads:
                 h = hg * HG + hh
                 nc.tensor.matmul_mx(
-                    out=h_bank[n][:, hh, :],
+                    out=h_bank[n, heads[0]][:, hh, :],
                     lhsT=e_codes[n][:, hh * P : (hh + 1) * P].bitcast(FP8X4),
                     lhsT_scale=e_scales[n][:, hh * P : (hh + 1) * P],
                     rhs=v_codes[:, b, h * P : (h + 1) * P].bitcast(FP8X4),
@@ -473,19 +481,22 @@ def tile_multiheadedselfattention_pa_kernel(
                     stop=True,
                 )
 
-        def blend(n):
+        def blend(n, heads=ALL):
             b, hg, it = units[n]
-            for hh in range(HG):
+            for hh in heads:
                 cols = slice(hh * P, (hh + 1) * P)
                 nc.vector.scalar_tensor_tensor(
                     out=result[n][:, cols],
-                    in0=h_bank[n][:, hh, :],
+                    in0=h_bank[n, heads[0]][:, hh, :],
                     scalar=weight[n][:, hh : hh + 1],
                     in1=result[n][:, cols],
                     op0=ALU.mult,
                     op1=ALU.add,
                 )
-            nc.sync.dma_start(out=out_view[b][:, it, hg * W : (hg + 1) * W], in_=result[n][:])
+            cols = slice(heads[0] * P, (heads[-1] + 1) * P)
+            nc.sync.dma_start(
+                out=out_view[b][:, it, hg * W + cols.start : hg * W + cols.stop], in_=result[n][:, cols]
+            )
 
         heads = [(b, h) for b in range(B) for h in range(H)]
         groups = [(b, hg) for b in range(B) for hg in range(H // HG)]
@@ -505,54 +516,67 @@ def tile_multiheadedselfattention_pa_kernel(
         for i, first in enumerate((D, 0, S)):
             at(1 + i, lambda first=first: small_copy(first), tensor=lambda first=first: small_spread(first))
         at(3, gate_scales)
+        last = len(units) - 1
         for n in range(len(units)):
             start = n * HG
-            at(start + 3, lambda n=n: group_e(n, 0), tensor=lambda n=n: transpose_e(n, 0))
-            at(start + 5, lambda n=n: group_e(n, 1), tensor=lambda n=n: transpose_e(n, 1))
-            at(start + 5, lambda n=n: invert_sums(n))
-            at(start + 6, lambda n=n: blend_rest(n))
-            at(start + 7, lambda n=n: quantise_e(n))
-            at(start + 9, lambda n=n: blend_weights(n))
+            at(start + 4, lambda n=n: group_e(n, 0), tensor=lambda n=n: transpose_e(n, 0))
+            at(start + 6, lambda n=n: group_e(n, 1), tensor=lambda n=n: transpose_e(n, 1))
+            at(start + 6, lambda n=n: invert_sums(n))
+            if n < last:
+                at(start + 7, lambda n=n: blend_rest(n))
+                at(start + 8, lambda n=n: blend_weights(n))
+                at(start + 8, lambda n=n: quantise_e(n))
+            else:
+                at(start + 6, lambda n=n: blend_rest(n))
+                at(start + 6, lambda n=n: blend_weights(n))
+                for half in range(2):
+                    at(start + 5 + 2 * half, lambda n=n, half=half: quantise_e(n, ALL[2 * half : 2 * half + 2]))
         for c in range(HG, len(heads)):
             b, h = heads[c]
             at((c - HG) * HG + 1, lambda b=b, h=h: copy_kq(b, h), tensor=lambda b=b, h=h: transpose_kq(b, h))
         for g, (b, hg) in enumerate(groups):
-            slot = g * NT * HG if g > 0 else 3
+            slot = g * NT * HG - 1 if g > 0 else 3
             if g > 0:
                 at(slot - 2 * HG, lambda b=b, hg=hg: key_terms(b, hg), tensor=lambda b=b, hg=hg: key_sums(b, hg))
             at(slot, lambda b=b, hg=hg: gates(b, hg), tensor=lambda b=b, hg=hg: pool_scores(b, hg))
             at(slot + 2, lambda b=b, hg=hg: sigmoids(b, hg))
-        for w in range(1, PASSES * WV_PARTS):
-            at(w - 1, lambda w=w: weights_regroup(w // WV_PARTS, w % WV_PARTS))
         for w in range(PASSES * WV_PARTS):
-            at(w + 1, lambda w=w: weights_quantise(w // WV_PARTS, w % WV_PARTS))
-        for b, slot, stride in ((0, 5, 1), (1, 10, 2)):
+            if w >= WV_PARTS:
+                at(2 * (w - WV_PARTS) + 1, lambda w=w: weights_regroup(w // WV_PARTS, w % WV_PARTS))
+            at(max(0, 2 * (w - WV_PARTS) + 4), lambda w=w: weights_quantise(w // WV_PARTS, w % WV_PARTS))
+        for b, slot in ((0, 4), (1, 10)):
             for t in range(NT):
-                at(
-                    slot + t * stride, lambda b=b, t=t: tokens_group(b, t),
-                    tensor=lambda b=b, t=t: tokens_transpose(b, t),
-                )
+                at(slot + t * (1 + b), lambda b=b, t=t: tokens_group(b, t), tensor=lambda b=b, t=t: tokens_transpose(b, t))
             for g in range(PASSES):
-                at(slot + (NT - 1) * stride + 1 + g, lambda b=b, g=g: tokens_quantise(b, g))
+                at(slot + NT * (1 + b) + g, lambda b=b, g=g: tokens_quantise(b, g))
         v_slot = {}
         for c, (b, h) in enumerate(heads):
             slot = 4 * HG + 2 * c if b == 0 else (4 + h) * HG + 4 * HG
             v_slot[b, h // HG] = slot + 1
             at(slot, lambda b=b, h=h: values_add(b, h), mx=lambda b=b, h=h: values_matmul(b, h))
-            at(slot + 1, lambda b=b, h=h: values_quantise(b, h))
+            if h % 2 == 1:
+                at(slot + 1, lambda b=b, h=h: values_quantise(b, h // 2))
         free_slot = 0
         for n in range(len(units)):
             b, hg, it = units[n]
-            slot = max(n * HG + 10, v_slot[b, hg] + 2, free_slot)
-            at(slot, lambda n=n: blend(n), mx=lambda n=n: e_times_v(n))
-            free_slot = slot + 2
+            if n < last:
+                slot = max(n * HG + 14, v_slot[b, hg] + 2, free_slot)
+                at(slot, lambda n=n: blend(n), mx=lambda n=n: e_times_v(n))
+                free_slot = slot + 1
+            else:
+                for half in range(2):
+                    at(
+                        max(n * HG + 7, free_slot) + half, lambda n=n, half=half: blend(n, ALL[2 * half : 2 * half + 2]),
+                        mx=lambda n=n, half=half: e_times_v(n, ALL[2 * half : 2 * half + 2]),
+                    )
         for b in range(B):
             at(15 + b * 29, lambda b=b: copy_tail(b))
 
         for h in range(HG):
             transpose_kq(0, h)
             copy_kq(0, h)
-        weights_regroup(0, 0)
+        for w in range(WV_PARTS):
+            weights_regroup(0, w)
         for i in range(2):
             scores(i)
         for i in range(max(plan) + 1):
@@ -560,7 +584,8 @@ def tile_multiheadedselfattention_pa_kernel(
                 work()
             if i < slots:
                 maximum(i)
-                exponential(i)
+            if 0 < i <= slots:
+                exponential(i - 1)
             for work in plan.get(i, []):
                 work()
             if i + 2 < slots:

@@ -372,34 +372,35 @@ def tile_multiheadedselfattention_pa_kernel(
 
         s_bank = {}
 
-        def scores(i):
-            n, hh = divmod(i, HG)
-            b, hg, it = units[n]
-            h = hg * HG + hh
-            s_bank[i] = psum_s.tile([P, S], F32, tag="s", name="s_bank")
-            for t in range(NT):
+        def scores(first):
+            for i in (first, first + 1):
+                b = units[i // HG][0]
+                s_bank[i] = psum_s.tile([P, S], F32, tag="s", name="s_bank")
+                for t in range(NT):
+                    nc.tensor.matmul(
+                        out=s_bank[i][:, t * P : (t + 1) * P], lhsT=mask_bias_t[:, b * NT + t, :], rhs=ident_f32[:],
+                        is_transpose=True, start=(t == 0), stop=False,
+                    )
+            for i in (first, first + 1):
+                n, hh = divmod(i, HG)
+                b, hg, it = units[n]
+                h = hg * HG + hh
                 nc.tensor.matmul(
-                    out=s_bank[i][:, t * P : (t + 1) * P], lhsT=mask_bias_t[:, b * NT + t, :], rhs=ident_f32[:],
-                    is_transpose=True, start=(t == 0), stop=False,
+                    out=s_bank[i][:], lhsT=kqT[b][:, h, 1, it * P : (it + 1) * P], rhs=kqT[b][:, h, 0, :], start=False,
+                    stop=True,
                 )
-            nc.tensor.matmul(
-                out=s_bank[i][:], lhsT=kqT[b][:, h, 1, it * P : (it + 1) * P], rhs=kqT[b][:, h, 0, :], start=False,
-                stop=True,
-            )
-
-        highest = {}
 
         def maximum(i):
             n, hh = divmod(i, HG)
             if hh == 0:
-                highest[n] = small.tile([P, HG], F32, name="highest", bufs=3)
                 exp_bias[n] = small.tile([P, HG], F32, name="exp_bias", bufs=3)
                 e_bf[n] = stage.tile([P, HG, S], BF16, name="e_bf", bufs=3)
-                row_sum[n] = small.tile([P, HG], F32, name="row_sum", bufs=4)
-            nc.vector.tensor_reduce(out=highest[n][:, hh : hh + 1], in_=s_bank[i][:], axis=AX.X, op=ALU.max)
-            nc.gpsimd.tensor_scalar(
-                out=exp_bias[n][:, hh : hh + 1], in0=highest[n][:, hh : hh + 1], scalar1=-SCALE, scalar2=0.0,
-                op0=ALU.mult, op1=ALU.add,
+                if n % 2 == 0:
+                    row_sum[n // 2] = small.tile([P, 2, HG], F32, name="row_sum", bufs=3)
+            products = stage.tile([P, S], BF16, bufs=2, name="products")
+            nc.vector.tensor_scalar(
+                out=products[:], in0=s_bank[i][:], scalar1=-SCALE, scalar2=None, op0=ALU.mult, op1=ALU.min,
+                accum_out=exp_bias[n][:, hh : hh + 1],
             )
 
         def exponential(i):
@@ -410,7 +411,7 @@ def tile_multiheadedselfattention_pa_kernel(
                 func=ACT.Exp,
                 bias=exp_bias[n][:, hh : hh + 1],
                 scale=SCALE,
-                accum_out=row_sum[n][:, hh : hh + 1],
+                accum_out=row_sum[n // 2][:, n % 2, hh : hh + 1],
             )
 
         e_bank = {}
@@ -432,14 +433,17 @@ def tile_multiheadedselfattention_pa_kernel(
                 in_=e_bank[n, pair][:].rearrange("p h u i -> p h i u"),
             )
 
-        def invert_sums(n):
-            inv_sum[n] = small.tile([P, HG], F32, name="inv_sum")
-            nc.vector.reciprocal(out=inv_sum[n][:], in_=row_sum[n][:])
+        def invert_sums(first, count):
+            inverse = small.tile([P, 2, HG], F32, name="inverse", bufs=3)
+            which = slice(first % 2, first % 2 + count)
+            nc.vector.reciprocal(out=inverse[:, which, :], in_=row_sum[first // 2][:, which, :])
+            for n in range(first, first + count):
+                inv_sum[n] = inverse[:, n % 2, :]
 
         def blend_weights(n):
             b, hg, it = units[n]
             weight[n] = small.tile([P, HG], F32, name="weight", bufs=LAG)
-            nc.gpsimd.tensor_tensor(out=weight[n][:], in0=inv_sum[n][:], in1=gate[b, hg][:, it, :], op=ALU.mult)
+            nc.gpsimd.tensor_tensor(out=weight[n][:], in0=inv_sum[n], in1=gate[b, hg][:, it, :], op=ALU.mult)
 
         def blend_rest(n):
             b, hg, it = units[n]
@@ -512,46 +516,53 @@ def tile_multiheadedselfattention_pa_kernel(
             if mx is not None:
                 mx_plan.setdefault(slot, []).append(mx)
 
-        at(1, lambda: key_terms(0, 0), tensor=lambda: key_sums(0, 0))
+        at(2, lambda: key_terms(0, 0), tensor=lambda: key_sums(0, 0))
         for i, first in enumerate((D, 0, S)):
             at(1 + i, lambda first=first: small_copy(first), tensor=lambda first=first: small_spread(first))
         at(3, gate_scales)
         last = len(units) - 1
         for n in range(len(units)):
             start = n * HG
-            at(start + 4, lambda n=n: group_e(n, 0), tensor=lambda n=n: transpose_e(n, 0))
+            at(start + 5, lambda n=n: group_e(n, 0), tensor=lambda n=n: transpose_e(n, 0))
             at(start + 6, lambda n=n: group_e(n, 1), tensor=lambda n=n: transpose_e(n, 1))
-            at(start + 6, lambda n=n: invert_sums(n))
             if n < last:
-                at(start + 7, lambda n=n: blend_rest(n))
-                at(start + 8, lambda n=n: blend_weights(n))
-                at(start + 8, lambda n=n: quantise_e(n))
+                at(start + 8, lambda n=n: blend_rest(n))
+                at(start + 9, lambda n=n: quantise_e(n))
             else:
                 at(start + 6, lambda n=n: blend_rest(n))
-                at(start + 6, lambda n=n: blend_weights(n))
                 for half in range(2):
-                    at(start + 5 + 2 * half, lambda n=n, half=half: quantise_e(n, ALL[2 * half : 2 * half + 2]))
+                    at(start + 6 + half, lambda n=n, half=half: quantise_e(n, ALL[2 * half : 2 * half + 2]))
+            if n >= last - 1:
+                at(start + 5, lambda n=n: invert_sums(n, 1))
+                at(start + 6, lambda n=n: blend_weights(n))
+            elif n % 2 == 1:
+                at(start + 7, lambda n=n: invert_sums(n - 1, 2))
+                for unit in (n - 1, n):
+                    at(start + 9, lambda unit=unit: blend_weights(unit))
         for c in range(HG, len(heads)):
             b, h = heads[c]
             at((c - HG) * HG + 1, lambda b=b, h=h: copy_kq(b, h), tensor=lambda b=b, h=h: transpose_kq(b, h))
         for g, (b, hg) in enumerate(groups):
-            slot = g * NT * HG - 1 if g > 0 else 3
+            slot = g * NT * HG if g > 0 else 5
             if g > 0:
                 at(slot - 2 * HG, lambda b=b, hg=hg: key_terms(b, hg), tensor=lambda b=b, hg=hg: key_sums(b, hg))
             at(slot, lambda b=b, hg=hg: gates(b, hg), tensor=lambda b=b, hg=hg: pool_scores(b, hg))
             at(slot + 2, lambda b=b, hg=hg: sigmoids(b, hg))
+        for w in range(WV_PARTS):
+            at(2 + w, lambda w=w: weights_regroup(1, w))
         for w in range(PASSES * WV_PARTS):
-            if w >= WV_PARTS:
-                at(2 * (w - WV_PARTS) + 1, lambda w=w: weights_regroup(w // WV_PARTS, w % WV_PARTS))
-            at(max(0, 2 * (w - WV_PARTS) + 4), lambda w=w: weights_quantise(w // WV_PARTS, w % WV_PARTS))
+            at(w, lambda w=w: weights_quantise(w // WV_PARTS, w % WV_PARTS))
         for b, slot in ((0, 4), (1, 10)):
             for t in range(NT):
-                at(slot + t * (1 + b), lambda b=b, t=t: tokens_group(b, t), tensor=lambda b=b, t=t: tokens_transpose(b, t))
+                at(
+                    slot + t * (1 + b), lambda b=b, t=t: tokens_group(b, t),
+                    tensor=lambda b=b, t=t: tokens_transpose(b, t),
+                )
             for g in range(PASSES):
-                at(slot + NT * (1 + b) + g, lambda b=b, g=g: tokens_quantise(b, g))
+                at(slot + (NT - 1) * (1 + b) + 1 + g, lambda b=b, g=g: tokens_quantise(b, g))
         v_slot = {}
         for c, (b, h) in enumerate(heads):
-            slot = 4 * HG + 2 * c if b == 0 else (4 + h) * HG + 4 * HG
+            slot = 12 + c * 5 // 2 if c < HG else 22 + (c - HG) * 7 // 2
             v_slot[b, h // HG] = slot + 1
             at(slot, lambda b=b, h=h: values_add(b, h), mx=lambda b=b, h=h: values_matmul(b, h))
             if h % 2 == 1:
@@ -560,9 +571,10 @@ def tile_multiheadedselfattention_pa_kernel(
         for n in range(len(units)):
             b, hg, it = units[n]
             if n < last:
-                slot = max(n * HG + 14, v_slot[b, hg] + 2, free_slot)
+                ready = n * HG + (13 if n % 2 == 0 else 9) + 1
+                slot = max(ready, v_slot[b, hg] + 2, free_slot)
                 at(slot, lambda n=n: blend(n), mx=lambda n=n: e_times_v(n))
-                free_slot = slot + 1
+                free_slot = slot + 3
             else:
                 for half in range(2):
                     at(
@@ -577,8 +589,7 @@ def tile_multiheadedselfattention_pa_kernel(
             copy_kq(0, h)
         for w in range(WV_PARTS):
             weights_regroup(0, w)
-        for i in range(2):
-            scores(i)
+        scores(0)
         for i in range(max(plan) + 1):
             for work in mx_plan.get(i + 1, []) + tensor_plan.get(i + 1, []):
                 work()
@@ -588,5 +599,5 @@ def tile_multiheadedselfattention_pa_kernel(
                 exponential(i - 1)
             for work in plan.get(i, []):
                 work()
-            if i + 2 < slots:
+            if i % 2 == 0 and i + 2 < slots:
                 scores(i + 2)

@@ -69,15 +69,24 @@ def tile_multiheadedselfattention_pa_kernel(
         pvk_sb = {}
         out_view = [out[b].rearrange("(p t) c -> p t c", t=NT) for b in range(B)]
 
-        def load_k(b, hg):
-            cols = slice(hg * W, (hg + 1) * W)
-            nc.sync.dma_start(out=k_sb[b][:, :, cols], in_=k[b].rearrange("(t p) d -> p t d", p=P)[:, :, cols])
+        def load_k(b, hg, width):
+            k_sb[b, hg] = raw.tile([P, NT, width], BF16, name="k_sb%d%d" % (b, hg))
+            nc.sync.dma_start(
+                out=k_sb[b, hg][:], in_=k[b].rearrange("(t p) d -> p t d", p=P)[:, :, hg * W : hg * W + width]
+            )
 
-        def load_q(b, hg):
-            cols = slice(hg * W, (hg + 1) * W)
-            nc.sync.dma_start(out=q_sb[b][:, :, cols], in_=q[b].rearrange("(p t) d -> p t d", t=NT)[:, :, cols])
+        def load_q(b, hg, width):
+            q_sb[b, hg] = raw.tile([P, NT, width], BF16, name="q_sb%d%d" % (b, hg))
+            nc.sync.dma_start(
+                out=q_sb[b, hg][:], in_=q[b].rearrange("(p t) d -> p t d", t=NT)[:, :, hg * W : hg * W + width]
+            )
+
+        def of_head(tiles, b, h):
+            tile, first = (tiles[0, h // HG], h % HG * P) if b == 0 else (tiles[1, 0], h * P)
+            return tile[:, :, first : first + P]
 
         def load_pvk(b):
+            pvk_sb[b] = raw.tile([P, NT, D], BF16, name="pvk_sb%d" % b)
             nc.sync.dma_start(
                 out=pvk_sb[b][:].rearrange("p (u e) d -> p u (e d)", e=2),
                 in_=pre_value_key[b].rearrange("(u p e) d -> p u (e d)", u=2, e=2),
@@ -89,21 +98,16 @@ def tile_multiheadedselfattention_pa_kernel(
 
         wv_raw = {}
 
-        def load_wv(g, half):
-            cols = slice(half * S, (half + 1) * S)
-            wv_raw[g, half] = raw.tile([P, 4, S], BF16, name="wv_raw%d%d" % (g, half))
-            for u in range(2):
-                rows = slice((2 * g + u) * 2 * P, (2 * g + u + 1) * 2 * P)
-                nc.sync.dma_start(
-                    out=wv_raw[g, half][:, 2 * u : 2 * u + 2, :], in_=Wv[rows, cols].rearrange("(p e) n -> p e n", e=2)
-                )
+        def load_wv(g):
+            wv_raw[g] = raw.tile([P, 4, D], BF16, name="wv_raw%d" % g)
+            nc.sync.dma_start(
+                out=wv_raw[g][:].rearrange("p (u e) n -> p u (e n)", e=2),
+                in_=Wv[g * 4 * P : (g + 1) * 4 * P, :].rearrange("(u p e) n -> p u (e n)", u=2, e=2),
+            )
 
-        k_sb[0] = raw.tile([P, NT, D], BF16, name="k_sb0")
-        q_sb[0] = raw.tile([P, NT, D], BF16, name="q_sb0")
-        load_wv(0, 0)
-        load_k(0, 0)
-        load_q(0, 0)
-        load_wv(0, 1)
+        load_k(0, 0, W)
+        load_q(0, 0, W)
+        load_wv(0)
         for first, width, vector in (
             (BV0, D, bv.rearrange("(o n) -> o n", o=1)),
             (GAIN0, H, overall_gain.rearrange("a h b c -> a (h b c)")),
@@ -111,21 +115,14 @@ def tile_multiheadedselfattention_pa_kernel(
             (COUNT0, B, value_key_counts.rearrange("(o n) -> o n", o=1)),
         ):
             nc.sync.dma_start(out=small_row[0:1, first : first + width], in_=vector)
-        load_k(0, 1)
-        load_q(0, 1)
-        load_wv(1, 0)
-        load_wv(1, 1)
-        pvk_sb[0] = raw.tile([P, NT, D], BF16, name="pvk_sb0")
+        load_k(0, 1, W)
+        load_q(0, 1, W)
+        load_wv(1)
         load_pvk(0)
-        load_pq(0)
-
-        k_sb[1] = raw.tile([P, NT, D], BF16, name="k_sb1")
-        q_sb[1] = raw.tile([P, NT, D], BF16, name="q_sb1")
-        for hg in range(2):
-            load_k(1, hg)
-            load_q(1, hg)
-        pvk_sb[1] = raw.tile([P, NT, D], BF16, name="pvk_sb1")
         load_pvk(1)
+        load_q(1, 0, D)
+        load_pq(0)
+        load_k(1, 0, D)
         load_pq(1)
 
         ident_bf = const.tile([P, P], BF16)
@@ -159,7 +156,7 @@ def tile_multiheadedselfattention_pa_kernel(
                 h = hg * HG + hh
                 for t in range(NT):
                     nc.tensor.matmul(
-                        out=ks_bank[b, hg][:, hh : hh + 1], lhsT=k_sb[b][:, t, h * P : (h + 1) * P],
+                        out=ks_bank[b, hg][:, hh : hh + 1], lhsT=of_head(k_sb, b, h)[:, t, :],
                         rhs=mask_t[:, b * NT + t : b * NT + t + 1], start=(t == 0), stop=(t == NT - 1),
                     )
 
@@ -175,11 +172,10 @@ def tile_multiheadedselfattention_pa_kernel(
         kq_bank = {}
 
         def transpose_kq(b, h):
-            cols = slice(h * P, (h + 1) * P)
             kq_bank[b, h] = psum_c.tile([P, 2, NT, P], BF16, tag="c", name="kq_bank")
-            for i, tokens in enumerate((k_sb[b], q_sb[b])):
+            for i, tokens in enumerate((of_head(k_sb, b, h), of_head(q_sb, b, h))):
                 for t in range(NT):
-                    nc.tensor.transpose(kq_bank[b, h][:, i, t, :], tokens[:, t, cols], ident_bf[:])
+                    nc.tensor.transpose(kq_bank[b, h][:, i, t, :], tokens[:, t, :], ident_bf[:])
 
         def copy_kq(b, h):
             nc.scalar.copy(out=kqT[b][:, h, :, :], in_=kq_bank[b, h][:].rearrange("p i t r -> p i (t r)"))
@@ -218,10 +214,10 @@ def tile_multiheadedselfattention_pa_kernel(
         wv_grouped = {}
 
         def weights_regroup(g, part):
-            half, first = divmod(part * WV_PART, S)
+            first = part * WV_PART
             grouped = stage.tile([P, WV_PART, 4], BF16, align_bytes=64, name="wv_grouped", bufs=4)
             out_cols = grouped[:].rearrange("p (c i) t -> p c t i", i=4)
-            in_cols = wv_raw[g, half][:, :, first : first + WV_PART].rearrange("p t (c i) -> p c t i", i=4)
+            in_cols = wv_raw[g][:, :, first : first + WV_PART].rearrange("p t (c i) -> p c t i", i=4)
             nc.vector.tensor_copy(out=out_cols, in_=in_cols)
             wv_grouped[g, part] = grouped
 
@@ -516,22 +512,15 @@ def tile_multiheadedselfattention_pa_kernel(
             if mx is not None:
                 mx_plan.setdefault(slot, []).append(mx)
 
-        at(2, lambda: key_terms(0, 0), tensor=lambda: key_sums(0, 0))
+        at(1, lambda: key_terms(0, 0), tensor=lambda: key_sums(0, 0))
         for i, first in enumerate((D, 0, S)):
             at(1 + i, lambda first=first: small_copy(first), tensor=lambda first=first: small_spread(first))
         at(3, gate_scales)
         last = len(units) - 1
         for n in range(len(units)):
             start = n * HG
-            at(start + 5, lambda n=n: group_e(n, 0), tensor=lambda n=n: transpose_e(n, 0))
+            at(start + 4, lambda n=n: group_e(n, 0), tensor=lambda n=n: transpose_e(n, 0))
             at(start + 6, lambda n=n: group_e(n, 1), tensor=lambda n=n: transpose_e(n, 1))
-            if n < last:
-                at(start + 8, lambda n=n: blend_rest(n))
-                at(start + 9, lambda n=n: quantise_e(n))
-            else:
-                at(start + 6, lambda n=n: blend_rest(n))
-                for half in range(2):
-                    at(start + 6 + half, lambda n=n, half=half: quantise_e(n, ALL[2 * half : 2 * half + 2]))
             if n >= last - 1:
                 at(start + 5, lambda n=n: invert_sums(n, 1))
                 at(start + 6, lambda n=n: blend_weights(n))
@@ -539,30 +528,34 @@ def tile_multiheadedselfattention_pa_kernel(
                 at(start + 7, lambda n=n: invert_sums(n - 1, 2))
                 for unit in (n - 1, n):
                     at(start + 9, lambda unit=unit: blend_weights(unit))
+            if n < last:
+                at(start + 9, lambda n=n: blend_rest(n))
+                at(start + 7, lambda n=n: quantise_e(n))
+            else:
+                at(start + 3, lambda n=n: blend_rest(n))
+                for half in range(2):
+                    at(start + 5 + 2 * half, lambda n=n, half=half: quantise_e(n, ALL[2 * half : 2 * half + 2]))
         for c in range(HG, len(heads)):
             b, h = heads[c]
-            at((c - HG) * HG + 1, lambda b=b, h=h: copy_kq(b, h), tensor=lambda b=b, h=h: transpose_kq(b, h))
+            at((c - HG) * HG + 2, lambda b=b, h=h: copy_kq(b, h), tensor=lambda b=b, h=h: transpose_kq(b, h))
         for g, (b, hg) in enumerate(groups):
             slot = g * NT * HG if g > 0 else 5
             if g > 0:
-                at(slot - 2 * HG, lambda b=b, hg=hg: key_terms(b, hg), tensor=lambda b=b, hg=hg: key_sums(b, hg))
+                at(slot - 2 * HG + 1, lambda b=b, hg=hg: key_terms(b, hg), tensor=lambda b=b, hg=hg: key_sums(b, hg))
             at(slot, lambda b=b, hg=hg: gates(b, hg), tensor=lambda b=b, hg=hg: pool_scores(b, hg))
             at(slot + 2, lambda b=b, hg=hg: sigmoids(b, hg))
         for w in range(WV_PARTS):
-            at(2 + w, lambda w=w: weights_regroup(1, w))
+            at(3 + w, lambda w=w: weights_regroup(1, w))
         for w in range(PASSES * WV_PARTS):
             at(w, lambda w=w: weights_quantise(w // WV_PARTS, w % WV_PARTS))
-        for b, slot in ((0, 4), (1, 10)):
+        for b, slot in ((0, 5), (1, 12)):
             for t in range(NT):
-                at(
-                    slot + t * (1 + b), lambda b=b, t=t: tokens_group(b, t),
-                    tensor=lambda b=b, t=t: tokens_transpose(b, t),
-                )
+                at(slot + t, lambda b=b, t=t: tokens_group(b, t), tensor=lambda b=b, t=t: tokens_transpose(b, t))
             for g in range(PASSES):
-                at(slot + (NT - 1) * (1 + b) + 1 + g, lambda b=b, g=g: tokens_quantise(b, g))
+                at(slot + NT + g, lambda b=b, g=g: tokens_quantise(b, g))
         v_slot = {}
         for c, (b, h) in enumerate(heads):
-            slot = 12 + c * 5 // 2 if c < HG else 22 + (c - HG) * 7 // 2
+            slot = 12 + c * 5 // 2 if c < HG else 22 + (c - HG) * 2
             v_slot[b, h // HG] = slot + 1
             at(slot, lambda b=b, h=h: values_add(b, h), mx=lambda b=b, h=h: values_matmul(b, h))
             if h % 2 == 1:
@@ -571,10 +564,10 @@ def tile_multiheadedselfattention_pa_kernel(
         for n in range(len(units)):
             b, hg, it = units[n]
             if n < last:
-                ready = n * HG + (13 if n % 2 == 0 else 9) + 1
-                slot = max(ready, v_slot[b, hg] + 2, free_slot)
+                weighed = n * HG + 10 + (HG if n % 2 == 0 and n < last - 1 else 0)
+                slot = max(weighed, v_slot[b, hg] + 2, free_slot)
                 at(slot, lambda n=n: blend(n), mx=lambda n=n: e_times_v(n))
-                free_slot = slot + 3
+                free_slot = slot + 2
             else:
                 for half in range(2):
                     at(
@@ -582,7 +575,7 @@ def tile_multiheadedselfattention_pa_kernel(
                         mx=lambda n=n, half=half: e_times_v(n, ALL[2 * half : 2 * half + 2]),
                     )
         for b in range(B):
-            at(15 + b * 29, lambda b=b: copy_tail(b))
+            at(24 + b * 20, lambda b=b: copy_tail(b))
 
         for h in range(HG):
             transpose_kq(0, h)

@@ -120,9 +120,9 @@ def tile_multiheadedselfattention_pa_kernel(
         load_wv(1)
         load_pvk(0)
         load_pvk(1)
-        load_q(1, 0, D)
         load_pq(0)
         load_k(1, 0, D)
+        load_q(1, 0, D)
         load_pq(1)
 
         ident_bf = const.tile([P, P], BF16)
@@ -178,7 +178,8 @@ def tile_multiheadedselfattention_pa_kernel(
                     nc.tensor.transpose(kq_bank[b, h][:, i, t, :], tokens[:, t, :], ident_bf[:])
 
         def copy_kq(b, h):
-            nc.scalar.copy(out=kqT[b][:, h, :, :], in_=kq_bank[b, h][:].rearrange("p i t r -> p i (t r)"))
+            copy = nc.vector.tensor_copy if (b, h) == (0, 1) else nc.scalar.copy
+            copy(out=kqT[b][:, h, :, :], in_=kq_bank[b, h][:].rearrange("p i t r -> p i (t r)"))
 
         small_bc = const.tile([P, SMALL_W], F32)
         small_bank = {}
@@ -514,8 +515,8 @@ def tile_multiheadedselfattention_pa_kernel(
 
         at(1, lambda: key_terms(0, 0), tensor=lambda: key_sums(0, 0))
         for i, first in enumerate((D, 0, S)):
-            at(1 + i, lambda first=first: small_copy(first), tensor=lambda first=first: small_spread(first))
-        at(3, gate_scales)
+            at(i, lambda first=first: small_copy(first), tensor=lambda first=first: small_spread(first))
+        at(2, gate_scales)
         last = len(units) - 1
         for n in range(len(units)):
             start = n * HG
@@ -527,10 +528,10 @@ def tile_multiheadedselfattention_pa_kernel(
             elif n % 2 == 1:
                 at(start + 7, lambda n=n: invert_sums(n - 1, 2))
                 for unit in (n - 1, n):
-                    at(start + 9, lambda unit=unit: blend_weights(unit))
+                    at(start + 10, lambda unit=unit: blend_weights(unit))
             if n < last:
-                at(start + 9, lambda n=n: blend_rest(n))
-                at(start + 7, lambda n=n: quantise_e(n))
+                at(start + 7, lambda n=n: blend_rest(n))
+                at(start + 9, lambda n=n: quantise_e(n))
             else:
                 at(start + 3, lambda n=n: blend_rest(n))
                 for half in range(2):
@@ -539,23 +540,27 @@ def tile_multiheadedselfattention_pa_kernel(
             b, h = heads[c]
             at((c - HG) * HG + 2, lambda b=b, h=h: copy_kq(b, h), tensor=lambda b=b, h=h: transpose_kq(b, h))
         for g, (b, hg) in enumerate(groups):
-            slot = g * NT * HG if g > 0 else 5
+            slot = g * NT * HG + 1 if g > 0 else 4
             if g > 0:
-                at(slot - 2 * HG + 1, lambda b=b, hg=hg: key_terms(b, hg), tensor=lambda b=b, hg=hg: key_sums(b, hg))
+                at(slot - 2 * HG, lambda b=b, hg=hg: key_terms(b, hg), tensor=lambda b=b, hg=hg: key_sums(b, hg))
             at(slot, lambda b=b, hg=hg: gates(b, hg), tensor=lambda b=b, hg=hg: pool_scores(b, hg))
             at(slot + 2, lambda b=b, hg=hg: sigmoids(b, hg))
-        for w in range(WV_PARTS):
-            at(3 + w, lambda w=w: weights_regroup(1, w))
-        for w in range(PASSES * WV_PARTS):
-            at(w, lambda w=w: weights_quantise(w // WV_PARTS, w % WV_PARTS))
-        for b, slot in ((0, 5), (1, 12)):
+        for w in range(1, PASSES * WV_PARTS):
+            slot = 2 + (w - 2) * 3 // 2
+            if w >= 2:
+                at(slot, lambda w=w: weights_regroup(w // WV_PARTS, w % WV_PARTS))
+            at(slot + 3, lambda w=w: weights_quantise(w // WV_PARTS, w % WV_PARTS))
+        for b, slot, stride in ((0, 6, 1), (1, 12, 3)):
             for t in range(NT):
-                at(slot + t, lambda b=b, t=t: tokens_group(b, t), tensor=lambda b=b, t=t: tokens_transpose(b, t))
+                at(
+                    slot + t * stride, lambda b=b, t=t: tokens_group(b, t),
+                    tensor=lambda b=b, t=t: tokens_transpose(b, t),
+                )
             for g in range(PASSES):
-                at(slot + NT + g, lambda b=b, g=g: tokens_quantise(b, g))
+                at(slot + (NT - 1) * stride + 1 + g, lambda b=b, g=g: tokens_quantise(b, g))
         v_slot = {}
         for c, (b, h) in enumerate(heads):
-            slot = 12 + c * 5 // 2 if c < HG else 22 + (c - HG) * 2
+            slot = 14 + 3 * c
             v_slot[b, h // HG] = slot + 1
             at(slot, lambda b=b, h=h: values_add(b, h), mx=lambda b=b, h=h: values_matmul(b, h))
             if h % 2 == 1:
@@ -565,9 +570,9 @@ def tile_multiheadedselfattention_pa_kernel(
             b, hg, it = units[n]
             if n < last:
                 weighed = n * HG + 10 + (HG if n % 2 == 0 and n < last - 1 else 0)
-                slot = max(weighed, v_slot[b, hg] + 2, free_slot)
+                slot = max(weighed + 1, v_slot[b, hg] + 2, free_slot)
                 at(slot, lambda n=n: blend(n), mx=lambda n=n: e_times_v(n))
-                free_slot = slot + 2
+                free_slot = slot + 3
             else:
                 for half in range(2):
                     at(
@@ -575,14 +580,17 @@ def tile_multiheadedselfattention_pa_kernel(
                         mx=lambda n=n, half=half: e_times_v(n, ALL[2 * half : 2 * half + 2]),
                     )
         for b in range(B):
-            at(24 + b * 20, lambda b=b: copy_tail(b))
+            at(15 + b * 29, lambda b=b: copy_tail(b))
 
         for h in range(HG):
             transpose_kq(0, h)
             copy_kq(0, h)
-        for w in range(WV_PARTS):
+        for w in range(2):
             weights_regroup(0, w)
+        weights_quantise(0, 0)
         scores(0)
+        for work in tensor_plan[0]:
+            work()
         for i in range(max(plan) + 1):
             for work in mx_plan.get(i + 1, []) + tensor_plan.get(i + 1, []):
                 work()

@@ -216,7 +216,7 @@ def tile_multiheadedselfattention_pa_kernel(
 
         def weights_regroup(g, part):
             first = part * WV_PART
-            grouped = stage.tile([P, WV_PART, 4], BF16, align_bytes=64, name="wv_grouped", bufs=4)
+            grouped = stage.tile([P, WV_PART, 4], BF16, align_bytes=64, name="wv_grouped", bufs=3)
             out_cols = grouped[:].rearrange("p (c i) t -> p c t i", i=4)
             in_cols = wv_raw[g][:, :, first : first + WV_PART].rearrange("p t (c i) -> p c t i", i=4)
             nc.vector.tensor_copy(out=out_cols, in_=in_cols)
@@ -368,6 +368,7 @@ def tile_multiheadedselfattention_pa_kernel(
         ALL = range(HG)
 
         s_bank = {}
+        products = {}
 
         def scores(first):
             for i in (first, first + 1):
@@ -394,9 +395,9 @@ def tile_multiheadedselfattention_pa_kernel(
                 e_bf[n] = stage.tile([P, HG, S], BF16, name="e_bf", bufs=3)
                 if n % 2 == 0:
                     row_sum[n // 2] = small.tile([P, 2, HG], F32, name="row_sum", bufs=3)
-            products = stage.tile([P, S], BF16, bufs=2, name="products")
+            products[i] = stage.tile([P, S], F32, bufs=3, name="products")
             nc.vector.tensor_scalar(
-                out=products[:], in0=s_bank[i][:], scalar1=-SCALE, scalar2=None, op0=ALU.mult, op1=ALU.min,
+                out=products[i][:], in0=s_bank[i][:], scalar1=-SCALE, scalar2=None, op0=ALU.mult, op1=ALU.min,
                 accum_out=exp_bias[n][:, hh : hh + 1],
             )
 
@@ -404,10 +405,10 @@ def tile_multiheadedselfattention_pa_kernel(
             n, hh = divmod(i, HG)
             nc.scalar.activation(
                 out=e_bf[n][:, hh, :],
-                in_=s_bank[i][:],
+                in_=products[i][:],
                 func=ACT.Exp,
                 bias=exp_bias[n][:, hh : hh + 1],
-                scale=SCALE,
+                scale=-1.0,
                 accum_out=row_sum[n // 2][:, n % 2, hh : hh + 1],
             )
 

@@ -380,6 +380,9 @@ def tile_multiheadedselfattention_pa_kernel(
                         is_transpose=True, start=(t == 0), stop=False,
                     )
             for i in (first, first + 1):
+                if i > first:
+                    for work in mx_plan.get(first, []) + mx_plan.get(first + 1, []):
+                        work()
                 n, hh = divmod(i, HG)
                 b, hg, it = units[n]
                 h = hg * HG + hh
@@ -593,7 +596,8 @@ def tile_multiheadedselfattention_pa_kernel(
         for work in tensor_plan[0]:
             work()
         for i in range(max(plan) + 1):
-            for work in mx_plan.get(i + 1, []) + tensor_plan.get(i + 1, []):
+            late = mx_plan.get(i + 1, []) if i + 1 >= slots else []
+            for work in late + tensor_plan.get(i + 1, []):
                 work()
             if i < slots:
                 maximum(i)

@@ -419,7 +419,8 @@ def tile_multiheadedselfattention_pa_kernel(
 
         def transpose_e(n, pair):
             e_words = e_bf[n][:].bitcast(F32)
-            e_bank[n, pair] = psum_b.tile([P, 2, 2, P], F32, tag="b", name="e_bank")
+            pool, tag = (psum_s, "s") if (n, pair) == (len(units) - 1, 1) else (psum_b, "b")
+            e_bank[n, pair] = pool.tile([P, 2, 2, P], F32, tag=tag, name="e_bank")
             for h2 in range(2):
                 for u in range(2):
                     nc.tensor.transpose(
@@ -534,7 +535,7 @@ def tile_multiheadedselfattention_pa_kernel(
                 for unit in (n - 1, n):
                     at(start + 10, lambda unit=unit: blend_weights(unit))
             if n < last:
-                at(start + 7, lambda n=n: blend_rest(n))
+                at(max(start + 9, 14), lambda n=n: blend_rest(n))
                 at(start + 9, lambda n=n: quantise_e(n))
             else:
                 at(start + 3, lambda n=n: blend_rest(n))

@@ -55,6 +55,8 @@ def tile_multiheadedselfattention_pa_kernel(
         psum_b = ctx.enter_context(tc.psum_pool(name="psum_b", bufs=1))
         psum_c = ctx.enter_context(tc.psum_pool(name="psum_c", bufs=3))
 
+        ones_f32 = const.tile([P, P], F32)
+        nc.vector.memset(ones_f32[:], 1.0)
         mask_rows = const.tile([P, P], BF16)
         nc.vector.memset(mask_rows[:], 0.0)
         nc.sync.dma_start(
@@ -134,6 +136,13 @@ def tile_multiheadedselfattention_pa_kernel(
         warm = const.tile([P, 1], F32)
         nc.scalar.activation(out=warm[:], in_=ones_bf[:, 0:1], func=ACT.Exp)
 
+        warm_bank = psum_b.tile([P, P], F32, tag="b", name="warm_bank")
+
+        def keep_warm(count):
+            for w in range(count):
+                nc.tensor.matmul(out=warm_bank[:], lhsT=ones_f32[:], rhs=ones_f32[:], start=True, stop=True)
+
+        keep_warm(8)
         mask_ps = psum_c.tile([P, P], BF16, tag="c", name="mask_ps")
         nc.tensor.transpose(mask_ps[:], mask_rows[:], ident_bf[:])
         mask_t = const.tile([P, B * NT], BF16)
@@ -162,7 +171,7 @@ def tile_multiheadedselfattention_pa_kernel(
 
         def key_terms(b, hg):
             ks[b, hg] = small.tile([P, HG], F32, name="ks")
-            nc.vector.tensor_copy(out=ks[b, hg][:], in_=ks_bank[b, hg][:])
+            nc.scalar.copy(out=ks[b, hg][:], in_=ks_bank[b, hg][:])
             terms = small.tile([P, HG, 2], BF16, name="ksum_terms")
             nc.gpsimd.tensor_copy(out=terms[:, :, 0], in_=ks[b, hg][:])
             nc.gpsimd.tensor_tensor(out=terms[:, :, 1], in0=ks[b, hg][:], in1=terms[:, :, 0], op=ALU.subtract)
@@ -176,6 +185,17 @@ def tile_multiheadedselfattention_pa_kernel(
             for i, tokens in enumerate((of_head(k_sb, b, h), of_head(q_sb, b, h))):
                 for t in range(NT):
                     nc.tensor.transpose(kq_bank[b, h][:, i, t, :], tokens[:, t, :], ident_bf[:])
+
+        def transpose_half(h, i):
+            if i == 0:
+                pool, tag = (psum_s, "s") if h == HG - 1 else (psum_c, "c")
+                kq_bank[0, h] = pool.tile([P, 2, NT, P], BF16, tag=tag, name="kq_bank")
+            tokens = of_head((k_sb, q_sb)[i], 0, h)
+            for t in range(NT):
+                nc.tensor.transpose(kq_bank[0, h][:, i, t, :], tokens[:, t, :], ident_bf[:])
+
+        def copy_half(h, i, copy):
+            copy(out=kqT[0][:, h, i, :], in_=kq_bank[0, h][:, i].rearrange("p t r -> p (t r)"))
 
         def copy_kq(b, h):
             copy = nc.vector.tensor_copy if (b, h) == (0, 1) else nc.scalar.copy
@@ -550,10 +570,9 @@ def tile_multiheadedselfattention_pa_kernel(
                 at(slot - 2 * HG, lambda b=b, hg=hg: key_terms(b, hg), tensor=lambda b=b, hg=hg: key_sums(b, hg))
             at(slot, lambda b=b, hg=hg: gates(b, hg), tensor=lambda b=b, hg=hg: pool_scores(b, hg))
             at(slot + 2, lambda b=b, hg=hg: sigmoids(b, hg))
-        for w in range(1, PASSES * WV_PARTS):
-            slot = 2 + (w - 2) * 3 // 2
-            if w >= 2:
-                at(slot, lambda w=w: weights_regroup(w // WV_PARTS, w % WV_PARTS))
+        for w in range(PASSES * WV_PARTS):
+            slot = max(w * 3 // 2 - 1, 0)
+            at(slot, lambda w=w: weights_regroup(w // WV_PARTS, w % WV_PARTS))
             at(slot + 3, lambda w=w: weights_quantise(w // WV_PARTS, w % WV_PARTS))
         for b, slot, stride in ((0, 6, 1), (1, 12, 3)):
             for t in range(NT):
@@ -588,11 +607,12 @@ def tile_multiheadedselfattention_pa_kernel(
             at(15 + b * 29, lambda b=b: copy_tail(b))
 
         for h in range(HG):
-            transpose_kq(0, h)
-            copy_kq(0, h)
-        for w in range(2):
-            weights_regroup(0, w)
-        weights_quantise(0, 0)
+            transpose_half(h, 0)
+            copy_half(h, 0, nc.vector.tensor_copy if h % 2 == 1 else nc.scalar.copy)
+        keep_warm(3)
+        for h in range(HG):
+            transpose_half(h, 1)
+            copy_half(h, 1, nc.vector.tensor_copy if h == 1 else nc.scalar.copy)
         scores(0)
         for work in tensor_plan[0]:
             work()

@@ -25,9 +25,9 @@ HG = 4
 W = HG * P
 SCALE = 1.0 / math.sqrt(P)
 MASKED = 1.0e30
-WV_PARTS = 4
+WV_PARTS = 2
 WV_PART = D // WV_PARTS
-LAG = 7
+LAG = 6
 
 BV0 = 0
 GAIN0 = BV0 + D
@@ -83,9 +83,25 @@ def tile_multiheadedselfattention_pa_kernel(
                 out=q_sb[b, hg][:], in_=q[b].rearrange("(p t) d -> p t d", t=NT)[:, :, hg * W : hg * W + width]
             )
 
-        def of_head(tiles, b, h):
-            tile, first = (tiles[0, h // HG], h % HG * P) if b == 0 else (tiles[1, 0], h * P)
-            return tile[:, :, first : first + P]
+        q0_parts = []
+
+        def load_q0(tiles, cols):
+            count, width = tiles.stop - tiles.start, cols.stop - cols.start
+            part = raw.tile([P, count, width], BF16, name="q0_part%d" % len(q0_parts))
+            nc.sync.dma_start(out=part[:], in_=q[0].rearrange("(p t) d -> p t d", t=NT)[:, tiles, cols])
+            q0_parts.append((tiles, cols, part))
+
+        def tokens_of(i, b, h, t):
+            first = h * P
+            if i == 0:
+                if b == 1:
+                    return k_sb[b, 0][:, t, first : first + P]
+                return k_sb[b, h // HG][:, t, first % W : first % W + P]
+            if b == 1:
+                return q_sb[b, 0][:, t, first : first + P]
+            for tiles, cols, part in q0_parts:
+                if tiles.start <= t < tiles.stop and cols.start <= first < cols.stop:
+                    return part[:, t - tiles.start, first - cols.start : first - cols.start + P]
 
         def load_pvk(b):
             pvk_sb[b] = raw.tile([P, NT, D], BF16, name="pvk_sb%d" % b)
@@ -108,7 +124,8 @@ def tile_multiheadedselfattention_pa_kernel(
             )
 
         load_k(0, 0, W)
-        load_q(0, 0, W)
+        load_q0(slice(0, 1), slice(0, W))
+        load_q0(slice(1, NT), slice(0, D))
         load_wv(0)
         for first, width, vector in (
             (BV0, D, bv.rearrange("(o n) -> o n", o=1)),
@@ -118,7 +135,7 @@ def tile_multiheadedselfattention_pa_kernel(
         ):
             nc.sync.dma_start(out=small_row[0:1, first : first + width], in_=vector)
         load_k(0, 1, W)
-        load_q(0, 1, W)
+        load_q0(slice(0, 1), slice(W, D))
         load_wv(1)
         load_pvk(0)
         load_pvk(1)
@@ -147,13 +164,10 @@ def tile_multiheadedselfattention_pa_kernel(
         nc.tensor.transpose(mask_ps[:], mask_rows[:], ident_bf[:])
         mask_t = const.tile([P, B * NT], BF16)
         nc.vector.tensor_copy(out=mask_t[:], in_=mask_ps[:, 0 : B * NT])
-        mask_bias_t = const.tile([P, B * NT, P], F32)
-        for b in range(B):
-            tiles = slice(b * NT, (b + 1) * NT)
-            nc.vector.tensor_scalar(
-                out=mask_bias_t[:, tiles, :], in0=mask_t[:, tiles].unsqueeze(2).to_broadcast([P, NT, P]),
-                scalar1=1.0, scalar2=MASKED, op0=ALU.subtract, op1=ALU.mult,
-            )
+        mask_bias_t = const.tile([P, B * NT], F32)
+        nc.vector.tensor_scalar(
+            out=mask_bias_t[:], in0=mask_t[:], scalar1=1.0, scalar2=MASKED, op0=ALU.subtract, op1=ALU.mult
+        )
 
         ks_bank = {}
         ks = {}
@@ -165,7 +179,7 @@ def tile_multiheadedselfattention_pa_kernel(
                 h = hg * HG + hh
                 for t in range(NT):
                     nc.tensor.matmul(
-                        out=ks_bank[b, hg][:, hh : hh + 1], lhsT=of_head(k_sb, b, h)[:, t, :],
+                        out=ks_bank[b, hg][:, hh : hh + 1], lhsT=tokens_of(0, b, h, t),
                         rhs=mask_t[:, b * NT + t : b * NT + t + 1], start=(t == 0), stop=(t == NT - 1),
                     )
 
@@ -182,24 +196,35 @@ def tile_multiheadedselfattention_pa_kernel(
 
         def transpose_kq(b, h):
             kq_bank[b, h] = psum_c.tile([P, 2, NT, P], BF16, tag="c", name="kq_bank")
-            for i, tokens in enumerate((of_head(k_sb, b, h), of_head(q_sb, b, h))):
+            for i in range(2):
                 for t in range(NT):
-                    nc.tensor.transpose(kq_bank[b, h][:, i, t, :], tokens[:, t, :], ident_bf[:])
+                    nc.tensor.transpose(kq_bank[b, h][:, i, t, :], tokens_of(i, b, h, t), ident_bf[:])
 
-        def transpose_half(h, i):
-            if i == 0:
-                pool, tag = (psum_s, "s") if h == HG - 1 else (psum_c, "c")
-                kq_bank[0, h] = pool.tile([P, 2, NT, P], BF16, tag=tag, name="kq_bank")
-            tokens = of_head((k_sb, q_sb)[i], 0, h)
+        def transpose_first_k(h):
+            pool, tag = (psum_s, "s") if h == HG - 1 else (psum_c, "c")
+            kq_bank[0, h] = pool.tile([P, NT, P], BF16, tag=tag, name="k_bank")
             for t in range(NT):
-                nc.tensor.transpose(kq_bank[0, h][:, i, t, :], tokens[:, t, :], ident_bf[:])
+                nc.tensor.transpose(kq_bank[0, h][:, t, :], tokens_of(0, 0, h, t), ident_bf[:])
 
-        def copy_half(h, i, copy):
-            copy(out=kqT[0][:, h, i, :], in_=kq_bank[0, h][:, i].rearrange("p t r -> p (t r)"))
+        def copy_first_k(h, copy):
+            copy(out=kqT[0][:, h, 0, :], in_=kq_bank[0, h][:].rearrange("p t r -> p (t r)"))
+
+        q_bank = {}
+
+        def transpose_first_q(h, count, first, tiles):
+            q_bank[h, first] = psum_c.tile([P, count, tiles, P], BF16, tag="c", name="q_bank")
+            for i in range(count):
+                for t in range(tiles):
+                    nc.tensor.transpose(q_bank[h, first][:, i, t, :], tokens_of(1, 0, h + i, first + t), ident_bf[:])
+
+        def copy_first_q(h, count, first, tiles):
+            nc.scalar.copy(
+                out=kqT[0][:, h : h + count, 1, first * P : (first + tiles) * P],
+                in_=q_bank[h, first][:].rearrange("p h t r -> p h (t r)"),
+            )
 
         def copy_kq(b, h):
-            copy = nc.vector.tensor_copy if (b, h) == (0, 1) else nc.scalar.copy
-            copy(out=kqT[b][:, h, :, :], in_=kq_bank[b, h][:].rearrange("p i t r -> p i (t r)"))
+            nc.scalar.copy(out=kqT[b][:, h, :, :], in_=kq_bank[b, h][:].rearrange("p i t r -> p i (t r)"))
 
         small_bc = const.tile([P, SMALL_W], F32)
         small_bank = {}
@@ -236,7 +261,7 @@ def tile_multiheadedselfattention_pa_kernel(
 
         def weights_regroup(g, part):
             first = part * WV_PART
-            grouped = stage.tile([P, WV_PART, 4], BF16, align_bytes=64, name="wv_grouped", bufs=3)
+            grouped = stage.tile([P, WV_PART, 4], BF16, align_bytes=64, name="wv_grouped", bufs=2)
             out_cols = grouped[:].rearrange("p (c i) t -> p c t i", i=4)
             in_cols = wv_raw[g][:, :, first : first + WV_PART].rearrange("p t (c i) -> p c t i", i=4)
             nc.vector.tensor_copy(out=out_cols, in_=in_cols)
@@ -396,7 +421,8 @@ def tile_multiheadedselfattention_pa_kernel(
                 s_bank[i] = psum_s.tile([P, S], F32, tag="s", name="s_bank")
                 for t in range(NT):
                     nc.tensor.matmul(
-                        out=s_bank[i][:, t * P : (t + 1) * P], lhsT=mask_bias_t[:, b * NT + t, :], rhs=ident_f32[:],
+                        out=s_bank[i][:, t * P : (t + 1) * P], lhsT=mask_bias_t[:, b * NT + t : b * NT + t + 1].to_broadcast([P, P]),
+                        rhs=ident_f32[:],
                         is_transpose=True, start=(t == 0), stop=False,
                     )
             for i in (first, first + 1):
@@ -538,6 +564,10 @@ def tile_multiheadedselfattention_pa_kernel(
             if mx is not None:
                 mx_plan.setdefault(slot, []).append(mx)
 
+        for slot, h in ((0, 0), (2, 2)):
+            at(
+                slot, lambda h=h: copy_first_q(h, 2, 1, NT - 1), tensor=lambda h=h: transpose_first_q(h, 2, 1, NT - 1)
+            )
         at(1, lambda: key_terms(0, 0), tensor=lambda: key_sums(0, 0))
         for i, first in enumerate((D, 0, S)):
             at(i, lambda first=first: small_copy(first), tensor=lambda first=first: small_spread(first))
@@ -571,7 +601,7 @@ def tile_multiheadedselfattention_pa_kernel(
             at(slot, lambda b=b, hg=hg: gates(b, hg), tensor=lambda b=b, hg=hg: pool_scores(b, hg))
             at(slot + 2, lambda b=b, hg=hg: sigmoids(b, hg))
         for w in range(PASSES * WV_PARTS):
-            slot = max(w * 3 // 2 - 1, 0)
+            slot = max(3 * w - 1, 0)
             at(slot, lambda w=w: weights_regroup(w // WV_PARTS, w % WV_PARTS))
             at(slot + 3, lambda w=w: weights_quantise(w // WV_PARTS, w % WV_PARTS))
         for b, slot, stride in ((0, 6, 1), (1, 12, 3)):
@@ -607,12 +637,10 @@ def tile_multiheadedselfattention_pa_kernel(
             at(15 + b * 29, lambda b=b: copy_tail(b))
 
         for h in range(HG):
-            transpose_half(h, 0)
-            copy_half(h, 0, nc.vector.tensor_copy if h % 2 == 1 else nc.scalar.copy)
-        keep_warm(3)
-        for h in range(HG):
-            transpose_half(h, 1)
-            copy_half(h, 1, nc.vector.tensor_copy if h == 1 else nc.scalar.copy)
+            transpose_first_k(h)
+            copy_first_k(h, nc.vector.tensor_copy if h % 2 == 1 else nc.scalar.copy)
+        transpose_first_q(0, HG, 0, 1)
+        copy_first_q(0, HG, 0, 1)
         scores(0)
         for work in tensor_plan[0]:
             work()

from contextlib import ExitStack
import math

import concourse.mybir as mybir
from concourse.masks import make_identity

F32 = mybir.dt.float32
BF16 = mybir.dt.bfloat16
U32 = mybir.dt.uint32
U8 = mybir.dt.uint8
FP8X4 = mybir.dt.float8_e4m3fn_x4
ALU = mybir.AluOpType
ACT = mybir.ActivationFunctionType
AX = mybir.AxisListType

P = 128
B = 2
S = 512
H = 8
D = 1024
DQ = 1280
NT = S // P
PASSES = D // (4 * P)
HG = 4
W = HG * P
SCALE = 1.0 / math.sqrt(P)
MASKED = 1.0e30
WV_PARTS = 2
WV_PART = D // WV_PARTS
LAG = 6

BV0 = 0
GAIN0 = BV0 + D
GATE_BIAS0 = GAIN0 + 16
COUNT0 = GAIN0 + 32
ROW_W = GAIN0 + 48
SMALL_W = ROW_W - BV0

FLOPS = 2 * B * S * D * D + 2 * 2 * B * H * S * S * P


def tile_multiheadedselfattention_pa_kernel(
    tc, q, k, pre_value_key, Wv, bv, value_key_masks, value_key_counts,
    overall_gain, overall_bias, pre_query, out,
):
    nc = tc.nc
    with ExitStack() as ctx:
        ctx.enter_context(tc.manual_schedule())
        const = ctx.enter_context(tc.tile_pool(name="const", bufs=1))
        raw = ctx.enter_context(tc.tile_pool(name="raw", bufs=1))
        keep = ctx.enter_context(tc.tile_pool(name="keep", bufs=1))
        stage = ctx.enter_context(tc.tile_pool(name="stage", bufs=2))
        small = ctx.enter_context(tc.tile_pool(name="small", bufs=2))
        psum_s = ctx.enter_context(tc.psum_pool(name="psum_s", bufs=4))
        psum_b = ctx.enter_context(tc.psum_pool(name="psum_b", bufs=1))
        psum_c = ctx.enter_context(tc.psum_pool(name="psum_c", bufs=3))

        ones_f32 = const.tile([P, P], F32)
        nc.vector.memset(ones_f32[:], 1.0)
        mask_rows = const.tile([P, P], BF16)
        nc.vector.memset(mask_rows[:], 0.0)
        nc.sync.dma_start(
            out=mask_rows[0 : B * NT, :], in_=value_key_masks.rearrange("b (t p) -> (b t) p", p=P)
        )
        small_row = const.tile([P, ROW_W], BF16)
        nc.vector.memset(small_row[:], 0.0)

        k_sb = {}
        q_sb = {}
        pq_sb = {}
        pvk_sb = {}
        out_view = [out[b].rearrange("(p t) c -> p t c", t=NT) for b in range(B)]

        def load_k(b, hg, width):
            k_sb[b, hg] = raw.tile([P, NT, width], BF16, name="k_sb%d%d" % (b, hg))
            nc.sync.dma_start(
                out=k_sb[b, hg][:], in_=k[b].rearrange("(t p) d -> p t d", p=P)[:, :, hg * W : hg * W + width]
            )

        def load_q(b, hg, width):
            q_sb[b, hg] = raw.tile([P, NT, width], BF16, name="q_sb%d%d" % (b, hg))
            nc.sync.dma_start(
                out=q_sb[b, hg][:], in_=q[b].rearrange("(p t) d -> p t d", t=NT)[:, :, hg * W : hg * W + width]
            )

        q0_parts = []

        def load_q0(tiles, cols):
            count, width = tiles.stop - tiles.start, cols.stop - cols.start
            part = raw.tile([P, count, width], BF16, name="q0_part%d" % len(q0_parts))
            nc.sync.dma_start(out=part[:], in_=q[0].rearrange("(p t) d -> p t d", t=NT)[:, tiles, cols])
            q0_parts.append((tiles, cols, part))

        def tokens_of(i, b, h, t):
            first = h * P
            if i == 0:
                if b == 1:
                    return k_sb[b, 0][:, t, first : first + P]
                return k_sb[b, h // HG][:, t, first % W : first % W + P]
            if b == 1:
                return q_sb[b, 0][:, t, first : first + P]
            for tiles, cols, part in q0_parts:
                if tiles.start <= t < tiles.stop and cols.start <= first < cols.stop:
                    return part[:, t - tiles.start, first - cols.start : first - cols.start + P]

        def load_pvk(b):
            pvk_sb[b] = raw.tile([P, NT, D], BF16, name="pvk_sb%d" % b)
            nc.sync.dma_start(
                out=pvk_sb[b][:].rearrange("p (u e) d -> p u (e d)", e=2),
                in_=pre_value_key[b].rearrange("(u p e) d -> p u (e d)", u=2, e=2),
            )

        def load_pq(b):
            pq_sb[b] = raw.tile([P, NT, DQ], BF16, name="pq_sb%d" % b)
            nc.sync.dma_start(out=pq_sb[b][:], in_=pre_query[b].rearrange("(p t) c -> p t c", t=NT))

        wv_raw = {}

        def load_wv(g):
            wv_raw[g] = raw.tile([P, 4, D], BF16, name="wv_raw%d" % g)
            nc.sync.dma_start(
                out=wv_raw[g][:].rearrange("p (u e) n -> p u (e n)", e=2),
                in_=Wv[g * 4 * P : (g + 1) * 4 * P, :].rearrange("(u p e) n -> p u (e n)", u=2, e=2),
            )

        load_k(0, 0, W)
        load_q0(slice(0, 1), slice(0, W))
        load_q0(slice(1, NT), slice(0, D))
        load_wv(0)
        for first, width, vector in (
            (BV0, D, bv.rearrange("(o n) -> o n", o=1)),
            (GAIN0, H, overall_gain.rearrange("a h b c -> a (h b c)")),
            (GATE_BIAS0, H, overall_bias.rearrange("a h b c -> a (h b c)")),
            (COUNT0, B, value_key_counts.rearrange("(o n) -> o n", o=1)),
        ):
            nc.sync.dma_start(out=small_row[0:1, first : first + width], in_=vector)
        load_k(0, 1, W)
        load_q0(slice(0, 1), slice(W, D))
        load_wv(1)
        load_pvk(0)
        load_pvk(1)
        load_pq(0)
        load_k(1, 0, D)
        load_q(1, 0, D)
        load_pq(1)

        ident_bf = const.tile([P, P], BF16)
        make_identity(nc, ident_bf[:])
        ident_f32 = const.tile([P, P], F32)
        make_identity(nc, ident_f32[:])
        ones_bf = const.tile([P, P], BF16)
        nc.vector.memset(ones_bf[:], 1.0)
        warm = const.tile([P, 1], F32)
        nc.scalar.activation(out=warm[:], in_=ones_bf[:, 0:1], func=ACT.Exp)

        warm_bank = psum_b.tile([P, P], F32, tag="b", name="warm_bank")

        def keep_warm(count):
            for w in range(count):
                nc.tensor.matmul(out=warm_bank[:], lhsT=ones_f32[:], rhs=ones_f32[:], start=True, stop=True)

        keep_warm(8)
        mask_ps = psum_c.tile([P, P], BF16, tag="c", name="mask_ps")
        nc.tensor.transpose(mask_ps[:], mask_rows[:], ident_bf[:])
        mask_t = const.tile([P, B * NT], BF16)
        nc.vector.tensor_copy(out=mask_t[:], in_=mask_ps[:, 0 : B * NT])
        mask_bias_t = const.tile([P, B * NT], F32)
        nc.vector.tensor_scalar(
            out=mask_bias_t[:], in0=mask_t[:], scalar1=1.0, scalar2=MASKED, op0=ALU.subtract, op1=ALU.mult
        )

        ks_bank = {}
        ks = {}
        ksum_terms = {}

        def key_sums(b, hg):
            ks_bank[b, hg] = psum_c.tile([P, HG], F32, tag="c", name="ks_bank")
            for hh in range(HG):
                h = hg * HG + hh
                for t in range(NT):
                    nc.tensor.matmul(
                        out=ks_bank[b, hg][:, hh : hh + 1], lhsT=tokens_of(0, b, h, t),
                        rhs=mask_t[:, b * NT + t : b * NT + t + 1], start=(t == 0), stop=(t == NT - 1),
                    )

        def key_terms(b, hg):
            ks[b, hg] = small.tile([P, HG], F32, name="ks")
            nc.scalar.copy(out=ks[b, hg][:], in_=ks_bank[b, hg][:])
            terms = small.tile([P, HG, 2], BF16, name="ksum_terms")
            nc.gpsimd.tensor_copy(out=terms[:, :, 0], in_=ks[b, hg][:])
            nc.gpsimd.tensor_tensor(out=terms[:, :, 1], in0=ks[b, hg][:], in1=terms[:, :, 0], op=ALU.subtract)
            ksum_terms[b, hg] = terms

        kqT = [keep.tile([P, H, 2, S], BF16, name="kqT%d" % b) for b in range(B)]
        kq_bank = {}

        def transpose_kq(b, h):
            kq_bank[b, h] = psum_c.tile([P, 2, NT, P], BF16, tag="c", name="kq_bank")
            for i in range(2):
                for t in range(NT):
                    nc.tensor.transpose(kq_bank[b, h][:, i, t, :], tokens_of(i, b, h, t), ident_bf[:])

        def transpose_first_k(h):
            pool, tag = (psum_s, "s") if h == HG - 1 else (psum_c, "c")
            kq_bank[0, h] = pool.tile([P, NT, P], BF16, tag=tag, name="k_bank")
            for t in range(NT):
                nc.tensor.transpose(kq_bank[0, h][:, t, :], tokens_of(0, 0, h, t), ident_bf[:])

        def copy_first_k(h, copy):
            copy(out=kqT[0][:, h, 0, :], in_=kq_bank[0, h][:].rearrange("p t r -> p (t r)"))

        q_bank = {}

        def transpose_first_q(h, count, first, tiles):
            q_bank[h, first] = psum_c.tile([P, count, tiles, P], BF16, tag="c", name="q_bank")
            for i in range(count):
                for t in range(tiles):
                    nc.tensor.transpose(q_bank[h, first][:, i, t, :], tokens_of(1, 0, h + i, first + t), ident_bf[:])

        def copy_first_q(h, count, first, tiles):
            nc.scalar.copy(
                out=kqT[0][:, h : h + count, 1, first * P : (first + tiles) * P],
                in_=q_bank[h, first][:].rearrange("p h t r -> p h (t r)"),
            )

        def copy_kq(b, h):
            nc.scalar.copy(out=kqT[b][:, h, :, :], in_=kq_bank[b, h][:].rearrange("p i t r -> p i (t r)"))

        small_bc = const.tile([P, SMALL_W], F32)
        small_bank = {}

        def small_spread(first):
            width = min(S, SMALL_W - first)
            small_bank[first] = psum_c.tile([P, S], F32, tag="c", name="small_bank")
            nc.tensor.matmul(
                out=small_bank[first][:, 0:width], lhsT=ones_bf[:], rhs=small_row[:, BV0 + first : BV0 + first + width],
                start=True, stop=True,
            )

        def small_copy(first):
            width = min(S, SMALL_W - first)
            nc.scalar.copy(out=small_bc[:, first : first + width], in_=small_bank[first][:, 0:width])

        gain_bc = small_bc[:, GAIN0 - BV0 : GAIN0 - BV0 + H]
        gate_bias_bc = small_bc[:, GATE_BIAS0 - BV0 : GATE_BIAS0 - BV0 + H]
        count_bc = small_bc[:, COUNT0 - BV0 : COUNT0 - BV0 + B]
        inv_count = const.tile([P, B], F32)
        gate_scale = const.tile([P, B, H], F32)

        def gate_scales():
            nc.vector.reciprocal(out=inv_count[:], in_=count_bc)
            for b in range(B):
                nc.gpsimd.tensor_scalar(
                    out=gate_scale[:, b, :], in0=gain_bc, scalar1=inv_count[:, b : b + 1], scalar2=SCALE, op0=ALU.mult,
                    op1=ALU.mult,
                )

        wv_codes = keep.tile([P, PASSES, D], U32, align_bytes=64)
        wv_scales = keep.tile([P, PASSES, D], U8, align_bytes=64)
        wv_grouped = {}

        def weights_regroup(g, part):
            first = part * WV_PART
            grouped = stage.tile([P, WV_PART, 4], BF16, align_bytes=64, name="wv_grouped", bufs=2)
            out_cols = grouped[:].rearrange("p (c i) t -> p c t i", i=4)
            in_cols = wv_raw[g][:, :, first : first + WV_PART].rearrange("p t (c i) -> p c t i", i=4)
            nc.vector.tensor_copy(out=out_cols, in_=in_cols)
            wv_grouped[g, part] = grouped

        def weights_quantise(g, part):
            cols = slice(part * WV_PART, (part + 1) * WV_PART)
            nc.vector.quantize_mx(
                out=wv_codes[:, g, cols].bitcast(FP8X4),
                scales=wv_scales[:, g, cols],
                in_=wv_grouped[g, part][:].rearrange("p c t -> p (c t)"),
            )

        pvk_codes = keep.tile([P, PASSES, B * S], U32, align_bytes=64)
        pvk_scales = keep.tile([P, PASSES, B * S], U8, align_bytes=64)
        v_codes = keep.tile([P, B, D], U32, align_bytes=64)
        v_scales = keep.tile([P, B, D], U8, align_bytes=64)
        pvk_grouped = {}

        w_bank = {}

        def tokens_transpose(b, t):
            pvk_words = pvk_sb[b][:].bitcast(F32)
            w_bank[b, t] = psum_c.tile([P, PASSES, 2, P], F32, tag="c", name="w_bank")
            for g in range(PASSES):
                for u in range(2):
                    first = (2 * g + u) * P
                    nc.tensor.transpose(
                        w_bank[b, t][:, g, u, :], pvk_words[:, t, first : first + P], ident_f32[:]
                    )

        def tokens_group(b, t):
            if t == 0:
                pvk_grouped[b] = stage.tile([P, PASSES, S, 4], BF16, align_bytes=64, name="pvk_grouped", bufs=1)
            nc.scalar.copy(
                out=pvk_grouped[b][:].bitcast(F32)[:, :, t * P : (t + 1) * P, :],
                in_=w_bank[b, t][:].rearrange("p g u r -> p g r u"),
            )

        def tokens_quantise(b, g):
                nc.vector.quantize_mx(
             out=pvk_codes[:, g, b * S : (b + 1) * S].bitcast(FP8X4),
             scales=pvk_scales[:, g, b * S : (b + 1) * S],
             in_=pvk_grouped[b][:, g].rearrange("p r t -> p (r t)"),
                )

        v_bank = {}
        v_grouped = {}

        def values_matmul(b, h):
            cols = slice(h * P, (h + 1) * P)
            v_bank[b, h] = psum_c.tile([P, NT, P], F32, tag="c", name="v_bank")
            for t in range(NT):
                toks = slice(b * S + t * P, b * S + (t + 1) * P)
                for g in range(PASSES):
                    nc.tensor.matmul_mx(
                        out=v_bank[b, h][:, t, :],
                        lhsT=pvk_codes[:, g, toks].bitcast(FP8X4),
                        lhsT_scale=pvk_scales[:, g, toks],
                        rhs=wv_codes[:, g, cols].bitcast(FP8X4),
                        rhs_scale=wv_scales[:, g, cols],
                        start=(g == 0),
                        stop=(g == PASSES - 1),
                    )

        def values_add(b, h):
            cols = slice(h * P, (h + 1) * P)
            if h % 2 == 0:
                v_grouped[b, h // 2] = stage.tile([P, 2, P, NT], BF16, align_bytes=64, name="v_grouped", bufs=2)
            nc.vector.tensor_tensor(
                out=v_grouped[b, h // 2][:, h % 2],
                in0=v_bank[b, h][:].rearrange("p t c -> p c t"),
                in1=small_bc[:, cols].unsqueeze(2).to_broadcast([P, P, NT]),
                op=ALU.add,
            )

        def values_quantise(b, pair):
            cols = slice(pair * 2 * P, (pair + 1) * 2 * P)
            nc.vector.quantize_mx(
                out=v_codes[:, b, cols].bitcast(FP8X4),
                scales=v_scales[:, b, cols],
                in_=v_grouped[b, pair][:].rearrange("p h c t -> p (h c t)"),
            )

        gate = {}
        one_minus_gate = {}
        pooled_bank = {}
        shifted_score = {}

        def pool_scores(b, hg):
            pooled_bank[b, hg] = psum_c.tile([P, NT, HG, 2], F32, tag="c", name="pooled_bank")
            for it in range(NT):
                for hh in range(HG):
                    nc.tensor.matmul(
                        out=pooled_bank[b, hg][:, it, hh, :],
                        lhsT=kqT[b][:, hg * HG + hh, 1, it * P : (it + 1) * P],
                        rhs=ksum_terms[b, hg][:, hh, :],
                        start=True,
                        stop=True,
                    )

        def gates(b, hg):
            heads = slice(hg * HG, (hg + 1) * HG)
            pooled_ps = pooled_bank[b, hg]
            pooled = small.tile([P, NT, HG], F32)
            nc.vector.tensor_reduce(out=pooled[:], in_=pooled_ps[:], axis=AX.X, op=ALU.add)
            scaled = small.tile([P, NT, HG], F32)
            nc.gpsimd.tensor_tensor(
                out=scaled[:], in0=pooled[:], in1=gate_scale[:, b, heads].unsqueeze(1).to_broadcast([P, NT, HG]),
                op=ALU.mult,
            )
            shifted = small.tile([P, NT, HG], F32)
            nc.gpsimd.tensor_tensor(
                out=shifted[:], in0=scaled[:], in1=gate_bias_bc[:, heads].unsqueeze(1).to_broadcast([P, NT, HG]),
                op=ALU.add,
            )
            shifted_score[b, hg] = shifted

        def sigmoids(b, hg):
            tanh_half = small.tile([P, NT, HG], F32)
            nc.scalar.activation(out=tanh_half[:], in_=shifted_score[b, hg][:], func=ACT.Tanh, scale=0.5)
            gate[b, hg] = keep.tile([P, NT, HG], F32, name="gate%d%d" % (b, hg))
            nc.gpsimd.tensor_scalar(
                out=gate[b, hg][:], in0=tanh_half[:], scalar1=0.5, scalar2=0.5, op0=ALU.mult, op1=ALU.add
            )
            one_minus_gate[b, hg] = keep.tile([P, NT, HG], F32, name="one_minus_gate%d%d" % (b, hg))
            nc.gpsimd.tensor_scalar(
                out=one_minus_gate[b, hg][:], in0=tanh_half[:], scalar1=-0.5, scalar2=0.5, op0=ALU.mult, op1=ALU.add
            )

        def copy_tail(b):
            tail = stage.tile([P, NT, DQ - D], F32, bufs=1, name="tail")
            nc.gpsimd.tensor_scalar(
                out=tail[:], in0=pq_sb[b][:, :, D:DQ], scalar1=1.0, scalar2=0.0, op0=ALU.mult, op1=ALU.add
            )
            nc.sync.dma_start(out=out_view[b][:, :, D:DQ], in_=tail[:])

        units = [(b, hg, it) for b in range(B) for hg in range(H // HG) for it in range(NT)]
        exp_bias = {}
        e_bf = {}
        row_sum = {}
        inv_sum = {}
        e_grouped = {}
        e_codes = {}
        e_scales = {}
        weight = {}
        h_bank = {}
        result = {}
        ALL = range(HG)

        s_bank = {}
        products = {}

        def scores(first):
            for i in (first, first + 1):
                b = units[i // HG][0]
                s_bank[i] = psum_s.tile([P, S], F32, tag="s", name="s_bank")
                for t in range(NT):
                    nc.tensor.matmul(
                        out=s_bank[i][:, t * P : (t + 1) * P], lhsT=mask_bias_t[:, b * NT + t : b * NT + t + 1].to_broadcast([P, P]),
                        rhs=ident_f32[:],
                        is_transpose=True, start=(t == 0), stop=False,
                    )
            for i in (first, first + 1):
                if i > first:
                    for work in mx_plan.get(first, []) + mx_plan.get(first + 1, []):
                        work()
                n, hh = divmod(i, HG)
                b, hg, it = units[n]
                h = hg * HG + hh
                nc.tensor.matmul(
                    out=s_bank[i][:], lhsT=kqT[b][:, h, 1, it * P : (it + 1) * P], rhs=kqT[b][:, h, 0, :], start=False,
                    stop=True,
                )

        def maximum(i):
            n, hh = divmod(i, HG)
            if hh == 0:
                exp_bias[n] = small.tile([P, HG], F32, name="exp_bias", bufs=3)
                e_bf[n] = stage.tile([P, HG, S], BF16, name="e_bf", bufs=3)
                if n % 2 == 0:
                    row_sum[n // 2] = small.tile([P, 2, HG], F32, name="row_sum", bufs=3)
            products[i] = stage.tile([P, S], F32, bufs=3, name="products")
            nc.vector.tensor_scalar(
                out=products[i][:], in0=s_bank[i][:], scalar1=-SCALE, scalar2=None, op0=ALU.mult, op1=ALU.min,
                accum_out=exp_bias[n][:, hh : hh + 1],
            )

        def exponential(i):
            n, hh = divmod(i, HG)
            nc.scalar.activation(
                out=e_bf[n][:, hh, :],
                in_=products[i][:],
                func=ACT.Exp,
                bias=exp_bias[n][:, hh : hh + 1],
                scale=-1.0,
                accum_out=row_sum[n // 2][:, n % 2, hh : hh + 1],
            )

        e_bank = {}

        def transpose_e(n, pair):
            e_words = e_bf[n][:].bitcast(F32)
            pool, tag = (psum_s, "s") if (n, pair) == (len(units) - 1, 1) else (psum_b, "b")
            e_bank[n, pair] = pool.tile([P, 2, 2, P], F32, tag=tag, name="e_bank")
            for h2 in range(2):
                for u in range(2):
                    nc.tensor.transpose(
                        e_bank[n, pair][:, h2, u, :], e_words[:, 2 * pair + h2, u * P : (u + 1) * P], ident_f32[:]
                    )

        def group_e(n, pair):
            if pair == 0:
                e_grouped[n] = stage.tile([P, HG, P, 4], BF16, align_bytes=64, name="e_grouped", bufs=2)
            nc.scalar.copy(
                out=e_grouped[n][:].bitcast(F32)[:, 2 * pair : 2 * pair + 2, :, :],
                in_=e_bank[n, pair][:].rearrange("p h u i -> p h i u"),
            )

        def invert_sums(first, count):
            inverse = small.tile([P, 2, HG], F32, name="inverse", bufs=3)
            which = slice(first % 2, first % 2 + count)
            nc.vector.reciprocal(out=inverse[:, which, :], in_=row_sum[first // 2][:, which, :])
            for n in range(first, first + count):
                inv_sum[n] = inverse[:, n % 2, :]

        def blend_weights(n):
            b, hg, it = units[n]
            weight[n] = small.tile([P, HG], F32, name="weight", bufs=LAG)
            nc.gpsimd.tensor_tensor(out=weight[n][:], in0=inv_sum[n], in1=gate[b, hg][:, it, :], op=ALU.mult)

        def blend_rest(n):
            b, hg, it = units[n]
            result[n] = stage.tile([P, W], F32, name="result", bufs=LAG)
            for hh in range(HG):
                h = hg * HG + hh
                nc.gpsimd.tensor_scalar(
                    out=result[n][:, hh * P : (hh + 1) * P],
                    in0=pq_sb[b][:, it, h * P : (h + 1) * P],
                    scalar1=one_minus_gate[b, hg][:, it, hh : hh + 1],
                    scalar2=0.0,
                    op0=ALU.mult,
                    op1=ALU.add,
                )

        def quantise_e(n, heads=ALL):
            if heads[0] == 0:
                e_codes[n] = stage.tile([P, W], U32, align_bytes=64, name="e_codes", bufs=LAG)
                e_scales[n] = stage.tile([P, W], U8, align_bytes=64, name="e_scales", bufs=LAG)
            cols = slice(heads[0] * P, (heads[-1] + 1) * P)
            nc.vector.quantize_mx(
                out=e_codes[n][:, cols].bitcast(FP8X4),
                scales=e_scales[n][:, cols],
                in_=e_grouped[n][:, heads[0] : heads[-1] + 1].rearrange("p h i t -> p (h i t)"),
            )

        def e_times_v(n, heads=ALL):
            b, hg, it = units[n]
            h_bank[n, heads[0]] = psum_c.tile([P, HG, P], F32, tag="c", name="h_bank")
            for hh in heads:
                h = hg * HG + hh
                nc.tensor.matmul_mx(
                    out=h_bank[n, heads[0]][:, hh, :],
                    lhsT=e_codes[n][:, hh * P : (hh + 1) * P].bitcast(FP8X4),
                    lhsT_scale=e_scales[n][:, hh * P : (hh + 1) * P],
                    rhs=v_codes[:, b, h * P : (h + 1) * P].bitcast(FP8X4),
                    rhs_scale=v_scales[:, b, h * P : (h + 1) * P],
                    start=True,
                    stop=True,
                )

        def blend(n, heads=ALL):
            b, hg, it = units[n]
            for hh in heads:
                cols = slice(hh * P, (hh + 1) * P)
                nc.vector.scalar_tensor_tensor(
                    out=result[n][:, cols],
                    in0=h_bank[n, heads[0]][:, hh, :],
                    scalar=weight[n][:, hh : hh + 1],
                    in1=result[n][:, cols],
                    op0=ALU.mult,
                    op1=ALU.add,
                )
            cols = slice(heads[0] * P, (heads[-1] + 1) * P)
            nc.sync.dma_start(
                out=out_view[b][:, it, hg * W + cols.start : hg * W + cols.stop], in_=result[n][:, cols]
            )

        heads = [(b, h) for b in range(B) for h in range(H)]
        groups = [(b, hg) for b in range(B) for hg in range(H // HG)]
        slots = len(units) * HG
        mx_plan = {}
        tensor_plan = {}
        plan = {}

        def at(slot, rest, tensor=None, mx=None):
            plan.setdefault(slot, []).append(rest)
            if tensor is not None:
                tensor_plan.setdefault(slot, []).append(tensor)
            if mx is not None:
                mx_plan.setdefault(slot, []).append(mx)

        for slot, h in ((0, 0), (2, 2)):
            at(
                slot, lambda h=h: copy_first_q(h, 2, 1, NT - 1), tensor=lambda h=h: transpose_first_q(h, 2, 1, NT - 1)
            )
        at(1, lambda: key_terms(0, 0), tensor=lambda: key_sums(0, 0))
        for i, first in enumerate((D, 0, S)):
            at(i, lambda first=first: small_copy(first), tensor=lambda first=first: small_spread(first))
        at(2, gate_scales)
        last = len(units) - 1
        for n in range(len(units)):
            start = n * HG
            at(start + 4, lambda n=n: group_e(n, 0), tensor=lambda n=n: transpose_e(n, 0))
            at(start + 6, lambda n=n: group_e(n, 1), tensor=lambda n=n: transpose_e(n, 1))
            if n >= last - 1:
                at(start + 5, lambda n=n: invert_sums(n, 1))
                at(start + 6, lambda n=n: blend_weights(n))
            elif n % 2 == 1:
                at(start + 7, lambda n=n: invert_sums(n - 1, 2))
                for unit in (n - 1, n):
                    at(start + 10, lambda unit=unit: blend_weights(unit))
            if n < last:
                at(max(start + 9, 14), lambda n=n: blend_rest(n))
                at(start + 9, lambda n=n: quantise_e(n))
            else:
                at(start + 3, lambda n=n: blend_rest(n))
                for half in range(2):
                    at(start + 5 + 2 * half, lambda n=n, half=half: quantise_e(n, ALL[2 * half : 2 * half + 2]))
        for c in range(HG, len(heads)):
            b, h = heads[c]
            at((c - HG) * HG + 2, lambda b=b, h=h: copy_kq(b, h), tensor=lambda b=b, h=h: transpose_kq(b, h))
        for g, (b, hg) in enumerate(groups):
            slot = g * NT * HG + 1 if g > 0 else 4
            if g > 0:
                at(slot - 2 * HG, lambda b=b, hg=hg: key_terms(b, hg), tensor=lambda b=b, hg=hg: key_sums(b, hg))
            at(slot, lambda b=b, hg=hg: gates(b, hg), tensor=lambda b=b, hg=hg: pool_scores(b, hg))
            at(slot + 2, lambda b=b, hg=hg: sigmoids(b, hg))
        for w in range(PASSES * WV_PARTS):
            slot = max(3 * w - 1, 0)
            at(slot, lambda w=w: weights_regroup(w // WV_PARTS, w % WV_PARTS))
            at(slot + 3, lambda w=w: weights_quantise(w // WV_PARTS, w % WV_PARTS))
        for b, slot, stride in ((0, 6, 1), (1, 12, 3)):
            for t in range(NT):
                at(
                    slot + t * stride, lambda b=b, t=t: tokens_group(b, t),
                    tensor=lambda b=b, t=t: tokens_transpose(b, t),
                )
            for g in range(PASSES):
                at(slot + (NT - 1) * stride + 1 + g, lambda b=b, g=g: tokens_quantise(b, g))
        v_slot = {}
        for c, (b, h) in enumerate(heads):
            slot = 14 + 3 * c
            v_slot[b, h // HG] = slot + 1
            at(slot, lambda b=b, h=h: values_add(b, h), mx=lambda b=b, h=h: values_matmul(b, h))
            if h % 2 == 1:
                at(slot + 1, lambda b=b, h=h: values_quantise(b, h // 2))
        free_slot = 0
        for n in range(len(units)):
            b, hg, it = units[n]
            if n < last:
                weighed = n * HG + 10 + (HG if n % 2 == 0 and n < last - 1 else 0)
                slot = max(weighed + 1, v_slot[b, hg] + 2, free_slot)
                at(slot, lambda n=n: blend(n), mx=lambda n=n: e_times_v(n))
                free_slot = slot + 3
            else:
                for half in range(2):
                    at(
                        max(n * HG + 7, free_slot) + half, lambda n=n, half=half: blend(n, ALL[2 * half : 2 * half + 2]),
                        mx=lambda n=n, half=half: e_times_v(n, ALL[2 * half : 2 * half + 2]),
                    )
        for b in range(B):
            at(15 + b * 29, lambda b=b: copy_tail(b))

        for h in range(HG):
            transpose_first_k(h)
            copy_first_k(h, nc.vector.tensor_copy if h % 2 == 1 else nc.scalar.copy)
        transpose_first_q(0, HG, 0, 1)
        copy_first_q(0, HG, 0, 1)
        scores(0)
        for work in tensor_plan[0]:
            work()
        for i in range(max(plan) + 1):
            late = mx_plan.get(i + 1, []) if i + 1 >= slots else []
            for work in late + tensor_plan.get(i + 1, []):
                work()
            if i < slots:
                maximum(i)
            if 0 < i <= slots:
                exponential(i - 1)
            for work in plan.get(i, []):
                work()
            if i % 2 == 0 and i + 2 < slots:
                scores(i + 2)
